import numpy as np
import ml_dtypes


def mxq(x, axis, fmt="e4m3"):
    dtype, down = {"e4m3": (ml_dtypes.float8_e4m3fn, 7), "e5m2": (ml_dtypes.float8_e5m2, 14)}[fmt]
    v = np.moveaxis(np.asarray(x, np.float32).astype(ml_dtypes.bfloat16).astype(np.float64), axis, -1)
    blocks = v.reshape(v.shape[:-1] + (-1, 32))
    amax = np.abs(blocks).max(-1, keepdims=True)
    byte = np.maximum(np.where(amax > 0, np.frexp(amax)[1] - 1 + 127, 0) - down, 1)
    scale = np.exp2(byte - 127.0)
    codes = (blocks / scale).astype(np.float32).astype(dtype).astype(np.float64)
    return np.moveaxis((codes * scale).reshape(v.shape), -1, axis)


WIDE = False


def mx_kscale(k):
    if not WIDE:
        return np.ones(k)
    levels = np.array([10, -10, 5, -5, 0])
    a = np.random.permutation(np.resize(levels, k // 512 * 4)).reshape(k // 512, 4)
    idx = np.arange(k)
    return np.exp2(a[idx // 512, idx % 128 // 32])


BF16 = ml_dtypes.bfloat16


def bf(x):
    return np.asarray(x, np.float32).astype(BF16)


def f64(x):
    return np.asarray(x).astype(np.float64)


B, L, E, H, WINDOW = 2, 512, 1024, 16, 4
D = E // H
NREL = 2 * WINDOW + 1


def band_of(p):
    t = np.arange(L)
    cols = []
    for j in range(NREL):
        s = t + j - WINDOW
        ok = (s >= 0) & (s < L)
        cols.append(np.where(ok[None, :], p[:, t, np.clip(s, 0, L - 1)], 0.0))
    return np.stack(cols, axis=-1)


def setup_inputs():
    u = mx_kscale(E)
    td = np.repeat(np.array([u.max(), u.min()]), D // 2)
    t = np.tile(td, H)
    return {
        "logits": bf(np.random.standard_normal((B * H, L, L)) * 1.5),
        "v": bf(np.random.standard_normal((B * H, L, D)) * td),
        "emb_rel_v": bf(np.random.standard_normal((1, NREL, D)) * td),
        "Wo": bf(np.random.standard_normal((E, E)) * 3.0 / np.sqrt(E) / t[:, None]),
        "bo": bf(np.random.standard_normal(E) * 0.1),
    }


def reference(logits, v, emb_rel_v, Wo, bo):
    a = f64(logits)
    e = np.exp(a - a.max(-1, keepdims=True))
    z = e.sum(-1, keepdims=True)
    ctx = mxq(e, 2, "e4m3") @ mxq(f64(v), 1, "e4m3")
    band = band_of(e)
    rv = f64(emb_rel_v)[0]
    rel = np.zeros_like(ctx)
    for j in range(NREL):
        rel = rel + band[:, :, j:j + 1] * rv[j][None, None, :]
    attn = (ctx + rel) / z
    merged = attn.reshape(B, H, L, D).transpose(0, 2, 1, 3).reshape(B, L, E)
    return (mxq(merged, 2, "e4m3") @ mxq(f64(Wo), 0, "e4m3")) + f64(bo)

@@ -1,0 +1,398 @@
+from contextlib import ExitStack
+
+import concourse.mybir as mybir
+from concourse.masks import make_identity
+
+F32 = mybir.dt.float32
+BF16 = mybir.dt.bfloat16
+U32 = mybir.dt.uint32
+U8 = mybir.dt.uint8
+FP8X4 = mybir.dt.float8_e4m3fn_x4
+ALU = mybir.AluOpType
+ACT = mybir.ActivationFunctionType
+AXIS = mybir.AxisListType
+
+P = 128
+B, H, L, D, WINDOW = 2, 16, 512, 64, 4
+E = H * D
+NH = B * H
+NREL = 2 * WINDOW + 1
+QT = L // P
+PACK = 4
+K_PASS = P * PACK
+N_TILE = 512
+PAIRS = NH // 2
+PAIRS_PER_BATCH = H // 2
+BAND_PITCH = 16
+FOLD_WIDTHS = (L // 2, L // 4, L // 8)
+V_CHUNK = 8
+MASKED = -1.0e30
+
+FLOPS = 2 * NH * L * L * D + 2 * NH * L * NREL * D + 2 * B * L * E * E
+
+
+def tile_vitsattention_pa_kernel(tc, logits, v, emb_rel_v, Wo, bo, out):
+    nc = tc.nc
+    flat_logits = logits.rearrange("n t k -> (n t k)")
+
+    with ExitStack() as stack:
+        keep = stack.enter_context(tc.tile_pool(name="keep", bufs=1))
+        logit_pool = stack.enter_context(tc.tile_pool(name="logit_pool", bufs=6))
+        band_pool = stack.enter_context(tc.tile_pool(name="band_pool", bufs=4))
+        fold_pool = stack.enter_context(tc.tile_pool(name="fold_pool", bufs=2))
+        e_pool = stack.enter_context(tc.tile_pool(name="e_pool", bufs=6))
+        grouped_pool = stack.enter_context(tc.tile_pool(name="grouped_pool", bufs=6))
+        code_pool = stack.enter_context(tc.tile_pool(name="code_pool", bufs=4))
+        weight_pool = stack.enter_context(tc.tile_pool(name="weight_pool", bufs=2))
+        attn_pool = stack.enter_context(tc.tile_pool(name="attn_pool", bufs=3))
+        out_pool = stack.enter_context(tc.tile_pool(name="out_pool", bufs=3))
+        psum_words = stack.enter_context(tc.psum_pool(name="psum_words", bufs=4))
+        psum_band = stack.enter_context(tc.psum_pool(name="psum_band", bufs=1))
+        psum_acc = stack.enter_context(tc.psum_pool(name="psum_acc", bufs=3))
+
+        neg_max = keep.tile([P, PAIRS, QT, 2], F32)
+        row_sum = keep.tile([P, PAIRS, QT, 2], F32)
+        inv_sum = keep.tile([P, PAIRS, QT, 2], F32)
+        merged = keep.tile([P, B, QT, E], BF16)
+        v_codes = keep.tile([P, NH * D], U32, align_bytes=64)
+        v_scales = keep.tile([P, NH * D], U8, align_bytes=64)
+        wo_raw = keep.tile([P, E // K_PASS, PACK, E], BF16)
+        wo_codes = keep.tile([P, E // K_PASS, E], U32, align_bytes=64)
+        wo_scales = keep.tile([P, E // K_PASS, E], U8, align_bytes=64)
+        bias_rows = keep.tile([P, E], BF16)
+
+        logit_tiles = {}
+        band_logit_tiles = {}
+        shifted_tiles = {}
+        band_e_tiles = {}
+        band_t_tiles = {}
+        band_bank_tiles = {}
+        e_tiles = {}
+        word_banks = {}
+        grouped_tiles = {}
+        code_tiles = {}
+        v_raw_tiles = {}
+        acc_tiles = {}
+
+        def band_windows(n, t0, rows):
+            start = n * L * L + t0 * (L + 1) - WINDOW
+            run = flat_logits[start : start + rows * (L + 1)]
+            return run.rearrange("(t s) -> t s", s=L + 1)[:, 0:NREL]
+
+        def load_band(band_logits, n, hh):
+            if n == 0:
+                nc.sync.dma_start(
+                    out=band_logits[:, 1:QT, hh, 0:NREL],
+                    in_=band_windows(n, P, L - P).rearrange("(q p) j -> p q j", p=P),
+                )
+                nc.sync.dma_start(out=band_logits[1:P, 0, hh, 0:NREL], in_=band_windows(n, 1, P - 1))
+                nc.sync.dma_start(
+                    out=band_logits[0:1, 0, hh, WINDOW:NREL], in_=flat_logits[0 : WINDOW + 1].unsqueeze(0)
+                )
+            elif n == NH - 1:
+                nc.sync.dma_start(
+                    out=band_logits[:, 0 : QT - 1, hh, 0:NREL],
+                    in_=band_windows(n, 0, L - P).rearrange("(q p) j -> p q j", p=P),
+                )
+                nc.sync.dma_start(
+                    out=band_logits[0 : P - 1, QT - 1, hh, 0:NREL], in_=band_windows(n, L - P, P - 1)
+                )
+                nc.sync.dma_start(
+                    out=band_logits[P - 1 : P, QT - 1, hh, 0 : WINDOW + 1],
+                    in_=flat_logits[NH * L * L - (WINDOW + 1) : NH * L * L].unsqueeze(0),
+                )
+            else:
+                nc.sync.dma_start(
+                    out=band_logits[:, :, hh, 0:NREL],
+                    in_=band_windows(n, 0, L).rearrange("(q p) j -> p q j", p=P),
+                )
+
+        def load_pair(i):
+            band_logits = band_pool.tile([P, QT, 2, BAND_PITCH], BF16, name="band_logits")
+            if i == 0 or i == PAIRS - 1:
+                nc.gpsimd.memset(band_logits[:], 0.0)
+            for hh in range(2):
+                n = 2 * i + hh
+                a = logit_pool.tile([P, QT, L], BF16, name="a")
+                nc.sync.dma_start(out=a[:], in_=logits[n].rearrange("(q p) k -> p q k", p=P))
+                logit_tiles[n] = a
+                load_band(band_logits, n, hh)
+            band_logit_tiles[i] = band_logits
+
+        def load_v(c):
+            v_raw = weight_pool.tile([P, V_CHUNK, PACK, D], BF16, name="v_raw")
+            nc.sync.dma_start(
+                out=v_raw[:].rearrange("p n (u c) d -> p n u (c d)", u=2),
+                in_=v[c * V_CHUNK : (c + 1) * V_CHUNK].rearrange("n (u p c) d -> p n u (c d)", u=2, p=P, c=2),
+            )
+            v_raw_tiles[c] = v_raw
+
+        def load_wo(g):
+            nc.sync.dma_start(
+                out=wo_raw[:, g].rearrange("p (u c) o -> p u (c o)", u=2),
+                in_=Wo[g * K_PASS : (g + 1) * K_PASS, :].rearrange("(u p c) o -> p u (c o)", u=2, p=P, c=2),
+            )
+
+        def quantise_v(c):
+            v_grouped = weight_pool.tile([P, V_CHUNK, D, PACK], BF16, name="v_grouped", align_bytes=64)
+            nc.vector.tensor_copy(out=v_grouped[:], in_=v_raw_tiles[c][:].rearrange("p n t d -> p n d t"))
+            cols = slice(c * V_CHUNK * D, (c + 1) * V_CHUNK * D)
+            nc.vector.quantize_mx(
+                out=v_codes[:, cols].bitcast(FP8X4),
+                scales=v_scales[:, cols],
+                in_=v_grouped[:].rearrange("p n d t -> p (n d t)"),
+            )
+
+        def quantise_wo(w):
+            g, half = divmod(w, E // N_TILE)
+            cols = slice(half * N_TILE, (half + 1) * N_TILE)
+            wo_grouped = weight_pool.tile([P, N_TILE, PACK], BF16, name="wo_grouped", align_bytes=64)
+            nc.vector.tensor_copy(out=wo_grouped[:], in_=wo_raw[:, g, :, cols].rearrange("p t o -> p o t"))
+            nc.vector.quantize_mx(
+                out=wo_codes[:, g, cols].bitcast(FP8X4),
+                scales=wo_scales[:, g, cols],
+                in_=wo_grouped[:].rearrange("p o t -> p (o t)"),
+            )
+
+        def row_max(i):
+            narrowed = {0: logit_tiles[2 * i], 1: logit_tiles[2 * i + 1]}
+            for width in FOLD_WIDTHS:
+                for hh in range(2):
+                    folded = fold_pool.tile([P, QT, width], BF16, name="folded", tag="folded_%d_%d" % (width, hh))
+                    nc.vector.tensor_tensor(
+                        out=folded[:],
+                        in0=narrowed[hh][:, :, 0:width],
+                        in1=narrowed[hh][:, :, width : 2 * width],
+                        op=ALU.max,
+                    )
+                    narrowed[hh] = folded
+            for hh in range(2):
+                nc.vector.tensor_reduce(
+                    out=neg_max[:, i, :, hh], in_=narrowed[hh][:], axis=AXIS.X, op=ALU.max, negate=True
+                )
+
+        def exponentials(n):
+            i, hh = divmod(n, 2)
+            e = e_pool.tile([P, QT, L], BF16, name="e")
+            for q in range(QT):
+                nc.scalar.activation(
+                    out=e[:, q, :],
+                    in_=logit_tiles[n][:, q, :],
+                    func=ACT.Exp,
+                    bias=neg_max[:, i, q, hh : hh + 1],
+                    scale=1.0,
+                    accum_out=row_sum[:, i, q, hh : hh + 1],
+                )
+            e_tiles[n] = e
+
+        def transpose_words(key, words, first_word):
+            for half in range(2):
+                bank = psum_words.tile([P, 2, 2 * P], F32, name="bank")
+                for u in range(2):
+                    for r in range(2):
+                        nc.tensor.transpose(
+                            bank[:, u, r * P : (r + 1) * P],
+                            words[:, 2 * half + r, first_word + u * P : first_word + (u + 1) * P],
+                            ident[:],
+                        )
+                word_banks[(key, half)] = bank
+
+        def regroup_words(key, copies):
+            grouped = grouped_pool.tile([P, L, PACK], BF16, name="grouped", align_bytes=64)
+            grouped_words = grouped[:].bitcast(F32)
+            for half in range(2):
+                source = word_banks[(key, half)][:].rearrange("p u r -> p r u")
+                target = grouped_words[:, half * 2 * P : (half + 1) * 2 * P, :]
+                copies[half](out=target, in_=source)
+            grouped_tiles[key] = grouped
+
+        def quantise_rows(key):
+            codes = code_pool.tile([P, L], U32, name="codes", align_bytes=64)
+            scales = code_pool.tile([P, L], U8, name="scales", align_bytes=64)
+            nc.vector.quantize_mx(
+                out=codes[:].bitcast(FP8X4),
+                scales=scales[:],
+                in_=grouped_tiles[key][:].rearrange("p r t -> p (r t)"),
+            )
+            code_tiles[key] = (codes, scales)
+
+        def context(i):
+            ctx = psum_acc.tile([P, N_TILE], F32, name="ctx", tag="acc")
+            ctx_view = ctx[:].rearrange("p (q h d) -> p q h d", q=QT, h=2)
+            for hh in range(2):
+                n = 2 * i + hh
+                codes, scales = code_tiles[("e", n)]
+                for q in range(QT):
+                    nc.tensor.matmul_mx(
+                        out=ctx_view[:, q, hh, :],
+                        lhsT=codes[:, q * P : (q + 1) * P].bitcast(FP8X4),
+                        lhsT_scale=scales[:, q * P : (q + 1) * P],
+                        rhs=v_codes[:, n * D : (n + 1) * D].bitcast(FP8X4),
+                        rhs_scale=v_scales[:, n * D : (n + 1) * D],
+                        start=True,
+                        stop=True,
+                    )
+            acc_tiles[("ctx", i)] = ctx
+
+        def shift_band(i):
+            shifted = band_pool.tile([P, QT, 2, NREL], F32, name="shifted")
+            nc.gpsimd.tensor_tensor(
+                out=shifted[:],
+                in0=band_logit_tiles[i][:, :, :, 0:NREL],
+                in1=neg_max[:, i].unsqueeze(3).to_broadcast([P, QT, 2, NREL]),
+                op=ALU.add,
+            )
+            nc.gpsimd.tensor_tensor(out=shifted[:], in0=shifted[:], in1=edge_mask[:], op=ALU.add)
+            shifted_tiles[i] = shifted
+
+        def band_exponentials(i):
+            band_e = band_pool.tile([P, QT, 2, NREL], F32, name="band_e")
+            nc.scalar.activation(out=band_e[:], in_=shifted_tiles[i][:], func=ACT.Exp)
+            band_e_tiles[i] = band_e
+
+        def normalise_band(i):
+            nc.vector.reciprocal(out=inv_sum[:, i], in_=row_sum[:, i])
+            padded = band_padded[i % 2]
+            nc.gpsimd.tensor_tensor(
+                out=padded[:, 0 : 2 * QT * NREL].rearrange("p (q h j) -> p q h j", q=QT, h=2),
+                in0=band_e_tiles[i][:],
+                in1=inv_sum[:, i].unsqueeze(3).to_broadcast([P, QT, 2, NREL]),
+                op=ALU.mult,
+            )
+
+        def transpose_band(i):
+            band_bank = psum_band.tile([P, P], F32, name="band_bank")
+            nc.tensor.transpose(band_bank[:], band_padded[i % 2][:], ident[:])
+            band_bank_tiles[i] = band_bank
+
+        def keep_band(i):
+            band_t = attn_pool.tile([P, P], F32, name="band_t")
+            nc.vector.tensor_copy(out=band_t[:], in_=band_bank_tiles[i][:])
+            band_t_tiles[i] = band_t
+
+        def relative(i):
+            rel = psum_acc.tile([P, N_TILE], F32, name="rel", tag="acc")
+            nc.tensor.matmul(out=rel[:], lhsT=band_t_tiles[i][:], rhs=rel_rows[:], start=True, stop=True)
+            acc_tiles[("rel", i)] = rel
+
+        def attention(i):
+            b, pair_in_batch = divmod(i, PAIRS_PER_BATCH)
+            scaled = attn_pool.tile([P, N_TILE], F32, name="scaled")
+            nc.vector.tensor_tensor(
+                out=scaled[:].rearrange("p (q h d) -> p q h d", q=QT, h=2),
+                in0=acc_tiles[("ctx", i)][:].rearrange("p (q h d) -> p q h d", q=QT, h=2),
+                in1=inv_sum[:, i].unsqueeze(3).to_broadcast([P, QT, 2, D]),
+                op=ALU.mult,
+            )
+            nc.vector.tensor_tensor(
+                out=merged[:, b, :, pair_in_batch * 2 * D : (pair_in_batch + 1) * 2 * D],
+                in0=scaled[:].rearrange("p (q c) -> p q c", q=QT),
+                in1=acc_tiles[("rel", i)][:].rearrange("p (q c) -> p q c", q=QT),
+                op=ALU.add,
+            )
+
+        def project(b):
+            merged_words = merged[:, b].bitcast(F32)
+            for g in range(E // K_PASS):
+                transpose_words(("m", g), merged_words, g * K_PASS // 2)
+                regroup_words(("m", g), (nc.scalar.copy, nc.vector.tensor_copy))
+            for g in range(E // K_PASS):
+                quantise_rows(("m", g))
+            for q in range(QT):
+                result = out_pool.tile([P, E], F32, name="result")
+                for half in range(E // N_TILE):
+                    cols = slice(half * N_TILE, (half + 1) * N_TILE)
+                    acc = psum_acc.tile([P, N_TILE], F32, name="acc", tag="acc")
+                    for g in range(E // K_PASS):
+                        codes, scales = code_tiles[("m", g)]
+                        nc.tensor.matmul_mx(
+                            out=acc[:],
+                            lhsT=codes[:, q * P : (q + 1) * P].bitcast(FP8X4),
+                            lhsT_scale=scales[:, q * P : (q + 1) * P],
+                            rhs=wo_codes[:, g, cols].bitcast(FP8X4),
+                            rhs_scale=wo_scales[:, g, cols],
+                            start=(g == 0),
+                            stop=(g == E // K_PASS - 1),
+                        )
+                    nc.vector.tensor_tensor(out=result[:, cols], in0=acc[:], in1=bias_rows[:, cols], op=ALU.add)
+                nc.sync.dma_start(out=out[b, q * P : (q + 1) * P, :], in_=result[:])
+
+        load_pair(0)
+        load_v(0)
+        load_pair(1)
+
+        ident = keep.tile([P, P], F32)
+        make_identity(nc, ident[:])
+
+        edge_mask = keep.tile([P, QT, 2, NREL], F32)
+        nc.gpsimd.memset(edge_mask[:], 0.0)
+        nc.gpsimd.affine_select(
+            out=edge_mask[:], in_=edge_mask[:], pattern=[[P, QT], [0, 2], [1, NREL]],
+            compare_op=ALU.is_ge, fill=MASKED, base=-WINDOW, channel_multiplier=1,
+        )
+        nc.gpsimd.affine_select(
+            out=edge_mask[:], in_=edge_mask[:], pattern=[[-P, QT], [0, 2], [-1, NREL]],
+            compare_op=ALU.is_ge, fill=MASKED, base=L - 1 + WINDOW, channel_multiplier=-1,
+        )
+
+        band_padded_0 = keep.tile([P, P], F32)
+        band_padded_1 = keep.tile([P, P], F32)
+        band_padded = (band_padded_0, band_padded_1)
+        nc.gpsimd.memset(band_padded_0[:], 0.0)
+        nc.gpsimd.memset(band_padded_1[:], 0.0)
+
+        rel_rows_bf16 = keep.tile([P, N_TILE], BF16)
+        nc.vector.memset(rel_rows_bf16[:], 0.0)
+        for tile_of_pair in range(2 * QT):
+            nc.scalar.dma_start(
+                out=rel_rows_bf16[
+                    tile_of_pair * NREL : (tile_of_pair + 1) * NREL, tile_of_pair * D : (tile_of_pair + 1) * D
+                ],
+                in_=emb_rel_v[0],
+            )
+        rel_rows = keep.tile([P, N_TILE], F32)
+        nc.vector.tensor_copy(out=rel_rows[:], in_=rel_rows_bf16[:])
+
+        row_max(0)
+
+        for s in range(PAIRS + 2):
+            if s + 2 < PAIRS:
+                load_pair(s + 2)
+            if s % 4 == 0 and s // 4 + 1 < NH // V_CHUNK:
+                load_v(s // 4 + 1)
+            if s < E // K_PASS:
+                load_wo(s)
+            if s == E // K_PASS:
+                nc.sync.dma_start(out=bias_rows[:], in_=bo.partition_broadcast(P))
+
+            if 0 <= s - 1 < PAIRS:
+                normalise_band(s - 1)
+                transpose_words(("e", 2 * s - 2), e_tiles[2 * s - 2][:].bitcast(F32), 0)
+                transpose_words(("e", 2 * s - 1), e_tiles[2 * s - 1][:].bitcast(F32), 0)
+                transpose_band(s - 1)
+            if s < PAIRS:
+                shift_band(s)
+            if 0 <= s - 2 < PAIRS:
+                quantise_rows(("e", 2 * s - 4))
+                quantise_rows(("e", 2 * s - 3))
+                relative(s - 2)
+                context(s - 2)
+            for hh in range(2):
+                if s < PAIRS:
+                    exponentials(2 * s + hh)
+                if 0 <= s - 1 < PAIRS:
+                    regroup_words(("e", 2 * s - 2 + hh), (nc.scalar.copy, nc.scalar.copy))
+            if s < PAIRS:
+                band_exponentials(s)
+            if s + 1 < PAIRS:
+                row_max(s + 1)
+            if s % 4 == 0 and s // 4 < NH // V_CHUNK:
+                quantise_v(s // 4)
+            if s % 2 == 1 and s // 2 < 2 * E // N_TILE:
+                quantise_wo(s // 2)
+            if 0 <= s - 1 < PAIRS:
+                keep_band(s - 1)
+            if 0 <= s - 2 < PAIRS:
+                attention(s - 2)
+                if (s - 2) % PAIRS_PER_BATCH == PAIRS_PER_BATCH - 1:
+                    project((s - 2) // PAIRS_PER_BATCH)

@@ -20,15 +20,23 @@ NREL = 2 * WINDOW + 1
 QT = L // P
 PACK = 4
 K_PASS = P * PACK
+PASSES = E // K_PASS
 N_TILE = 512
-PAIRS = NH // 2
-PAIRS_PER_BATCH = H // 2
+QUAD = 4
+UNIT = 2 * QUAD
+UNITS = NH * QT // UNIT
+BLOCKS = UNITS // 2
 BAND_PITCH = 16
 FOLD_WIDTHS = (L // 2, L // 4, L // 8)
-V_CHUNK = 8
 MASKED = -1.0e30
 
 FLOPS = 2 * NH * L * L * D + 2 * NH * L * NREL * D + 2 * B * L * E * E
+
+
+def place_of_unit(i):
+    block, half = divmod(i, 2)
+    b, q = divmod(block, QT)
+    return b, q, half, b * H + half * UNIT
 
 
 def tile_vitsattention_pa_kernel(tc, logits, v, emb_rel_v, Wo, bo, out):
@@ -38,7 +46,7 @@ def tile_vitsattention_pa_kernel(tc, logits, v, emb_rel_v, Wo, bo, out):
     with ExitStack() as stack:
         keep = stack.enter_context(tc.tile_pool(name="keep", bufs=1))
         logit_pool = stack.enter_context(tc.tile_pool(name="logit_pool", bufs=6))
-        band_pool = stack.enter_context(tc.tile_pool(name="band_pool", bufs=4))
+        band_pool = stack.enter_context(tc.tile_pool(name="band_pool", bufs=3))
         fold_pool = stack.enter_context(tc.tile_pool(name="fold_pool", bufs=2))
         e_pool = stack.enter_context(tc.tile_pool(name="e_pool", bufs=6))
         grouped_pool = stack.enter_context(tc.tile_pool(name="grouped_pool", bufs=6))
@@ -47,85 +55,81 @@ def tile_vitsattention_pa_kernel(tc, logits, v, emb_rel_v, Wo, bo, out):
         attn_pool = stack.enter_context(tc.tile_pool(name="attn_pool", bufs=3))
         out_pool = stack.enter_context(tc.tile_pool(name="out_pool", bufs=3))
         psum_words = stack.enter_context(tc.psum_pool(name="psum_words", bufs=4))
-        psum_band = stack.enter_context(tc.psum_pool(name="psum_band", bufs=1))
-        psum_acc = stack.enter_context(tc.psum_pool(name="psum_acc", bufs=3))
+        psum_acc = stack.enter_context(tc.psum_pool(name="psum_acc", bufs=4))
 
-        neg_max = keep.tile([P, PAIRS, QT, 2], F32)
-        row_sum = keep.tile([P, PAIRS, QT, 2], F32)
-        inv_sum = keep.tile([P, PAIRS, QT, 2], F32)
-        merged = keep.tile([P, B, QT, E], BF16)
+        neg_max = keep.tile([P, UNITS, UNIT], F32)
+        row_sum = keep.tile([P, UNITS, UNIT], F32)
+        inv_sum = keep.tile([P, UNITS, UNIT], F32)
+        band_logits = keep.tile([P, QT, NH, BAND_PITCH], BF16)
+        v_raw = keep.tile([P, NH, PACK, D], BF16)
         v_codes = keep.tile([P, NH * D], U32, align_bytes=64)
         v_scales = keep.tile([P, NH * D], U8, align_bytes=64)
-        wo_raw = keep.tile([P, E // K_PASS, PACK, E], BF16)
-        wo_codes = keep.tile([P, E // K_PASS, E], U32, align_bytes=64)
-        wo_scales = keep.tile([P, E // K_PASS, E], U8, align_bytes=64)
+        wo_raw = keep.tile([P, PASSES, PACK, E], BF16)
+        wo_codes = keep.tile([P, PASSES, E], U32, align_bytes=64)
+        wo_scales = keep.tile([P, PASSES, E], U8, align_bytes=64)
         bias_rows = keep.tile([P, E], BF16)
 
         logit_tiles = {}
-        band_logit_tiles = {}
         shifted_tiles = {}
         band_e_tiles = {}
-        band_t_tiles = {}
         band_bank_tiles = {}
+        band_t_tiles = {}
         e_tiles = {}
         word_banks = {}
         grouped_tiles = {}
         code_tiles = {}
-        v_raw_tiles = {}
         acc_tiles = {}
+        merged_tiles = {}
 
-        def band_windows(n, t0, rows):
-            start = n * L * L + t0 * (L + 1) - WINDOW
-            run = flat_logits[start : start + rows * (L + 1)]
-            return run.rearrange("(t s) -> t s", s=L + 1)[:, 0:NREL]
-
-        def load_band(band_logits, n, hh):
-            if n == 0:
-                nc.sync.dma_start(
-                    out=band_logits[:, 1:QT, hh, 0:NREL],
-                    in_=band_windows(n, P, L - P).rearrange("(q p) j -> p q j", p=P),
-                )
-                nc.sync.dma_start(out=band_logits[1:P, 0, hh, 0:NREL], in_=band_windows(n, 1, P - 1))
-                nc.sync.dma_start(
-                    out=band_logits[0:1, 0, hh, WINDOW:NREL], in_=flat_logits[0 : WINDOW + 1].unsqueeze(0)
-                )
-            elif n == NH - 1:
-                nc.sync.dma_start(
-                    out=band_logits[:, 0 : QT - 1, hh, 0:NREL],
-                    in_=band_windows(n, 0, L - P).rearrange("(q p) j -> p q j", p=P),
-                )
-                nc.sync.dma_start(
-                    out=band_logits[0 : P - 1, QT - 1, hh, 0:NREL], in_=band_windows(n, L - P, P - 1)
-                )
-                nc.sync.dma_start(
-                    out=band_logits[P - 1 : P, QT - 1, hh, 0 : WINDOW + 1],
-                    in_=flat_logits[NH * L * L - (WINDOW + 1) : NH * L * L].unsqueeze(0),
-                )
+        def band_windows(first_head, heads, t0, rows):
+            start = first_head * L * L + t0 * (L + 1) - WINDOW
+            if heads == 1:
+                by_head = flat_logits[start : start + rows * (L + 1)].unsqueeze(0)
             else:
-                nc.sync.dma_start(
-                    out=band_logits[:, :, hh, 0:NREL],
-                    in_=band_windows(n, 0, L).rearrange("(q p) j -> p q j", p=P),
-                )
+                whole_heads = flat_logits[start : start + heads * L * L].rearrange("(n r) -> n r", n=heads)
+                by_head = whole_heads[:, 0 : rows * (L + 1)]
+            return by_head.rearrange("n (t s) -> t n s", s=L + 1)[:, :, 0:NREL]
 
-        def load_pair(i):
-            band_logits = band_pool.tile([P, QT, 2, BAND_PITCH], BF16, name="band_logits")
-            if i == 0 or i == PAIRS - 1:
-                nc.gpsimd.memset(band_logits[:], 0.0)
-            for hh in range(2):
-                n = 2 * i + hh
-                a = logit_pool.tile([P, QT, L], BF16, name="a")
-                nc.sync.dma_start(out=a[:], in_=logits[n].rearrange("(q p) k -> p q k", p=P))
-                logit_tiles[n] = a
-                load_band(band_logits, n, hh)
-            band_logit_tiles[i] = band_logits
+        def load_band(q):
+            if q == 0:
+                nc.sync.dma_start(out=band_logits[:, q, 1:NH, 0:NREL], in_=band_windows(1, NH - 1, 0, P))
+                nc.gpsimd.memset(band_logits[:, q, 0, :], 0.0)
+                nc.sync.dma_start(out=band_logits[1:P, q, 0:1, 0:NREL], in_=band_windows(0, 1, 1, P - 1))
+                nc.sync.dma_start(
+                    out=band_logits[0:1, q, 0, WINDOW:NREL], in_=flat_logits[0 : WINDOW + 1].unsqueeze(0)
+                )
+                return
+            nc.sync.dma_start(out=band_logits[:, q, 0 : NH - 1, 0:NREL], in_=band_windows(0, NH - 1, q * P, P))
+            if q < QT - 1:
+                nc.sync.dma_start(
+                    out=band_logits[:, q, NH - 1 : NH, 0:NREL], in_=band_windows(NH - 1, 1, q * P, P)
+                )
+                return
+            nc.gpsimd.memset(band_logits[:, q, NH - 1, :], 0.0)
+            nc.sync.dma_start(
+                out=band_logits[0 : P - 1, q, NH - 1 : NH, 0:NREL], in_=band_windows(NH - 1, 1, q * P, P - 1)
+            )
+            nc.sync.dma_start(
+                out=band_logits[P - 1 : P, q, NH - 1, 0 : WINDOW + 1],
+                in_=flat_logits[NH * L * L - (WINDOW + 1) : NH * L * L].unsqueeze(0),
+            )
+
+        def load_unit(i):
+            b, q, half, first_head = place_of_unit(i)
+            for x in range(2):
+                n = first_head + x * QUAD
+                a = logit_pool.tile([P, QUAD, L], BF16, name="a")
+                nc.sync.dma_start(
+                    out=a[:], in_=logits[n : n + QUAD, q * P : (q + 1) * P, :].rearrange("n p k -> p n k")
+                )
+                logit_tiles[(i, x)] = a
 
         def load_v(c):
-            v_raw = weight_pool.tile([P, V_CHUNK, PACK, D], BF16, name="v_raw")
+            heads = slice(c * UNIT, (c + 1) * UNIT)
             nc.sync.dma_start(
-                out=v_raw[:].rearrange("p n (u c) d -> p n u (c d)", u=2),
-                in_=v[c * V_CHUNK : (c + 1) * V_CHUNK].rearrange("n (u p c) d -> p n u (c d)", u=2, p=P, c=2),
+                out=v_raw[:, heads].rearrange("p n (u c) d -> p n u (c d)", u=2),
+                in_=v[heads].rearrange("n (u p c) d -> p n u (c d)", u=2, p=P, c=2),
             )
-            v_raw_tiles[c] = v_raw
 
         def load_wo(g):
             nc.sync.dma_start(
@@ -134,9 +138,10 @@ def tile_vitsattention_pa_kernel(tc, logits, v, emb_rel_v, Wo, bo, out):
             )
 
         def quantise_v(c):
-            v_grouped = weight_pool.tile([P, V_CHUNK, D, PACK], BF16, name="v_grouped", align_bytes=64)
-            nc.vector.tensor_copy(out=v_grouped[:], in_=v_raw_tiles[c][:].rearrange("p n t d -> p n d t"))
-            cols = slice(c * V_CHUNK * D, (c + 1) * V_CHUNK * D)
+            heads = slice(c * UNIT, (c + 1) * UNIT)
+            cols = slice(c * UNIT * D, (c + 1) * UNIT * D)
+            v_grouped = weight_pool.tile([P, UNIT, D, PACK], BF16, name="v_grouped", align_bytes=64)
+            nc.vector.tensor_copy(out=v_grouped[:], in_=v_raw[:, heads].rearrange("p n t d -> p n d t"))
             nc.vector.quantize_mx(
                 out=v_codes[:, cols].bitcast(FP8X4),
                 scales=v_scales[:, cols],
@@ -155,113 +160,125 @@ def tile_vitsattention_pa_kernel(tc, logits, v, emb_rel_v, Wo, bo, out):
             )
 
         def row_max(i):
-            narrowed = {0: logit_tiles[2 * i], 1: logit_tiles[2 * i + 1]}
+            narrowed = {0: logit_tiles[(i, 0)], 1: logit_tiles[(i, 1)]}
             for width in FOLD_WIDTHS:
-                for hh in range(2):
-                    folded = fold_pool.tile([P, QT, width], BF16, name="folded", tag="folded_%d_%d" % (width, hh))
+                for x in range(2):
+                    folded = fold_pool.tile([P, QUAD, width], BF16, name="folded", tag="folded_%d_%d" % (width, x))
                     nc.vector.tensor_tensor(
                         out=folded[:],
-                        in0=narrowed[hh][:, :, 0:width],
-                        in1=narrowed[hh][:, :, width : 2 * width],
+                        in0=narrowed[x][:, :, 0:width],
+                        in1=narrowed[x][:, :, width : 2 * width],
                         op=ALU.max,
                     )
-                    narrowed[hh] = folded
-            for hh in range(2):
+                    narrowed[x] = folded
+            for x in range(2):
                 nc.vector.tensor_reduce(
-                    out=neg_max[:, i, :, hh], in_=narrowed[hh][:], axis=AXIS.X, op=ALU.max, negate=True
+                    out=neg_max[:, i, x * QUAD : (x + 1) * QUAD],
+                    in_=narrowed[x][:],
+                    axis=AXIS.X,
+                    op=ALU.max,
+                    negate=True,
                 )
 
-        def exponentials(n):
-            i, hh = divmod(n, 2)
-            e = e_pool.tile([P, QT, L], BF16, name="e")
-            for q in range(QT):
+        def exponentials(i, x):
+            e = e_pool.tile([P, QUAD, L], BF16, name="e")
+            for j in range(QUAD):
+                head = x * QUAD + j
                 nc.scalar.activation(
-                    out=e[:, q, :],
-                    in_=logit_tiles[n][:, q, :],
+                    out=e[:, j, :],
+                    in_=logit_tiles[(i, x)][:, j, :],
                     func=ACT.Exp,
-                    bias=neg_max[:, i, q, hh : hh + 1],
+                    bias=neg_max[:, i, head : head + 1],
                     scale=1.0,
-                    accum_out=row_sum[:, i, q, hh : hh + 1],
+                    accum_out=row_sum[:, i, head : head + 1],
                 )
-            e_tiles[n] = e
+            e_tiles[(i, x)] = e
 
-        def transpose_words(key, words, first_word):
+        def transpose_keys(i, x):
+            words = e_tiles[(i, x)][:].bitcast(F32)
             for half in range(2):
                 bank = psum_words.tile([P, 2, 2 * P], F32, name="bank")
                 for u in range(2):
                     for r in range(2):
                         nc.tensor.transpose(
-                            bank[:, u, r * P : (r + 1) * P],
-                            words[:, 2 * half + r, first_word + u * P : first_word + (u + 1) * P],
-                            ident[:],
+                            bank[:, u, r * P : (r + 1) * P], words[:, 2 * half + r, u * P : (u + 1) * P], ident[:]
                         )
-                word_banks[(key, half)] = bank
+                word_banks[(i, x, half)] = bank
 
-        def regroup_words(key, copies):
-            grouped = grouped_pool.tile([P, L, PACK], BF16, name="grouped", align_bytes=64)
+        def regroup_keys(i, x, copies):
+            grouped = grouped_pool.tile([P, QUAD * P, PACK], BF16, name="grouped", align_bytes=64)
             grouped_words = grouped[:].bitcast(F32)
             for half in range(2):
-                source = word_banks[(key, half)][:].rearrange("p u r -> p r u")
-                target = grouped_words[:, half * 2 * P : (half + 1) * 2 * P, :]
-                copies[half](out=target, in_=source)
-            grouped_tiles[key] = grouped
+                copies[half](
+                    out=grouped_words[:, half * 2 * P : (half + 1) * 2 * P, :],
+                    in_=word_banks[(i, x, half)][:].rearrange("p u r -> p r u"),
+                )
+            grouped_tiles[(i, x)] = grouped
 
-        def quantise_rows(key):
-            codes = code_pool.tile([P, L], U32, name="codes", align_bytes=64)
-            scales = code_pool.tile([P, L], U8, name="scales", align_bytes=64)
+        def quantise_keys(i, x):
+            codes = code_pool.tile([P, QUAD * P], U32, name="codes", align_bytes=64)
+            scales = code_pool.tile([P, QUAD * P], U8, name="scales", align_bytes=64)
             nc.vector.quantize_mx(
                 out=codes[:].bitcast(FP8X4),
                 scales=scales[:],
-                in_=grouped_tiles[key][:].rearrange("p r t -> p (r t)"),
+                in_=grouped_tiles[(i, x)][:].rearrange("p r t -> p (r t)"),
             )
-            code_tiles[key] = (codes, scales)
+            code_tiles[(i, x)] = (codes, scales)
 
         def context(i):
-            ctx = psum_acc.tile([P, N_TILE], F32, name="ctx", tag="acc")
-            ctx_view = ctx[:].rearrange("p (q h d) -> p q h d", q=QT, h=2)
-            for hh in range(2):
-                n = 2 * i + hh
-                codes, scales = code_tiles[("e", n)]
-                for q in range(QT):
-                    nc.tensor.matmul_mx(
-                        out=ctx_view[:, q, hh, :],
-                        lhsT=codes[:, q * P : (q + 1) * P].bitcast(FP8X4),
-                        lhsT_scale=scales[:, q * P : (q + 1) * P],
-                        rhs=v_codes[:, n * D : (n + 1) * D].bitcast(FP8X4),
-                        rhs_scale=v_scales[:, n * D : (n + 1) * D],
-                        start=True,
-                        stop=True,
-                    )
+            first_head = place_of_unit(i)[3]
+            ctx = psum_acc.tile([P, UNIT * D], F32, name="ctx", tag="acc")
+            for head in range(UNIT):
+                x, j = divmod(head, QUAD)
+                n = first_head + head
+                codes, scales = code_tiles[(i, x)]
+                nc.tensor.matmul_mx(
+                    out=ctx[:, head * D : (head + 1) * D],
+                    lhsT=codes[:, j * P : (j + 1) * P].bitcast(FP8X4),
+                    lhsT_scale=scales[:, j * P : (j + 1) * P],
+                    rhs=v_codes[:, n * D : (n + 1) * D].bitcast(FP8X4),
+                    rhs_scale=v_scales[:, n * D : (n + 1) * D],
+                    start=True,
+                    stop=True,
+                )
             acc_tiles[("ctx", i)] = ctx
 
         def shift_band(i):
-            shifted = band_pool.tile([P, QT, 2, NREL], F32, name="shifted")
+            b, q, half, first_head = place_of_unit(i)
+            shifted = band_pool.tile([P, UNIT, NREL], F32, name="shifted")
             nc.gpsimd.tensor_tensor(
                 out=shifted[:],
-                in0=band_logit_tiles[i][:, :, :, 0:NREL],
-                in1=neg_max[:, i].unsqueeze(3).to_broadcast([P, QT, 2, NREL]),
+                in0=band_logits[:, q, first_head : first_head + UNIT, 0:NREL],
+                in1=neg_max[:, i].unsqueeze(2).to_broadcast([P, UNIT, NREL]),
                 op=ALU.add,
             )
-            nc.gpsimd.tensor_tensor(out=shifted[:], in0=shifted[:], in1=edge_mask[:], op=ALU.add)
+            if q == 0 or q == QT - 1:
+                nc.gpsimd.tensor_tensor(
+                    out=shifted[:],
+                    in0=shifted[:],
+                    in1=edge_mask[:, q].unsqueeze(1).to_broadcast([P, UNIT, NREL]),
+                    op=ALU.add,
+                )
             shifted_tiles[i] = shifted
 
         def band_exponentials(i):
-            band_e = band_pool.tile([P, QT, 2, NREL], F32, name="band_e")
+            band_e = band_pool.tile([P, UNIT, NREL], F32, name="band_e")
             nc.scalar.activation(out=band_e[:], in_=shifted_tiles[i][:], func=ACT.Exp)
             band_e_tiles[i] = band_e
 
-        def normalise_band(i):
+        def invert_sums(i):
             nc.vector.reciprocal(out=inv_sum[:, i], in_=row_sum[:, i])
-            padded = band_padded[i % 2]
+
+        def normalise_band(i):
             nc.gpsimd.tensor_tensor(
-                out=padded[:, 0 : 2 * QT * NREL].rearrange("p (q h j) -> p q h j", q=QT, h=2),
+                out=band_padded[i % 2][:, 0 : UNIT * NREL].rearrange("p (h j) -> p h j", h=UNIT),
                 in0=band_e_tiles[i][:],
-                in1=inv_sum[:, i].unsqueeze(3).to_broadcast([P, QT, 2, NREL]),
+                in1=inv_sum[:, i].unsqueeze(2).to_broadcast([P, UNIT, NREL]),
                 op=ALU.mult,
             )
 
         def transpose_band(i):
-            band_bank = psum_band.tile([P, P], F32, name="band_bank")
+            band_bank = psum_acc.tile([P, P], F32, name="band_bank", tag="acc")
             nc.tensor.transpose(band_bank[:], band_padded[i % 2][:], ident[:])
             band_bank_tiles[i] = band_bank
 
@@ -271,67 +288,98 @@ def tile_vitsattention_pa_kernel(tc, logits, v, emb_rel_v, Wo, bo, out):
             band_t_tiles[i] = band_t
 
         def relative(i):
-            rel = psum_acc.tile([P, N_TILE], F32, name="rel", tag="acc")
+            rel = psum_acc.tile([P, UNIT * D], F32, name="rel", tag="acc")
             nc.tensor.matmul(out=rel[:], lhsT=band_t_tiles[i][:], rhs=rel_rows[:], start=True, stop=True)
             acc_tiles[("rel", i)] = rel
 
         def attention(i):
-            b, pair_in_batch = divmod(i, PAIRS_PER_BATCH)
-            scaled = attn_pool.tile([P, N_TILE], F32, name="scaled")
+            block, half = divmod(i, 2)
+            if half == 0:
+                merged = attn_pool.tile([P, E], BF16, name="merged")
+                merged_tiles[block] = merged
+            scaled = attn_pool.tile([P, UNIT * D], F32, name="scaled")
             nc.vector.tensor_tensor(
-                out=scaled[:].rearrange("p (q h d) -> p q h d", q=QT, h=2),
-                in0=acc_tiles[("ctx", i)][:].rearrange("p (q h d) -> p q h d", q=QT, h=2),
-                in1=inv_sum[:, i].unsqueeze(3).to_broadcast([P, QT, 2, D]),
+                out=scaled[:].rearrange("p (h d) -> p h d", h=UNIT),
+                in0=acc_tiles[("ctx", i)][:].rearrange("p (h d) -> p h d", h=UNIT),
+                in1=inv_sum[:, i].unsqueeze(2).to_broadcast([P, UNIT, D]),
                 op=ALU.mult,
             )
             nc.vector.tensor_tensor(
-                out=merged[:, b, :, pair_in_batch * 2 * D : (pair_in_batch + 1) * 2 * D],
-                in0=scaled[:].rearrange("p (q c) -> p q c", q=QT),
-                in1=acc_tiles[("rel", i)][:].rearrange("p (q c) -> p q c", q=QT),
+                out=merged_tiles[block][:, half * UNIT * D : (half + 1) * UNIT * D],
+                in0=scaled[:],
+                in1=acc_tiles[("rel", i)][:],
                 op=ALU.add,
             )
 
-        def project(b):
-            merged_words = merged[:, b].bitcast(F32)
-            for g in range(E // K_PASS):
-                transpose_words(("m", g), merged_words, g * K_PASS // 2)
-                regroup_words(("m", g), (nc.scalar.copy, nc.vector.tensor_copy))
-            for g in range(E // K_PASS):
-                quantise_rows(("m", g))
-            for q in range(QT):
-                result = out_pool.tile([P, E], F32, name="result")
-                for half in range(E // N_TILE):
-                    cols = slice(half * N_TILE, (half + 1) * N_TILE)
-                    acc = psum_acc.tile([P, N_TILE], F32, name="acc", tag="acc")
-                    for g in range(E // K_PASS):
-                        codes, scales = code_tiles[("m", g)]
-                        nc.tensor.matmul_mx(
-                            out=acc[:],
-                            lhsT=codes[:, q * P : (q + 1) * P].bitcast(FP8X4),
-                            lhsT_scale=scales[:, q * P : (q + 1) * P],
-                            rhs=wo_codes[:, g, cols].bitcast(FP8X4),
-                            rhs_scale=wo_scales[:, g, cols],
-                            start=(g == 0),
-                            stop=(g == E // K_PASS - 1),
-                        )
-                    nc.vector.tensor_tensor(out=result[:, cols], in0=acc[:], in1=bias_rows[:, cols], op=ALU.add)
-                nc.sync.dma_start(out=out[b, q * P : (q + 1) * P, :], in_=result[:])
+        def transpose_merged(block):
+            words = merged_tiles[block][:].bitcast(F32)
+            bank = psum_words.tile([P, PASSES, 2 * P], F32, name="bank")
+            for g in range(PASSES):
+                for u in range(2):
+                    nc.tensor.transpose(
+                        bank[:, g, u * P : (u + 1) * P], words[:, (2 * g + u) * P : (2 * g + u + 1) * P], ident[:]
+                    )
+            word_banks[block] = bank
 
-        load_pair(0)
-        load_v(0)
-        load_pair(1)
+        def regroup_merged(block):
+            m_grouped = grouped_pool.tile([P, PASSES, P, PACK], BF16, name="m_grouped", align_bytes=64)
+            nc.vector.tensor_copy(
+                out=m_grouped[:].bitcast(F32), in_=word_banks[block][:].rearrange("p g (u r) -> p g r u", u=2)
+            )
+            grouped_tiles[block] = m_grouped
+
+        def quantise_merged(block):
+            m_codes = code_pool.tile([P, PASSES * P], U32, name="m_codes", align_bytes=64)
+            m_scales = code_pool.tile([P, PASSES * P], U8, name="m_scales", align_bytes=64)
+            nc.vector.quantize_mx(
+                out=m_codes[:].bitcast(FP8X4),
+                scales=m_scales[:],
+                in_=grouped_tiles[block][:].rearrange("p g r t -> p (g r t)"),
+            )
+            code_tiles[block] = (m_codes, m_scales)
+
+        def project(block):
+            m_codes, m_scales = code_tiles[block]
+            for half in range(E // N_TILE):
+                cols = slice(half * N_TILE, (half + 1) * N_TILE)
+                acc = psum_acc.tile([P, N_TILE], F32, name="acc", tag="acc")
+                for g in range(PASSES):
+                    nc.tensor.matmul_mx(
+                        out=acc[:],
+                        lhsT=m_codes[:, g * P : (g + 1) * P].bitcast(FP8X4),
+                        lhsT_scale=m_scales[:, g * P : (g + 1) * P],
+                        rhs=wo_codes[:, g, cols].bitcast(FP8X4),
+                        rhs_scale=wo_scales[:, g, cols],
+                        start=(g == 0),
+                        stop=(g == PASSES - 1),
+                    )
+                acc_tiles[("out", block, half)] = acc
+
+        def store(block):
+            b, q = divmod(block, QT)
+            result = out_pool.tile([P, E], F32, name="result")
+            for half in range(E // N_TILE):
+                cols = slice(half * N_TILE, (half + 1) * N_TILE)
+                nc.vector.tensor_tensor(
+                    out=result[:, cols], in0=acc_tiles[("out", block, half)][:], in1=bias_rows[:, cols], op=ALU.add
+                )
+            nc.sync.dma_start(out=out[b, q * P : (q + 1) * P, :], in_=result[:])
+
+        load_unit(0)
+        load_unit(1)
+        load_band(0)
 
         ident = keep.tile([P, P], F32)
         make_identity(nc, ident[:])
 
-        edge_mask = keep.tile([P, QT, 2, NREL], F32)
+        edge_mask = keep.tile([P, QT, NREL], F32)
         nc.gpsimd.memset(edge_mask[:], 0.0)
         nc.gpsimd.affine_select(
-            out=edge_mask[:], in_=edge_mask[:], pattern=[[P, QT], [0, 2], [1, NREL]],
+            out=edge_mask[:], in_=edge_mask[:], pattern=[[P, QT], [1, NREL]],
             compare_op=ALU.is_ge, fill=MASKED, base=-WINDOW, channel_multiplier=1,
         )
         nc.gpsimd.affine_select(
-            out=edge_mask[:], in_=edge_mask[:], pattern=[[-P, QT], [0, 2], [-1, NREL]],
+            out=edge_mask[:], in_=edge_mask[:], pattern=[[-P, QT], [-1, NREL]],
             compare_op=ALU.is_ge, fill=MASKED, base=L - 1 + WINDOW, channel_multiplier=-1,
         )
 
@@ -341,58 +389,74 @@ def tile_vitsattention_pa_kernel(tc, logits, v, emb_rel_v, Wo, bo, out):
         nc.gpsimd.memset(band_padded_0[:], 0.0)
         nc.gpsimd.memset(band_padded_1[:], 0.0)
 
-        rel_rows_bf16 = keep.tile([P, N_TILE], BF16)
+        rel_rows_bf16 = keep.tile([P, UNIT * D], BF16)
+        rel_rows = keep.tile([P, UNIT * D], F32)
         nc.vector.memset(rel_rows_bf16[:], 0.0)
-        for tile_of_pair in range(2 * QT):
-            nc.scalar.dma_start(
-                out=rel_rows_bf16[
-                    tile_of_pair * NREL : (tile_of_pair + 1) * NREL, tile_of_pair * D : (tile_of_pair + 1) * D
-                ],
-                in_=emb_rel_v[0],
-            )
-        rel_rows = keep.tile([P, N_TILE], F32)
-        nc.vector.tensor_copy(out=rel_rows[:], in_=rel_rows_bf16[:])
 
         row_max(0)
+        for s in range(UNITS + 3):
+            loaded, maxed, exped, turned, closed = s + 2, s + 1, s, s - 1, s - 2
+            block = (s - 4) // 2 if s % 2 == 0 and s >= 4 else None
 
-        for s in range(PAIRS + 2):
-            if s + 2 < PAIRS:
-                load_pair(s + 2)
-            if s % 4 == 0 and s // 4 + 1 < NH // V_CHUNK:
-                load_v(s // 4 + 1)
-            if s < E // K_PASS:
+            if s < NH // UNIT:
+                load_v(s)
+            if s < PASSES:
                 load_wo(s)
-            if s == E // K_PASS:
+            if s == PASSES:
                 nc.sync.dma_start(out=bias_rows[:], in_=bo.partition_broadcast(P))
+            if loaded < UNITS:
+                load_unit(loaded)
+            if s + 1 < QT:
+                load_band(s + 1)
+            if s == 0:
+                for head in range(UNIT):
+                    nc.sync.dma_start(
+                        out=rel_rows_bf16[head * NREL : (head + 1) * NREL, head * D : (head + 1) * D],
+                        in_=emb_rel_v[0],
+                    )
 
-            if 0 <= s - 1 < PAIRS:
-                normalise_band(s - 1)
-                transpose_words(("e", 2 * s - 2), e_tiles[2 * s - 2][:].bitcast(F32), 0)
-                transpose_words(("e", 2 * s - 1), e_tiles[2 * s - 1][:].bitcast(F32), 0)
-                transpose_band(s - 1)
-            if s < PAIRS:
-                shift_band(s)
-            if 0 <= s - 2 < PAIRS:
-                quantise_rows(("e", 2 * s - 4))
-                quantise_rows(("e", 2 * s - 3))
-                relative(s - 2)
-                context(s - 2)
-            for hh in range(2):
-                if s < PAIRS:
-                    exponentials(2 * s + hh)
-                if 0 <= s - 1 < PAIRS:
-                    regroup_words(("e", 2 * s - 2 + hh), (nc.scalar.copy, nc.scalar.copy))
-            if s < PAIRS:
-                band_exponentials(s)
-            if s + 1 < PAIRS:
-                row_max(s + 1)
-            if s % 4 == 0 and s // 4 < NH // V_CHUNK:
-                quantise_v(s // 4)
-            if s % 2 == 1 and s // 2 < 2 * E // N_TILE:
-                quantise_wo(s // 2)
-            if 0 <= s - 1 < PAIRS:
-                keep_band(s - 1)
-            if 0 <= s - 2 < PAIRS:
-                attention(s - 2)
-                if (s - 2) % PAIRS_PER_BATCH == PAIRS_PER_BATCH - 1:
-                    project((s - 2) // PAIRS_PER_BATCH)
+            if 0 <= turned < UNITS:
+                invert_sums(turned)
+            if exped < UNITS:
+                shift_band(exped)
+            if 0 <= turned < UNITS:
+                normalise_band(turned)
+                transpose_keys(turned, 0)
+                transpose_keys(turned, 1)
+                transpose_band(turned)
+            if block is not None:
+                regroup_merged(block)
+            if 0 <= closed < UNITS:
+                quantise_keys(closed, 0)
+                quantise_keys(closed, 1)
+            if block is not None:
+                quantise_merged(block)
+                project(block)
+            if 0 <= closed < UNITS:
+                relative(closed)
+                context(closed)
+            if maxed < UNITS:
+                row_max(maxed)
+            for x in range(2):
+                if exped < UNITS:
+                    exponentials(exped, x)
+                if 0 <= turned < UNITS:
+                    regroup_keys(turned, x, (nc.scalar.copy, nc.scalar.copy))
+            if exped < UNITS:
+                band_exponentials(exped)
+            if 0 <= turned < UNITS:
+                keep_band(turned)
+            if block is not None:
+                store(block)
+            if s < 2 * PASSES:
+                quantise_wo(s)
+            if s == 1:
+                nc.vector.tensor_copy(out=rel_rows[:], in_=rel_rows_bf16[:])
+            if s < 2:
+                quantise_v(s)
+            elif 4 <= s < 6:
+                quantise_v(s - 2)
+            if 0 <= closed < UNITS:
+                attention(closed)
+                if closed % 2 == 1:
+                    transpose_merged(closed // 2)

@@ -20,23 +20,15 @@ NREL = 2 * WINDOW + 1
 QT = L // P
 PACK = 4
 K_PASS = P * PACK
-PASSES = E // K_PASS
 N_TILE = 512
-QUAD = 4
-UNIT = 2 * QUAD
-UNITS = NH * QT // UNIT
-BLOCKS = UNITS // 2
+PAIRS = NH // 2
+PAIRS_PER_BATCH = H // 2
 BAND_PITCH = 16
 FOLD_WIDTHS = (L // 2, L // 4, L // 8)
+V_CHUNK = 8
 MASKED = -1.0e30
 
 FLOPS = 2 * NH * L * L * D + 2 * NH * L * NREL * D + 2 * B * L * E * E
-
-
-def place_of_unit(i):
-    block, half = divmod(i, 2)
-    b, q = divmod(block, QT)
-    return b, q, half, b * H + half * UNIT
 
 
 def tile_vitsattention_pa_kernel(tc, logits, v, emb_rel_v, Wo, bo, out):
@@ -46,7 +38,7 @@ def tile_vitsattention_pa_kernel(tc, logits, v, emb_rel_v, Wo, bo, out):
     with ExitStack() as stack:
         keep = stack.enter_context(tc.tile_pool(name="keep", bufs=1))
         logit_pool = stack.enter_context(tc.tile_pool(name="logit_pool", bufs=6))
-        band_pool = stack.enter_context(tc.tile_pool(name="band_pool", bufs=3))
+        band_pool = stack.enter_context(tc.tile_pool(name="band_pool", bufs=4))
         fold_pool = stack.enter_context(tc.tile_pool(name="fold_pool", bufs=2))
         e_pool = stack.enter_context(tc.tile_pool(name="e_pool", bufs=6))
         grouped_pool = stack.enter_context(tc.tile_pool(name="grouped_pool", bufs=6))
@@ -55,81 +47,85 @@ def tile_vitsattention_pa_kernel(tc, logits, v, emb_rel_v, Wo, bo, out):
         attn_pool = stack.enter_context(tc.tile_pool(name="attn_pool", bufs=3))
         out_pool = stack.enter_context(tc.tile_pool(name="out_pool", bufs=3))
         psum_words = stack.enter_context(tc.psum_pool(name="psum_words", bufs=4))
-        psum_acc = stack.enter_context(tc.psum_pool(name="psum_acc", bufs=4))
+        psum_band = stack.enter_context(tc.psum_pool(name="psum_band", bufs=1))
+        psum_acc = stack.enter_context(tc.psum_pool(name="psum_acc", bufs=3))
 
-        neg_max = keep.tile([P, UNITS, UNIT], F32)
-        row_sum = keep.tile([P, UNITS, UNIT], F32)
-        inv_sum = keep.tile([P, UNITS, UNIT], F32)
-        band_logits = keep.tile([P, QT, NH, BAND_PITCH], BF16)
-        v_raw = keep.tile([P, NH, PACK, D], BF16)
+        neg_max = keep.tile([P, PAIRS, QT, 2], F32)
+        row_sum = keep.tile([P, PAIRS, QT, 2], F32)
+        inv_sum = keep.tile([P, PAIRS, QT, 2], F32)
+        merged = keep.tile([P, B, QT, E], BF16)
         v_codes = keep.tile([P, NH * D], U32, align_bytes=64)
         v_scales = keep.tile([P, NH * D], U8, align_bytes=64)
-        wo_raw = keep.tile([P, PASSES, PACK, E], BF16)
-        wo_codes = keep.tile([P, PASSES, E], U32, align_bytes=64)
-        wo_scales = keep.tile([P, PASSES, E], U8, align_bytes=64)
+        wo_raw = keep.tile([P, E // K_PASS, PACK, E], BF16)
+        wo_codes = keep.tile([P, E // K_PASS, E], U32, align_bytes=64)
+        wo_scales = keep.tile([P, E // K_PASS, E], U8, align_bytes=64)
         bias_rows = keep.tile([P, E], BF16)
 
         logit_tiles = {}
+        band_logit_tiles = {}
         shifted_tiles = {}
         band_e_tiles = {}
-        band_bank_tiles = {}
         band_t_tiles = {}
+        band_bank_tiles = {}
         e_tiles = {}
         word_banks = {}
         grouped_tiles = {}
         code_tiles = {}
+        v_raw_tiles = {}
         acc_tiles = {}
-        merged_tiles = {}
 
-        def band_windows(first_head, heads, t0, rows):
-            start = first_head * L * L + t0 * (L + 1) - WINDOW
-            if heads == 1:
-                by_head = flat_logits[start : start + rows * (L + 1)].unsqueeze(0)
+        def band_windows(n, t0, rows):
+            start = n * L * L + t0 * (L + 1) - WINDOW
+            run = flat_logits[start : start + rows * (L + 1)]
+            return run.rearrange("(t s) -> t s", s=L + 1)[:, 0:NREL]
+
+        def load_band(band_logits, n, hh):
+            if n == 0:
+                nc.sync.dma_start(
+                    out=band_logits[:, 1:QT, hh, 0:NREL],
+                    in_=band_windows(n, P, L - P).rearrange("(q p) j -> p q j", p=P),
+                )
+                nc.sync.dma_start(out=band_logits[1:P, 0, hh, 0:NREL], in_=band_windows(n, 1, P - 1))
+                nc.sync.dma_start(
+                    out=band_logits[0:1, 0, hh, WINDOW:NREL], in_=flat_logits[0 : WINDOW + 1].unsqueeze(0)
+                )
+            elif n == NH - 1:
+                nc.sync.dma_start(
+                    out=band_logits[:, 0 : QT - 1, hh, 0:NREL],
+                    in_=band_windows(n, 0, L - P).rearrange("(q p) j -> p q j", p=P),
+                )
+                nc.sync.dma_start(
+                    out=band_logits[0 : P - 1, QT - 1, hh, 0:NREL], in_=band_windows(n, L - P, P - 1)
+                )
+                nc.sync.dma_start(
+                    out=band_logits[P - 1 : P, QT - 1, hh, 0 : WINDOW + 1],
+                    in_=flat_logits[NH * L * L - (WINDOW + 1) : NH * L * L].unsqueeze(0),
+                )
             else:
-                whole_heads = flat_logits[start : start + heads * L * L].rearrange("(n r) -> n r", n=heads)
-                by_head = whole_heads[:, 0 : rows * (L + 1)]
-            return by_head.rearrange("n (t s) -> t n s", s=L + 1)[:, :, 0:NREL]
+                nc.sync.dma_start(
+                    out=band_logits[:, :, hh, 0:NREL],
+                    in_=band_windows(n, 0, L).rearrange("(q p) j -> p q j", p=P),
+                )
 
-        def load_band(q):
-            if q == 0:
-                nc.sync.dma_start(out=band_logits[:, q, 1:NH, 0:NREL], in_=band_windows(1, NH - 1, 0, P))
-                nc.gpsimd.memset(band_logits[:, q, 0, :], 0.0)
-                nc.sync.dma_start(out=band_logits[1:P, q, 0:1, 0:NREL], in_=band_windows(0, 1, 1, P - 1))
-                nc.sync.dma_start(
-                    out=band_logits[0:1, q, 0, WINDOW:NREL], in_=flat_logits[0 : WINDOW + 1].unsqueeze(0)
-                )
-                return
-            nc.sync.dma_start(out=band_logits[:, q, 0 : NH - 1, 0:NREL], in_=band_windows(0, NH - 1, q * P, P))
-            if q < QT - 1:
-                nc.sync.dma_start(
-                    out=band_logits[:, q, NH - 1 : NH, 0:NREL], in_=band_windows(NH - 1, 1, q * P, P)
-                )
-                return
-            nc.gpsimd.memset(band_logits[:, q, NH - 1, :], 0.0)
-            nc.sync.dma_start(
-                out=band_logits[0 : P - 1, q, NH - 1 : NH, 0:NREL], in_=band_windows(NH - 1, 1, q * P, P - 1)
-            )
-            nc.sync.dma_start(
-                out=band_logits[P - 1 : P, q, NH - 1, 0 : WINDOW + 1],
-                in_=flat_logits[NH * L * L - (WINDOW + 1) : NH * L * L].unsqueeze(0),
-            )
-
-        def load_unit(i):
-            b, q, half, first_head = place_of_unit(i)
-            for x in range(2):
-                n = first_head + x * QUAD
-                a = logit_pool.tile([P, QUAD, L], BF16, name="a")
-                nc.sync.dma_start(
-                    out=a[:], in_=logits[n : n + QUAD, q * P : (q + 1) * P, :].rearrange("n p k -> p n k")
-                )
-                logit_tiles[(i, x)] = a
+        def load_pair(i):
+            band_logits = band_pool.tile([P, QT, 2, BAND_PITCH], BF16, name="band_logits")
+            if i == 0 or i == PAIRS - 1:
+                nc.gpsimd.memset(band_logits[:], 0.0)
+            for hh in range(2):
+                n = 2 * i + hh
+                a = logit_pool.tile([P, QT, L], BF16, name="a")
+                nc.sync.dma_start(out=a[:], in_=logits[n].rearrange("(q p) k -> p q k", p=P))
+                logit_tiles[n] = a
+                load_band(band_logits, n, hh)
+            band_logit_tiles[i] = band_logits
 
         def load_v(c):
-            heads = slice(c * UNIT, (c + 1) * UNIT)
+            v_raw = weight_pool.tile([P, V_CHUNK, PACK, D], BF16, name="v_raw")
             nc.sync.dma_start(
-                out=v_raw[:, heads].rearrange("p n (u c) d -> p n u (c d)", u=2),
-                in_=v[heads].rearrange("n (u p c) d -> p n u (c d)", u=2, p=P, c=2),
+                out=v_raw[:].rearrange("p n (u c) d -> p n u (c d)", u=2),
+                in_=v[c * V_CHUNK : (c + 1) * V_CHUNK].rearrange("n (u p c) d -> p n u (c d)", u=2, p=P, c=2),
             )
+            v_raw_tiles[c] = v_raw
 
         def load_wo(g):
             nc.sync.dma_start(
@@ -138,10 +134,9 @@ def tile_vitsattention_pa_kernel(tc, logits, v, emb_rel_v, Wo, bo, out):
             )
 
         def quantise_v(c):
-            heads = slice(c * UNIT, (c + 1) * UNIT)
-            cols = slice(c * UNIT * D, (c + 1) * UNIT * D)
-            v_grouped = weight_pool.tile([P, UNIT, D, PACK], BF16, name="v_grouped", align_bytes=64)
-            nc.vector.tensor_copy(out=v_grouped[:], in_=v_raw[:, heads].rearrange("p n t d -> p n d t"))
+            v_grouped = weight_pool.tile([P, V_CHUNK, D, PACK], BF16, name="v_grouped", align_bytes=64)
+            nc.vector.tensor_copy(out=v_grouped[:], in_=v_raw_tiles[c][:].rearrange("p n t d -> p n d t"))
+            cols = slice(c * V_CHUNK * D, (c + 1) * V_CHUNK * D)
             nc.vector.quantize_mx(
                 out=v_codes[:, cols].bitcast(FP8X4),
                 scales=v_scales[:, cols],
@@ -160,125 +155,113 @@ def tile_vitsattention_pa_kernel(tc, logits, v, emb_rel_v, Wo, bo, out):
             )
 
         def row_max(i):
-            narrowed = {0: logit_tiles[(i, 0)], 1: logit_tiles[(i, 1)]}
+            narrowed = {0: logit_tiles[2 * i], 1: logit_tiles[2 * i + 1]}
             for width in FOLD_WIDTHS:
-                for x in range(2):
-                    folded = fold_pool.tile([P, QUAD, width], BF16, name="folded", tag="folded_%d_%d" % (width, x))
+                for hh in range(2):
+                    folded = fold_pool.tile([P, QT, width], BF16, name="folded", tag="folded_%d_%d" % (width, hh))
                     nc.vector.tensor_tensor(
                         out=folded[:],
-                        in0=narrowed[x][:, :, 0:width],
-                        in1=narrowed[x][:, :, width : 2 * width],
+                        in0=narrowed[hh][:, :, 0:width],
+                        in1=narrowed[hh][:, :, width : 2 * width],
                         op=ALU.max,
                     )
-                    narrowed[x] = folded
-            for x in range(2):
+                    narrowed[hh] = folded
+            for hh in range(2):
                 nc.vector.tensor_reduce(
-                    out=neg_max[:, i, x * QUAD : (x + 1) * QUAD],
-                    in_=narrowed[x][:],
-                    axis=AXIS.X,
-                    op=ALU.max,
-                    negate=True,
+                    out=neg_max[:, i, :, hh], in_=narrowed[hh][:], axis=AXIS.X, op=ALU.max, negate=True
                 )
 
-        def exponentials(i, x):
-            e = e_pool.tile([P, QUAD, L], BF16, name="e")
-            for j in range(QUAD):
-                head = x * QUAD + j
+        def exponentials(n):
+            i, hh = divmod(n, 2)
+            e = e_pool.tile([P, QT, L], BF16, name="e")
+            for q in range(QT):
                 nc.scalar.activation(
-                    out=e[:, j, :],
-                    in_=logit_tiles[(i, x)][:, j, :],
+                    out=e[:, q, :],
+                    in_=logit_tiles[n][:, q, :],
                     func=ACT.Exp,
-                    bias=neg_max[:, i, head : head + 1],
+                    bias=neg_max[:, i, q, hh : hh + 1],
                     scale=1.0,
-                    accum_out=row_sum[:, i, head : head + 1],
+                    accum_out=row_sum[:, i, q, hh : hh + 1],
                 )
-            e_tiles[(i, x)] = e
+            e_tiles[n] = e
 
-        def transpose_keys(i, x):
-            words = e_tiles[(i, x)][:].bitcast(F32)
+        def transpose_words(key, words, first_word):
             for half in range(2):
                 bank = psum_words.tile([P, 2, 2 * P], F32, name="bank")
                 for u in range(2):
                     for r in range(2):
                         nc.tensor.transpose(
-                            bank[:, u, r * P : (r + 1) * P], words[:, 2 * half + r, u * P : (u + 1) * P], ident[:]
+                            bank[:, u, r * P : (r + 1) * P],
+                            words[:, 2 * half + r, first_word + u * P : first_word + (u + 1) * P],
+                            ident[:],
                         )
-                word_banks[(i, x, half)] = bank
+                word_banks[(key, half)] = bank
 
-        def regroup_keys(i, x, copies):
-            grouped = grouped_pool.tile([P, QUAD * P, PACK], BF16, name="grouped", align_bytes=64)
+        def regroup_words(key, copies):
+            grouped = grouped_pool.tile([P, L, PACK], BF16, name="grouped", align_bytes=64)
             grouped_words = grouped[:].bitcast(F32)
             for half in range(2):
-                copies[half](
-                    out=grouped_words[:, half * 2 * P : (half + 1) * 2 * P, :],
-                    in_=word_banks[(i, x, half)][:].rearrange("p u r -> p r u"),
-                )
-            grouped_tiles[(i, x)] = grouped
+                source = word_banks[(key, half)][:].rearrange("p u r -> p r u")
+                target = grouped_words[:, half * 2 * P : (half + 1) * 2 * P, :]
+                copies[half](out=target, in_=source)
+            grouped_tiles[key] = grouped
 
-        def quantise_keys(i, x):
-            codes = code_pool.tile([P, QUAD * P], U32, name="codes", align_bytes=64)
-            scales = code_pool.tile([P, QUAD * P], U8, name="scales", align_bytes=64)
+        def quantise_rows(key):
+            codes = code_pool.tile([P, L], U32, name="codes", align_bytes=64)
+            scales = code_pool.tile([P, L], U8, name="scales", align_bytes=64)
             nc.vector.quantize_mx(
                 out=codes[:].bitcast(FP8X4),
                 scales=scales[:],
-                in_=grouped_tiles[(i, x)][:].rearrange("p r t -> p (r t)"),
+                in_=grouped_tiles[key][:].rearrange("p r t -> p (r t)"),
             )
-            code_tiles[(i, x)] = (codes, scales)
+            code_tiles[key] = (codes, scales)
 
         def context(i):
-            first_head = place_of_unit(i)[3]
-            ctx = psum_acc.tile([P, UNIT * D], F32, name="ctx", tag="acc")
-            for head in range(UNIT):
-                x, j = divmod(head, QUAD)
-                n = first_head + head
-                codes, scales = code_tiles[(i, x)]
-                nc.tensor.matmul_mx(
-                    out=ctx[:, head * D : (head + 1) * D],
-                    lhsT=codes[:, j * P : (j + 1) * P].bitcast(FP8X4),
-                    lhsT_scale=scales[:, j * P : (j + 1) * P],
-                    rhs=v_codes[:, n * D : (n + 1) * D].bitcast(FP8X4),
-                    rhs_scale=v_scales[:, n * D : (n + 1) * D],
-                    start=True,
-                    stop=True,
-                )
+            ctx = psum_acc.tile([P, N_TILE], F32, name="ctx", tag="acc")
+            ctx_view = ctx[:].rearrange("p (q h d) -> p q h d", q=QT, h=2)
+            for hh in range(2):
+                n = 2 * i + hh
+                codes, scales = code_tiles[("e", n)]
+                for q in range(QT):
+                    nc.tensor.matmul_mx(
+                        out=ctx_view[:, q, hh, :],
+                        lhsT=codes[:, q * P : (q + 1) * P].bitcast(FP8X4),
+                        lhsT_scale=scales[:, q * P : (q + 1) * P],
+                        rhs=v_codes[:, n * D : (n + 1) * D].bitcast(FP8X4),
+                        rhs_scale=v_scales[:, n * D : (n + 1) * D],
+                        start=True,
+                        stop=True,
+                    )
             acc_tiles[("ctx", i)] = ctx
 
         def shift_band(i):
-            b, q, half, first_head = place_of_unit(i)
-            shifted = band_pool.tile([P, UNIT, NREL], F32, name="shifted")
+            shifted = band_pool.tile([P, QT, 2, NREL], F32, name="shifted")
             nc.gpsimd.tensor_tensor(
                 out=shifted[:],
-                in0=band_logits[:, q, first_head : first_head + UNIT, 0:NREL],
-                in1=neg_max[:, i].unsqueeze(2).to_broadcast([P, UNIT, NREL]),
+                in0=band_logit_tiles[i][:, :, :, 0:NREL],
+                in1=neg_max[:, i].unsqueeze(3).to_broadcast([P, QT, 2, NREL]),
                 op=ALU.add,
             )
-            if q == 0 or q == QT - 1:
-                nc.gpsimd.tensor_tensor(
-                    out=shifted[:],
-                    in0=shifted[:],
-                    in1=edge_mask[:, q].unsqueeze(1).to_broadcast([P, UNIT, NREL]),
-                    op=ALU.add,
-                )
+            nc.gpsimd.tensor_tensor(out=shifted[:], in0=shifted[:], in1=edge_mask[:], op=ALU.add)
             shifted_tiles[i] = shifted
 
         def band_exponentials(i):
-            band_e = band_pool.tile([P, UNIT, NREL], F32, name="band_e")
+            band_e = band_pool.tile([P, QT, 2, NREL], F32, name="band_e")
             nc.scalar.activation(out=band_e[:], in_=shifted_tiles[i][:], func=ACT.Exp)
             band_e_tiles[i] = band_e
 
-        def invert_sums(i):
-            nc.vector.reciprocal(out=inv_sum[:, i], in_=row_sum[:, i])
-
         def normalise_band(i):
+            nc.vector.reciprocal(out=inv_sum[:, i], in_=row_sum[:, i])
+            padded = band_padded[i % 2]
             nc.gpsimd.tensor_tensor(
-                out=band_padded[i % 2][:, 0 : UNIT * NREL].rearrange("p (h j) -> p h j", h=UNIT),
+                out=padded[:, 0 : 2 * QT * NREL].rearrange("p (q h j) -> p q h j", q=QT, h=2),
                 in0=band_e_tiles[i][:],
-                in1=inv_sum[:, i].unsqueeze(2).to_broadcast([P, UNIT, NREL]),
+                in1=inv_sum[:, i].unsqueeze(3).to_broadcast([P, QT, 2, NREL]),
                 op=ALU.mult,
             )
 
         def transpose_band(i):
-            band_bank = psum_acc.tile([P, P], F32, name="band_bank", tag="acc")
+            band_bank = psum_band.tile([P, P], F32, name="band_bank")
             nc.tensor.transpose(band_bank[:], band_padded[i % 2][:], ident[:])
             band_bank_tiles[i] = band_bank
 
@@ -288,98 +271,67 @@ def tile_vitsattention_pa_kernel(tc, logits, v, emb_rel_v, Wo, bo, out):
             band_t_tiles[i] = band_t
 
         def relative(i):
-            rel = psum_acc.tile([P, UNIT * D], F32, name="rel", tag="acc")
+            rel = psum_acc.tile([P, N_TILE], F32, name="rel", tag="acc")
             nc.tensor.matmul(out=rel[:], lhsT=band_t_tiles[i][:], rhs=rel_rows[:], start=True, stop=True)
             acc_tiles[("rel", i)] = rel
 
         def attention(i):
-            block, half = divmod(i, 2)
-            if half == 0:
-                merged = attn_pool.tile([P, E], BF16, name="merged")
-                merged_tiles[block] = merged
-            scaled = attn_pool.tile([P, UNIT * D], F32, name="scaled")
+            b, pair_in_batch = divmod(i, PAIRS_PER_BATCH)
+            scaled = attn_pool.tile([P, N_TILE], F32, name="scaled")
             nc.vector.tensor_tensor(
-                out=scaled[:].rearrange("p (h d) -> p h d", h=UNIT),
-                in0=acc_tiles[("ctx", i)][:].rearrange("p (h d) -> p h d", h=UNIT),
-                in1=inv_sum[:, i].unsqueeze(2).to_broadcast([P, UNIT, D]),
+                out=scaled[:].rearrange("p (q h d) -> p q h d", q=QT, h=2),
+                in0=acc_tiles[("ctx", i)][:].rearrange("p (q h d) -> p q h d", q=QT, h=2),
+                in1=inv_sum[:, i].unsqueeze(3).to_broadcast([P, QT, 2, D]),
                 op=ALU.mult,
             )
             nc.vector.tensor_tensor(
-                out=merged_tiles[block][:, half * UNIT * D : (half + 1) * UNIT * D],
-                in0=scaled[:],
-                in1=acc_tiles[("rel", i)][:],
+                out=merged[:, b, :, pair_in_batch * 2 * D : (pair_in_batch + 1) * 2 * D],
+                in0=scaled[:].rearrange("p (q c) -> p q c", q=QT),
+                in1=acc_tiles[("rel", i)][:].rearrange("p (q c) -> p q c", q=QT),
                 op=ALU.add,
             )
 
-        def transpose_merged(block):
-            words = merged_tiles[block][:].bitcast(F32)
-            bank = psum_words.tile([P, PASSES, 2 * P], F32, name="bank")
-            for g in range(PASSES):
-                for u in range(2):
-                    nc.tensor.transpose(
-                        bank[:, g, u * P : (u + 1) * P], words[:, (2 * g + u) * P : (2 * g + u + 1) * P], ident[:]
-                    )
-            word_banks[block] = bank
+        def project(b):
+            merged_words = merged[:, b].bitcast(F32)
+            for g in range(E // K_PASS):
+                transpose_words(("m", g), merged_words, g * K_PASS // 2)
+                regroup_words(("m", g), (nc.scalar.copy, nc.vector.tensor_copy))
+            for g in range(E // K_PASS):
+                quantise_rows(("m", g))
+            for q in range(QT):
+                result = out_pool.tile([P, E], F32, name="result")
+                for half in range(E // N_TILE):
+                    cols = slice(half * N_TILE, (half + 1) * N_TILE)
+                    acc = psum_acc.tile([P, N_TILE], F32, name="acc", tag="acc")
+                    for g in range(E // K_PASS):
+                        codes, scales = code_tiles[("m", g)]
+                        nc.tensor.matmul_mx(
+                            out=acc[:],
+                            lhsT=codes[:, q * P : (q + 1) * P].bitcast(FP8X4),
+                            lhsT_scale=scales[:, q * P : (q + 1) * P],
+                            rhs=wo_codes[:, g, cols].bitcast(FP8X4),
+                            rhs_scale=wo_scales[:, g, cols],
+                            start=(g == 0),
+                            stop=(g == E // K_PASS - 1),
+                        )
+                    nc.vector.tensor_tensor(out=result[:, cols], in0=acc[:], in1=bias_rows[:, cols], op=ALU.add)
+                nc.sync.dma_start(out=out[b, q * P : (q + 1) * P, :], in_=result[:])
 
-        def regroup_merged(block):
-            m_grouped = grouped_pool.tile([P, PASSES, P, PACK], BF16, name="m_grouped", align_bytes=64)
-            nc.vector.tensor_copy(
-                out=m_grouped[:].bitcast(F32), in_=word_banks[block][:].rearrange("p g (u r) -> p g r u", u=2)
-            )
-            grouped_tiles[block] = m_grouped
-
-        def quantise_merged(block):
-            m_codes = code_pool.tile([P, PASSES * P], U32, name="m_codes", align_bytes=64)
-            m_scales = code_pool.tile([P, PASSES * P], U8, name="m_scales", align_bytes=64)
-            nc.vector.quantize_mx(
-                out=m_codes[:].bitcast(FP8X4),
-                scales=m_scales[:],
-                in_=grouped_tiles[block][:].rearrange("p g r t -> p (g r t)"),
-            )
-            code_tiles[block] = (m_codes, m_scales)
-
-        def project(block):
-            m_codes, m_scales = code_tiles[block]
-            for half in range(E // N_TILE):
-                cols = slice(half * N_TILE, (half + 1) * N_TILE)
-                acc = psum_acc.tile([P, N_TILE], F32, name="acc", tag="acc")
-                for g in range(PASSES):
-                    nc.tensor.matmul_mx(
-                        out=acc[:],
-                        lhsT=m_codes[:, g * P : (g + 1) * P].bitcast(FP8X4),
-                        lhsT_scale=m_scales[:, g * P : (g + 1) * P],
-                        rhs=wo_codes[:, g, cols].bitcast(FP8X4),
-                        rhs_scale=wo_scales[:, g, cols],
-                        start=(g == 0),
-                        stop=(g == PASSES - 1),
-                    )
-                acc_tiles[("out", block, half)] = acc
-
-        def store(block):
-            b, q = divmod(block, QT)
-            result = out_pool.tile([P, E], F32, name="result")
-            for half in range(E // N_TILE):
-                cols = slice(half * N_TILE, (half + 1) * N_TILE)
-                nc.vector.tensor_tensor(
-                    out=result[:, cols], in0=acc_tiles[("out", block, half)][:], in1=bias_rows[:, cols], op=ALU.add
-                )
-            nc.sync.dma_start(out=out[b, q * P : (q + 1) * P, :], in_=result[:])
-
-        load_unit(0)
-        load_unit(1)
-        load_band(0)
+        load_pair(0)
+        load_v(0)
+        load_pair(1)
 
         ident = keep.tile([P, P], F32)
         make_identity(nc, ident[:])
 
-        edge_mask = keep.tile([P, QT, NREL], F32)
+        edge_mask = keep.tile([P, QT, 2, NREL], F32)
         nc.gpsimd.memset(edge_mask[:], 0.0)
         nc.gpsimd.affine_select(
-            out=edge_mask[:], in_=edge_mask[:], pattern=[[P, QT], [1, NREL]],
+            out=edge_mask[:], in_=edge_mask[:], pattern=[[P, QT], [0, 2], [1, NREL]],
             compare_op=ALU.is_ge, fill=MASKED, base=-WINDOW, channel_multiplier=1,
         )
         nc.gpsimd.affine_select(
-            out=edge_mask[:], in_=edge_mask[:], pattern=[[-P, QT], [-1, NREL]],
+            out=edge_mask[:], in_=edge_mask[:], pattern=[[-P, QT], [0, 2], [-1, NREL]],
             compare_op=ALU.is_ge, fill=MASKED, base=L - 1 + WINDOW, channel_multiplier=-1,
         )
 
@@ -389,74 +341,59 @@ def tile_vitsattention_pa_kernel(tc, logits, v, emb_rel_v, Wo, bo, out):
         nc.gpsimd.memset(band_padded_0[:], 0.0)
         nc.gpsimd.memset(band_padded_1[:], 0.0)
 
-        rel_rows_bf16 = keep.tile([P, UNIT * D], BF16)
-        rel_rows = keep.tile([P, UNIT * D], F32)
+        rel_rows_bf16 = keep.tile([P, N_TILE], BF16)
         nc.vector.memset(rel_rows_bf16[:], 0.0)
+        for tile_of_pair in range(2 * QT):
+            nc.scalar.dma_start(
+                out=rel_rows_bf16[
+                    tile_of_pair * NREL : (tile_of_pair + 1) * NREL, tile_of_pair * D : (tile_of_pair + 1) * D
+                ],
+                in_=emb_rel_v[0],
+            )
+        rel_rows = keep.tile([P, N_TILE], F32)
+        nc.vector.tensor_copy(out=rel_rows[:], in_=rel_rows_bf16[:])
 
         row_max(0)
-        for s in range(UNITS + 3):
-            loaded, maxed, exped, turned, closed = s + 2, s + 1, s, s - 1, s - 2
-            block = (s - 4) // 2 if s % 2 == 0 and s >= 4 else None
 
-            if s < NH // UNIT:
-                load_v(s)
-            if s < PASSES:
+        for s in range(PAIRS + 2):
+            if s + 2 < PAIRS:
+                load_pair(s + 2)
+            if s % 4 == 0 and s // 4 + 1 < NH // V_CHUNK:
+                load_v(s // 4 + 1)
+            if s < E // K_PASS:
                 load_wo(s)
-            if s == PASSES:
+            if s == E // K_PASS:
                 nc.sync.dma_start(out=bias_rows[:], in_=bo.partition_broadcast(P))
-            if loaded < UNITS:
-                load_unit(loaded)
-            if s + 1 < QT:
-                load_band(s + 1)
-            if s == 0:
-                for head in range(UNIT):
-                    nc.sync.dma_start(
-                        out=rel_rows_bf16[head * NREL : (head + 1) * NREL, head * D : (head + 1) * D],
-                        in_=emb_rel_v[0],
-                    )
 
-            if 0 <= turned < UNITS:
-                invert_sums(turned)
-            if exped < UNITS:
-                shift_band(exped)
-            if 0 <= turned < UNITS:
-                normalise_band(turned)
-                transpose_keys(turned, 0)
-                transpose_keys(turned, 1)
-                transpose_band(turned)
-            if block is not None:
-                regroup_merged(block)
-            if 0 <= closed < UNITS:
-                quantise_keys(closed, 0)
-                quantise_keys(closed, 1)
-            if block is not None:
-                quantise_merged(block)
-                project(block)
-            if 0 <= closed < UNITS:
-                relative(closed)
-                context(closed)
-            if maxed < UNITS:
-                row_max(maxed)
-            for x in range(2):
-                if exped < UNITS:
-                    exponentials(exped, x)
-                if 0 <= turned < UNITS:
-                    regroup_keys(turned, x, (nc.scalar.copy, nc.scalar.copy))
-            if exped < UNITS:
-                band_exponentials(exped)
-            if 0 <= turned < UNITS:
-                keep_band(turned)
-            if block is not None:
-                store(block)
-            if s < 2 * PASSES:
-                quantise_wo(s)
-            if s == 1:
-                nc.vector.tensor_copy(out=rel_rows[:], in_=rel_rows_bf16[:])
-            if s < 2:
-                quantise_v(s)
-            elif 4 <= s < 6:
-                quantise_v(s - 2)
-            if 0 <= closed < UNITS:
-                attention(closed)
-                if closed % 2 == 1:
-                    transpose_merged(closed // 2)
+            if 0 <= s - 1 < PAIRS:
+                normalise_band(s - 1)
+                transpose_words(("e", 2 * s - 2), e_tiles[2 * s - 2][:].bitcast(F32), 0)
+                transpose_words(("e", 2 * s - 1), e_tiles[2 * s - 1][:].bitcast(F32), 0)
+                transpose_band(s - 1)
+            if s < PAIRS:
+                shift_band(s)
+            if 0 <= s - 2 < PAIRS:
+                quantise_rows(("e", 2 * s - 4))
+                quantise_rows(("e", 2 * s - 3))
+                relative(s - 2)
+                context(s - 2)
+            for hh in range(2):
+                if s < PAIRS:
+                    exponentials(2 * s + hh)
+                if 0 <= s - 1 < PAIRS:
+                    last_copy = nc.vector.tensor_copy if hh == 1 else nc.scalar.copy
+                    regroup_words(("e", 2 * s - 2 + hh), (nc.scalar.copy, last_copy))
+            if s < PAIRS:
+                band_exponentials(s)
+            if s + 1 < PAIRS:
+                row_max(s + 1)
+            if s % 4 == 0 and s // 4 < NH // V_CHUNK:
+                quantise_v(s // 4)
+            if s % 2 == 1 and s // 2 < 2 * E // N_TILE:
+                quantise_wo(s // 2)
+            if 0 <= s - 1 < PAIRS:
+                keep_band(s - 1)
+            if 0 <= s - 2 < PAIRS:
+                attention(s - 2)
+                if (s - 2) % PAIRS_PER_BATCH == PAIRS_PER_BATCH - 1:
+                    project((s - 2) // PAIRS_PER_BATCH)

@@ -381,8 +381,7 @@ def tile_vitsattention_pa_kernel(tc, logits, v, emb_rel_v, Wo, bo, out):
                 if s < PAIRS:
                     exponentials(2 * s + hh)
                 if 0 <= s - 1 < PAIRS:
-                    last_copy = nc.vector.tensor_copy if hh == 1 else nc.scalar.copy
-                    regroup_words(("e", 2 * s - 2 + hh), (nc.scalar.copy, last_copy))
+                    regroup_words(("e", 2 * s - 2 + hh), (nc.scalar.copy, nc.vector.tensor_copy))
             if s < PAIRS:
                 band_exponentials(s)
             if s + 1 < PAIRS:

@@ -26,6 +26,7 @@ PAIRS_PER_BATCH = H // 2
 BAND_PITCH = 16
 FOLD_WIDTHS = (L // 2, L // 4, L // 8)
 V_CHUNK = 8
+RUN = 4
 MASKED = -1.0e30
 
 FLOPS = 2 * NH * L * L * D + 2 * NH * L * NREL * D + 2 * B * L * E * E
@@ -72,6 +73,8 @@ def tile_vitsattention_pa_kernel(tc, logits, v, emb_rel_v, Wo, bo, out):
         grouped_tiles = {}
         code_tiles = {}
         v_raw_tiles = {}
+        v_grouped_tiles = {}
+        wo_grouped_tiles = {}
         acc_tiles = {}
 
         def band_windows(n, t0, rows):
@@ -133,31 +136,45 @@ def tile_vitsattention_pa_kernel(tc, logits, v, emb_rel_v, Wo, bo, out):
                 in_=Wo[g * K_PASS : (g + 1) * K_PASS, :].rearrange("(u p c) o -> p u (c o)", u=2, p=P, c=2),
             )
 
-        def quantise_v(c):
+        def regroup_v(c):
             v_grouped = weight_pool.tile([P, V_CHUNK, D, PACK], BF16, name="v_grouped", align_bytes=64)
-            nc.vector.tensor_copy(out=v_grouped[:], in_=v_raw_tiles[c][:].rearrange("p n t d -> p n d t"))
+            nc.vector.tensor_copy(
+                out=v_grouped[:].rearrange("p n (c i) t -> p n c t i", i=RUN),
+                in_=v_raw_tiles[c][:].rearrange("p n t (c i) -> p n c t i", i=RUN),
+            )
+            v_grouped_tiles[c] = v_grouped
+
+        def quantise_v(c):
             cols = slice(c * V_CHUNK * D, (c + 1) * V_CHUNK * D)
             nc.vector.quantize_mx(
                 out=v_codes[:, cols].bitcast(FP8X4),
                 scales=v_scales[:, cols],
-                in_=v_grouped[:].rearrange("p n d t -> p (n d t)"),
+                in_=v_grouped_tiles[c][:].rearrange("p n d t -> p (n d t)"),
             )
+
+        def regroup_wo(w):
+            g, half = divmod(w, E // N_TILE)
+            cols = slice(half * N_TILE, (half + 1) * N_TILE)
+            wo_grouped = weight_pool.tile([P, N_TILE, PACK], BF16, name="wo_grouped", align_bytes=64)
+            nc.vector.tensor_copy(
+                out=wo_grouped[:].rearrange("p (c i) t -> p c t i", i=RUN),
+                in_=wo_raw[:, g, :, cols].rearrange("p t (c i) -> p c t i", i=RUN),
+            )
+            wo_grouped_tiles[w] = wo_grouped
 
         def quantise_wo(w):
             g, half = divmod(w, E // N_TILE)
             cols = slice(half * N_TILE, (half + 1) * N_TILE)
-            wo_grouped = weight_pool.tile([P, N_TILE, PACK], BF16, name="wo_grouped", align_bytes=64)
-            nc.vector.tensor_copy(out=wo_grouped[:], in_=wo_raw[:, g, :, cols].rearrange("p t o -> p o t"))
             nc.vector.quantize_mx(
                 out=wo_codes[:, g, cols].bitcast(FP8X4),
                 scales=wo_scales[:, g, cols],
-                in_=wo_grouped[:].rearrange("p o t -> p (o t)"),
+                in_=wo_grouped_tiles[w][:].rearrange("p o t -> p (o t)"),
             )
 
-        def row_max(i):
+        def row_max(i, heads):
             narrowed = {0: logit_tiles[2 * i], 1: logit_tiles[2 * i + 1]}
             for width in FOLD_WIDTHS:
-                for hh in range(2):
+                for hh in heads:
                     folded = fold_pool.tile([P, QT, width], BF16, name="folded", tag="folded_%d_%d" % (width, hh))
                     nc.vector.tensor_tensor(
                         out=folded[:],
@@ -166,7 +183,7 @@ def tile_vitsattention_pa_kernel(tc, logits, v, emb_rel_v, Wo, bo, out):
                         op=ALU.max,
                     )
                     narrowed[hh] = folded
-            for hh in range(2):
+            for hh in heads:
                 nc.vector.tensor_reduce(
                     out=neg_max[:, i, :, hh], in_=narrowed[hh][:], axis=AXIS.X, op=ALU.max, negate=True
                 )
@@ -353,7 +370,8 @@ def tile_vitsattention_pa_kernel(tc, logits, v, emb_rel_v, Wo, bo, out):
         rel_rows = keep.tile([P, N_TILE], F32)
         nc.vector.tensor_copy(out=rel_rows[:], in_=rel_rows_bf16[:])
 
-        row_max(0)
+        row_max(0, (0,))
+        row_max(0, (1,))
 
         for s in range(PAIRS + 2):
             if s + 2 < PAIRS:
@@ -381,15 +399,21 @@ def tile_vitsattention_pa_kernel(tc, logits, v, emb_rel_v, Wo, bo, out):
                 if s < PAIRS:
                     exponentials(2 * s + hh)
                 if 0 <= s - 1 < PAIRS:
-                    regroup_words(("e", 2 * s - 2 + hh), (nc.scalar.copy, nc.vector.tensor_copy))
+                    to_vector = hh == 1 or s % 2 == 0
+                    second_copy = nc.vector.tensor_copy if to_vector else nc.scalar.copy
+                    regroup_words(("e", 2 * s - 2 + hh), (nc.scalar.copy, second_copy))
             if s < PAIRS:
                 band_exponentials(s)
             if s + 1 < PAIRS:
-                row_max(s + 1)
+                row_max(s + 1, (0, 1))
             if s % 4 == 0 and s // 4 < NH // V_CHUNK:
+                regroup_v(s // 4)
+            if s % 4 == 1 and s // 4 < NH // V_CHUNK:
                 quantise_v(s // 4)
-            if s % 2 == 1 and s // 2 < 2 * E // N_TILE:
-                quantise_wo(s // 2)
+            if s % 2 == 0 and 0 <= s // 2 - 1 < 2 * E // N_TILE:
+                regroup_wo(s // 2 - 1)
+            if s % 2 == 1 and 0 <= s // 2 - 1 < 2 * E // N_TILE:
+                quantise_wo(s // 2 - 1)
             if 0 <= s - 1 < PAIRS:
                 keep_band(s - 1)
             if 0 <= s - 2 < PAIRS:

@@ -20,16 +20,33 @@ NREL = 2 * WINDOW + 1
 QT = L // P
 PACK = 4
 K_PASS = P * PACK
+GROUPS = E // K_PASS
 N_TILE = 512
-PAIRS = NH // 2
+SLOTS = 8
+HALF = SLOTS // 2
+UNITS = NH * QT // SLOTS
+PAIR_UNITS = UNITS - QT
 PAIRS_PER_BATCH = H // 2
+LAST_HEADS = NH - SLOTS
 BAND_PITCH = 16
-FOLD_WIDTHS = (L // 2, L // 4, L // 8)
+FOLD_WIDTHS = (L // 2, L // 4, L // 8, L // 16)
 V_CHUNK = 8
 RUN = 4
+BAND_TERMS = 3
+BAND_ROWS = HALF * BAND_TERMS * NREL
 MASKED = -1.0e30
 
 FLOPS = 2 * NH * L * L * D + 2 * NH * L * NREL * D + 2 * B * L * E * E
+
+
+def is_pair(u):
+    return u < PAIR_UNITS
+
+
+def slots_of(u):
+    if is_pair(u):
+        return [(2 * u + k // QT, k % QT) for k in range(SLOTS)]
+    return [(LAST_HEADS + k, u - PAIR_UNITS) for k in range(SLOTS)]
 
 
 def tile_vitsattention_pa_kernel(tc, logits, v, emb_rel_v, Wo, bo, out):
@@ -38,11 +55,11 @@ def tile_vitsattention_pa_kernel(tc, logits, v, emb_rel_v, Wo, bo, out):
 
     with ExitStack() as stack:
         keep = stack.enter_context(tc.tile_pool(name="keep", bufs=1))
-        logit_pool = stack.enter_context(tc.tile_pool(name="logit_pool", bufs=6))
+        logit_pool = stack.enter_context(tc.tile_pool(name="logit_pool", bufs=4))
         band_pool = stack.enter_context(tc.tile_pool(name="band_pool", bufs=4))
         fold_pool = stack.enter_context(tc.tile_pool(name="fold_pool", bufs=2))
-        e_pool = stack.enter_context(tc.tile_pool(name="e_pool", bufs=6))
-        grouped_pool = stack.enter_context(tc.tile_pool(name="grouped_pool", bufs=6))
+        e_pool = stack.enter_context(tc.tile_pool(name="e_pool", bufs=3))
+        grouped_pool = stack.enter_context(tc.tile_pool(name="grouped_pool", bufs=4))
         code_pool = stack.enter_context(tc.tile_pool(name="code_pool", bufs=4))
         weight_pool = stack.enter_context(tc.tile_pool(name="weight_pool", bufs=2))
         attn_pool = stack.enter_context(tc.tile_pool(name="attn_pool", bufs=3))
@@ -51,15 +68,15 @@ def tile_vitsattention_pa_kernel(tc, logits, v, emb_rel_v, Wo, bo, out):
         psum_band = stack.enter_context(tc.psum_pool(name="psum_band", bufs=1))
         psum_acc = stack.enter_context(tc.psum_pool(name="psum_acc", bufs=3))
 
-        neg_max = keep.tile([P, PAIRS, QT, 2], F32)
-        row_sum = keep.tile([P, PAIRS, QT, 2], F32)
-        inv_sum = keep.tile([P, PAIRS, QT, 2], F32)
+        neg_max = keep.tile([P, UNITS, SLOTS], F32)
+        row_sum = keep.tile([P, UNITS, SLOTS], F32)
+        inv_sum = keep.tile([P, UNITS, SLOTS], F32)
         merged = keep.tile([P, B, QT, E], BF16)
         v_codes = keep.tile([P, NH * D], U32, align_bytes=64)
         v_scales = keep.tile([P, NH * D], U8, align_bytes=64)
-        wo_raw = keep.tile([P, E // K_PASS, PACK, E], BF16)
-        wo_codes = keep.tile([P, E // K_PASS, E], U32, align_bytes=64)
-        wo_scales = keep.tile([P, E // K_PASS, E], U8, align_bytes=64)
+        wo_raw = keep.tile([P, GROUPS, PACK, E], BF16)
+        wo_codes = keep.tile([P, GROUPS, E], U32, align_bytes=64)
+        wo_scales = keep.tile([P, GROUPS, E], U8, align_bytes=64)
         bias_rows = keep.tile([P, E], BF16)
 
         logit_tiles = {}
@@ -68,6 +85,7 @@ def tile_vitsattention_pa_kernel(tc, logits, v, emb_rel_v, Wo, bo, out):
         band_e_tiles = {}
         band_t_tiles = {}
         band_bank_tiles = {}
+        folded_tiles = {}
         e_tiles = {}
         word_banks = {}
         grouped_tiles = {}
@@ -76,51 +94,68 @@ def tile_vitsattention_pa_kernel(tc, logits, v, emb_rel_v, Wo, bo, out):
         v_grouped_tiles = {}
         wo_grouped_tiles = {}
         acc_tiles = {}
+        scaled_tiles = {}
 
         def band_windows(n, t0, rows):
             start = n * L * L + t0 * (L + 1) - WINDOW
             run = flat_logits[start : start + rows * (L + 1)]
             return run.rearrange("(t s) -> t s", s=L + 1)[:, 0:NREL]
 
-        def load_band(band_logits, n, hh):
+        def load_band_pair(band_logits, n, k0):
             if n == 0:
                 nc.sync.dma_start(
-                    out=band_logits[:, 1:QT, hh, 0:NREL],
+                    out=band_logits[:, 1:QT, 0:NREL],
                     in_=band_windows(n, P, L - P).rearrange("(q p) j -> p q j", p=P),
                 )
-                nc.sync.dma_start(out=band_logits[1:P, 0, hh, 0:NREL], in_=band_windows(n, 1, P - 1))
+                nc.sync.dma_start(out=band_logits[1:P, 0, 0:NREL], in_=band_windows(n, 1, P - 1))
                 nc.sync.dma_start(
-                    out=band_logits[0:1, 0, hh, WINDOW:NREL], in_=flat_logits[0 : WINDOW + 1].unsqueeze(0)
-                )
-            elif n == NH - 1:
-                nc.sync.dma_start(
-                    out=band_logits[:, 0 : QT - 1, hh, 0:NREL],
-                    in_=band_windows(n, 0, L - P).rearrange("(q p) j -> p q j", p=P),
-                )
-                nc.sync.dma_start(
-                    out=band_logits[0 : P - 1, QT - 1, hh, 0:NREL], in_=band_windows(n, L - P, P - 1)
-                )
-                nc.sync.dma_start(
-                    out=band_logits[P - 1 : P, QT - 1, hh, 0 : WINDOW + 1],
-                    in_=flat_logits[NH * L * L - (WINDOW + 1) : NH * L * L].unsqueeze(0),
+                    out=band_logits[0:1, 0, WINDOW:NREL], in_=flat_logits[0 : WINDOW + 1].unsqueeze(0)
                 )
             else:
                 nc.sync.dma_start(
-                    out=band_logits[:, :, hh, 0:NREL],
+                    out=band_logits[:, k0 : k0 + QT, 0:NREL],
                     in_=band_windows(n, 0, L).rearrange("(q p) j -> p q j", p=P),
                 )
 
-        def load_pair(i):
-            band_logits = band_pool.tile([P, QT, 2, BAND_PITCH], BF16, name="band_logits")
-            if i == 0 or i == PAIRS - 1:
+        def load_band_tile(band_logits, q):
+            start = LAST_HEADS * L * L + q * P * (L + 1) - WINDOW
+            whole = SLOTS - 1
+            heads = flat_logits[start : start + whole * L * L].rearrange("(n x) -> n x", x=L * L)
+            nc.sync.dma_start(
+                out=band_logits[:, 0:whole, 0:NREL],
+                in_=heads[:, 0 : P * (L + 1)].rearrange("n (t s) -> t n s", s=L + 1)[:, :, 0:NREL],
+            )
+            if q < QT - 1:
+                nc.sync.dma_start(out=band_logits[:, whole, 0:NREL], in_=band_windows(NH - 1, q * P, P))
+            else:
+                nc.sync.dma_start(
+                    out=band_logits[0 : P - 1, whole, 0:NREL], in_=band_windows(NH - 1, q * P, P - 1)
+                )
+                nc.sync.dma_start(
+                    out=band_logits[P - 1 : P, whole, 0 : WINDOW + 1],
+                    in_=flat_logits[NH * L * L - (WINDOW + 1) : NH * L * L].unsqueeze(0),
+                )
+
+        def load_unit(u):
+            a = logit_pool.tile([P, SLOTS, L], BF16, name="a")
+            band_logits = band_pool.tile([P, SLOTS, BAND_PITCH], BF16, name="band_logits")
+            if u == 0 or u == UNITS - 1:
                 nc.gpsimd.memset(band_logits[:], 0.0)
-            for hh in range(2):
-                n = 2 * i + hh
-                a = logit_pool.tile([P, QT, L], BF16, name="a")
-                nc.sync.dma_start(out=a[:], in_=logits[n].rearrange("(q p) k -> p q k", p=P))
-                logit_tiles[n] = a
-                load_band(band_logits, n, hh)
-            band_logit_tiles[i] = band_logits
+            if is_pair(u):
+                for hh in range(2):
+                    k0 = hh * QT
+                    nc.sync.dma_start(
+                        out=a[:, k0 : k0 + QT, :], in_=logits[2 * u + hh].rearrange("(q p) k -> p q k", p=P)
+                    )
+                    load_band_pair(band_logits, 2 * u + hh, k0)
+            else:
+                q = u - PAIR_UNITS
+                nc.sync.dma_start(
+                    out=a[:], in_=logits[LAST_HEADS:NH, q * P : (q + 1) * P, :].rearrange("n p k -> p n k")
+                )
+                load_band_tile(band_logits, q)
+            logit_tiles[u] = a
+            band_logit_tiles[u] = band_logits
 
         def load_v(c):
             v_raw = weight_pool.tile([P, V_CHUNK, PACK, D], BF16, name="v_raw")
@@ -171,252 +206,397 @@ def tile_vitsattention_pa_kernel(tc, logits, v, emb_rel_v, Wo, bo, out):
                 in_=wo_grouped_tiles[w][:].rearrange("p o t -> p (o t)"),
             )
 
-        def row_max(i, heads):
-            narrowed = {0: logit_tiles[2 * i], 1: logit_tiles[2 * i + 1]}
-            for width in FOLD_WIDTHS:
-                for hh in heads:
-                    folded = fold_pool.tile([P, QT, width], BF16, name="folded", tag="folded_%d_%d" % (width, hh))
-                    nc.vector.tensor_tensor(
-                        out=folded[:],
-                        in0=narrowed[hh][:, :, 0:width],
-                        in1=narrowed[hh][:, :, width : 2 * width],
-                        op=ALU.max,
-                    )
-                    narrowed[hh] = folded
-            for hh in heads:
-                nc.vector.tensor_reduce(
-                    out=neg_max[:, i, :, hh], in_=narrowed[hh][:], axis=AXIS.X, op=ALU.max, negate=True
-                )
+        def fold(u, level, k0=0, k1=SLOTS):
+            width = FOLD_WIDTHS[level]
+            if level == 0:
+                wide = logit_tiles[u][:, k0:k1, :]
+            else:
+                wide = folded_tiles[(u, level - 1)][:, k0:k1, :]
+            if (u, level) not in folded_tiles:
+                folded = fold_pool.tile([P, SLOTS, width], BF16, name="folded", tag="folded_%d" % width)
+                folded_tiles[(u, level)] = folded
+            nc.vector.tensor_tensor(
+                out=folded_tiles[(u, level)][:, k0:k1, :],
+                in0=wide[:, :, 0:width],
+                in1=wide[:, :, width : 2 * width],
+                op=ALU.max,
+            )
 
-        def exponentials(n):
-            i, hh = divmod(n, 2)
-            e = e_pool.tile([P, QT, L], BF16, name="e")
-            for q in range(QT):
+        def finish_max(u, k0=0, k1=SLOTS):
+            nc.vector.tensor_reduce(
+                out=neg_max[:, u, k0:k1],
+                in_=folded_tiles[(u, len(FOLD_WIDTHS) - 1)][:, k0:k1, :],
+                axis=AXIS.X,
+                op=ALU.max,
+                negate=True,
+            )
+
+        def exponentials(u, half):
+            if half == 0:
+                e = e_pool.tile([P, SLOTS, L], BF16, name="e")
+                e_tiles[u] = e
+            for k in range(half * HALF, (half + 1) * HALF):
                 nc.scalar.activation(
-                    out=e[:, q, :],
-                    in_=logit_tiles[n][:, q, :],
+                    out=e_tiles[u][:, k, :],
+                    in_=logit_tiles[u][:, k, :],
                     func=ACT.Exp,
-                    bias=neg_max[:, i, q, hh : hh + 1],
+                    bias=neg_max[:, u, k : k + 1],
                     scale=1.0,
-                    accum_out=row_sum[:, i, q, hh : hh + 1],
+                    accum_out=row_sum[:, u, k : k + 1],
                 )
-            e_tiles[n] = e
 
-        def transpose_words(key, words, first_word):
-            for half in range(2):
+        def transpose_e(u, half):
+            words = e_tiles[u][:].bitcast(F32)
+            for part in range(2):
                 bank = psum_words.tile([P, 2, 2 * P], F32, name="bank")
-                for u in range(2):
+                for w in range(2):
                     for r in range(2):
                         nc.tensor.transpose(
-                            bank[:, u, r * P : (r + 1) * P],
-                            words[:, 2 * half + r, first_word + u * P : first_word + (u + 1) * P],
+                            bank[:, w, r * P : (r + 1) * P],
+                            words[:, half * HALF + 2 * part + r, w * P : (w + 1) * P],
                             ident[:],
                         )
-                word_banks[(key, half)] = bank
+                word_banks[(u, half, part)] = bank
 
-        def regroup_words(key, copies):
-            grouped = grouped_pool.tile([P, L, PACK], BF16, name="grouped", align_bytes=64)
-            grouped_words = grouped[:].bitcast(F32)
-            for half in range(2):
-                source = word_banks[(key, half)][:].rearrange("p u r -> p r u")
-                target = grouped_words[:, half * 2 * P : (half + 1) * 2 * P, :]
-                copies[half](out=target, in_=source)
-            grouped_tiles[key] = grouped
+        def regroup_e(u, half, part, copy):
+            if (u, half) not in grouped_tiles:
+                grouped = grouped_pool.tile([P, L, PACK], BF16, name="grouped", align_bytes=64)
+                grouped_tiles[(u, half)] = grouped
+            rows = grouped_tiles[(u, half)][:].bitcast(F32)[:, part * 2 * P : (part + 1) * 2 * P, :]
+            copy(out=rows, in_=word_banks[(u, half, part)][:].rearrange("p w r -> p r w"))
 
-        def quantise_rows(key):
+        def quantise_e(u, half):
             codes = code_pool.tile([P, L], U32, name="codes", align_bytes=64)
             scales = code_pool.tile([P, L], U8, name="scales", align_bytes=64)
             nc.vector.quantize_mx(
                 out=codes[:].bitcast(FP8X4),
                 scales=scales[:],
-                in_=grouped_tiles[key][:].rearrange("p r t -> p (r t)"),
+                in_=grouped_tiles[(u, half)][:].rearrange("p r t -> p (r t)"),
             )
-            code_tiles[key] = (codes, scales)
+            code_tiles[(u, half)] = (codes, scales)
 
-        def context(i):
-            ctx = psum_acc.tile([P, N_TILE], F32, name="ctx", tag="acc")
-            ctx_view = ctx[:].rearrange("p (q h d) -> p q h d", q=QT, h=2)
-            for hh in range(2):
-                n = 2 * i + hh
-                codes, scales = code_tiles[("e", n)]
-                for q in range(QT):
-                    nc.tensor.matmul_mx(
-                        out=ctx_view[:, q, hh, :],
-                        lhsT=codes[:, q * P : (q + 1) * P].bitcast(FP8X4),
-                        lhsT_scale=scales[:, q * P : (q + 1) * P],
-                        rhs=v_codes[:, n * D : (n + 1) * D].bitcast(FP8X4),
-                        rhs_scale=v_scales[:, n * D : (n + 1) * D],
-                        start=True,
-                        stop=True,
-                    )
-            acc_tiles[("ctx", i)] = ctx
+        def context(u, half):
+            if half == 0:
+                ctx = psum_acc.tile([P, SLOTS, D], F32, name="ctx", tag="acc")
+                acc_tiles[("ctx", u)] = ctx
+            codes, scales = code_tiles[(u, half)]
+            for j in range(HALF):
+                k = half * HALF + j
+                n = slots_of(u)[k][0]
+                nc.tensor.matmul_mx(
+                    out=acc_tiles[("ctx", u)][:, k, :],
+                    lhsT=codes[:, j * P : (j + 1) * P].bitcast(FP8X4),
+                    lhsT_scale=scales[:, j * P : (j + 1) * P],
+                    rhs=v_codes[:, n * D : (n + 1) * D].bitcast(FP8X4),
+                    rhs_scale=v_scales[:, n * D : (n + 1) * D],
+                    start=True,
+                    stop=True,
+                )
 
-        def shift_band(i):
-            shifted = band_pool.tile([P, QT, 2, NREL], F32, name="shifted")
+        def shift_band(u):
+            shifted = band_pool.tile([P, SLOTS, NREL], F32, name="shifted")
             nc.gpsimd.tensor_tensor(
                 out=shifted[:],
-                in0=band_logit_tiles[i][:, :, :, 0:NREL],
-                in1=neg_max[:, i].unsqueeze(3).to_broadcast([P, QT, 2, NREL]),
+                in0=band_logit_tiles[u][:, :, 0:NREL],
+                in1=neg_max[:, u].unsqueeze(2).to_broadcast([P, SLOTS, NREL]),
                 op=ALU.add,
             )
-            nc.gpsimd.tensor_tensor(out=shifted[:], in0=shifted[:], in1=edge_mask[:], op=ALU.add)
-            shifted_tiles[i] = shifted
+            if is_pair(u):
+                by_tile = shifted[:].rearrange("p (h q) j -> p h q j", q=QT)
+                mask = edge_mask[:].unsqueeze(1).to_broadcast([P, 2, QT, NREL])
+                nc.gpsimd.tensor_tensor(out=by_tile, in0=by_tile, in1=mask, op=ALU.add)
+            elif slots_of(u)[0][1] in (0, QT - 1):
+                mask = edge_mask[:, slots_of(u)[0][1]].unsqueeze(1).to_broadcast([P, SLOTS, NREL])
+                nc.gpsimd.tensor_tensor(out=shifted[:], in0=shifted[:], in1=mask, op=ALU.add)
+            shifted_tiles[u] = shifted
 
-        def band_exponentials(i):
-            band_e = band_pool.tile([P, QT, 2, NREL], F32, name="band_e")
-            nc.scalar.activation(out=band_e[:], in_=shifted_tiles[i][:], func=ACT.Exp)
-            band_e_tiles[i] = band_e
+        def band_exponentials(u):
+            band_e = band_pool.tile([P, SLOTS, NREL], F32, name="band_e")
+            nc.scalar.activation(out=band_e[:], in_=shifted_tiles[u][:], func=ACT.Exp)
+            band_e_tiles[u] = band_e
 
-        def normalise_band(i):
-            nc.vector.reciprocal(out=inv_sum[:, i], in_=row_sum[:, i])
-            padded = band_padded[i % 2]
-            nc.gpsimd.tensor_tensor(
-                out=padded[:, 0 : 2 * QT * NREL].rearrange("p (q h j) -> p q h j", q=QT, h=2),
-                in0=band_e_tiles[i][:],
-                in1=inv_sum[:, i].unsqueeze(3).to_broadcast([P, QT, 2, NREL]),
+        def invert_sums(u):
+            nc.vector.reciprocal(out=inv_sum[:, u], in_=row_sum[:, u])
+
+        def split_band(u):
+            spread_inv = (
+                inv_sum[:, u].rearrange("p (g k) -> p g k", k=HALF).unsqueeze(3).to_broadcast([P, 2, HALF, NREL])
+            )
+            columns = band_padded[u % 2][:, :, 0:BAND_ROWS].rearrange("p g (k t j) -> p g k t j", k=HALF, t=BAND_TERMS)
+            high, middle, low = (columns[:, :, :, term, :] for term in range(BAND_TERMS))
+            weight = band_pool.tile([P, 2, HALF, NREL], F32, name="weight")
+            rest = band_pool.tile([P, 2, HALF, NREL], F32, name="rest")
+            band_e = band_e_tiles[u][:].rearrange("p (g k) j -> p g k j", k=HALF)
+            nc.gpsimd.tensor_tensor(out=weight[:], in0=band_e, in1=spread_inv, op=ALU.mult)
+            nc.gpsimd.tensor_tensor(out=high, in0=band_e, in1=spread_inv, op=ALU.mult)
+            nc.gpsimd.tensor_tensor(out=rest[:], in0=weight[:], in1=high, op=ALU.subtract)
+            nc.gpsimd.tensor_tensor(out=middle, in0=weight[:], in1=high, op=ALU.subtract)
+            nc.gpsimd.tensor_tensor(out=low, in0=rest[:], in1=middle, op=ALU.subtract)
+
+        def transpose_band(u):
+            band_bank = psum_band.tile([P, 2, P], BF16, name="band_bank")
+            for half in range(2):
+                nc.tensor.transpose(band_bank[:, half, :], band_padded[u % 2][:, half, :], ident_bf16[:])
+            band_bank_tiles[u] = band_bank
+
+        def keep_band(u):
+            band_t = attn_pool.tile([P, 2, P], BF16, name="band_t")
+            nc.scalar.copy(out=band_t[:], in_=band_bank_tiles[u][:])
+            band_t_tiles[u] = band_t
+
+        def relative(u):
+            rel = psum_acc.tile([P, SLOTS, D], F32, name="rel", tag="acc")
+            for half in range(2):
+                nc.tensor.matmul(
+                    out=rel[:, half * HALF : (half + 1) * HALF, :].rearrange("p k d -> p (k d)"),
+                    lhsT=band_t_tiles[u][:, half, :],
+                    rhs=rel_rows[:].rearrange("p k d -> p (k d)"),
+                    start=True,
+                    stop=True,
+                )
+            acc_tiles[("rel", u)] = rel
+
+        def scale_context(u):
+            scaled = attn_pool.tile([P, SLOTS, D], F32, name="scaled")
+            nc.vector.tensor_tensor(
+                out=scaled[:],
+                in0=acc_tiles[("ctx", u)][:],
+                in1=inv_sum[:, u].unsqueeze(2).to_broadcast([P, SLOTS, D]),
                 op=ALU.mult,
             )
+            scaled_tiles[u] = scaled
 
-        def transpose_band(i):
-            band_bank = psum_band.tile([P, P], F32, name="band_bank")
-            nc.tensor.transpose(band_bank[:], band_padded[i % 2][:], ident[:])
-            band_bank_tiles[i] = band_bank
+        def merge(u):
+            scaled = scaled_tiles[u][:]
+            rel = acc_tiles[("rel", u)][:]
+            if is_pair(u):
+                b, pair_in_batch = divmod(u, PAIRS_PER_BATCH)
+                cols = slice(pair_in_batch * 2 * D, (pair_in_batch + 1) * 2 * D)
+                target = merged[:, b, :, cols].rearrange("p q (h d) -> p h q d", h=2)
+                scaled = scaled.rearrange("p (h q) d -> p h q d", q=QT)
+                rel = rel.rearrange("p (h q) d -> p h q d", q=QT)
+            else:
+                cols = slice(E - SLOTS * D, E)
+                target = merged[:, B - 1, u - PAIR_UNITS, cols].rearrange("p (k d) -> p k d", d=D)
+            nc.vector.tensor_tensor(out=target, in0=scaled, in1=rel, op=ALU.add)
 
-        def keep_band(i):
-            band_t = attn_pool.tile([P, P], F32, name="band_t")
-            nc.vector.tensor_copy(out=band_t[:], in_=band_bank_tiles[i][:])
-            band_t_tiles[i] = band_t
+        def transpose_merged(b, q):
+            words = merged[:, b, q, :].bitcast(F32)
+            bank = psum_words.tile([P, GROUPS, 2, P], F32, name="bank")
+            for g in range(GROUPS):
+                for w in range(2):
+                    first_word = g * K_PASS // 2 + w * P
+                    nc.tensor.transpose(bank[:, g, w, :], words[:, first_word : first_word + P], ident[:])
+            word_banks[("m", b, q)] = bank
 
-        def relative(i):
-            rel = psum_acc.tile([P, N_TILE], F32, name="rel", tag="acc")
-            nc.tensor.matmul(out=rel[:], lhsT=band_t_tiles[i][:], rhs=rel_rows[:], start=True, stop=True)
-            acc_tiles[("rel", i)] = rel
+        def regroup_merged(b, q, copy):
+            grouped = grouped_pool.tile([P, GROUPS, P, PACK], BF16, name="grouped_m", align_bytes=64)
+            copy(out=grouped[:].bitcast(F32), in_=word_banks[("m", b, q)][:].rearrange("p g w r -> p g r w"))
+            grouped_tiles[("m", b, q)] = grouped
 
-        def attention(i):
-            b, pair_in_batch = divmod(i, PAIRS_PER_BATCH)
-            scaled = attn_pool.tile([P, N_TILE], F32, name="scaled")
-            nc.vector.tensor_tensor(
-                out=scaled[:].rearrange("p (q h d) -> p q h d", q=QT, h=2),
-                in0=acc_tiles[("ctx", i)][:].rearrange("p (q h d) -> p q h d", q=QT, h=2),
-                in1=inv_sum[:, i].unsqueeze(3).to_broadcast([P, QT, 2, D]),
-                op=ALU.mult,
+        def quantise_merged(b, q):
+            codes = code_pool.tile([P, GROUPS * P], U32, name="codes_m", align_bytes=64)
+            scales = code_pool.tile([P, GROUPS * P], U8, name="scales_m", align_bytes=64)
+            nc.vector.quantize_mx(
+                out=codes[:].bitcast(FP8X4),
+                scales=scales[:],
+                in_=grouped_tiles[("m", b, q)][:].rearrange("p g r t -> p (g r t)"),
             )
+            code_tiles[("m", b, q)] = (codes, scales)
+
+        def project(b, q, part):
+            cols = slice(part * N_TILE, (part + 1) * N_TILE)
+            codes, scales = code_tiles[("m", b, q)]
+            acc = psum_acc.tile([P, N_TILE], F32, name="acc", tag="acc")
+            for g in range(GROUPS):
+                nc.tensor.matmul_mx(
+                    out=acc[:],
+                    lhsT=codes[:, g * P : (g + 1) * P].bitcast(FP8X4),
+                    lhsT_scale=scales[:, g * P : (g + 1) * P],
+                    rhs=wo_codes[:, g, cols].bitcast(FP8X4),
+                    rhs_scale=wo_scales[:, g, cols],
+                    start=(g == 0),
+                    stop=(g == GROUPS - 1),
+                )
+            acc_tiles[("out", b, q, part)] = acc
+
+        def finish_output(b, q, part):
+            cols = slice(part * N_TILE, (part + 1) * N_TILE)
+            result = out_pool.tile([P, N_TILE], F32, name="result")
             nc.vector.tensor_tensor(
-                out=merged[:, b, :, pair_in_batch * 2 * D : (pair_in_batch + 1) * 2 * D],
-                in0=scaled[:].rearrange("p (q c) -> p q c", q=QT),
-                in1=acc_tiles[("rel", i)][:].rearrange("p (q c) -> p q c", q=QT),
-                op=ALU.add,
+                out=result[:], in0=acc_tiles[("out", b, q, part)][:], in1=bias_rows[:, cols], op=ALU.add
             )
+            nc.sync.dma_start(out=out[b, q * P : (q + 1) * P, cols], in_=result[:])
 
-        def project(b):
-            merged_words = merged[:, b].bitcast(F32)
-            for g in range(E // K_PASS):
-                transpose_words(("m", g), merged_words, g * K_PASS // 2)
-                regroup_words(("m", g), (nc.scalar.copy, nc.vector.tensor_copy))
-            for g in range(E // K_PASS):
-                quantise_rows(("m", g))
-            for q in range(QT):
-                result = out_pool.tile([P, E], F32, name="result")
-                for half in range(E // N_TILE):
-                    cols = slice(half * N_TILE, (half + 1) * N_TILE)
-                    acc = psum_acc.tile([P, N_TILE], F32, name="acc", tag="acc")
-                    for g in range(E // K_PASS):
-                        codes, scales = code_tiles[("m", g)]
-                        nc.tensor.matmul_mx(
-                            out=acc[:],
-                            lhsT=codes[:, q * P : (q + 1) * P].bitcast(FP8X4),
-                            lhsT_scale=scales[:, q * P : (q + 1) * P],
-                            rhs=wo_codes[:, g, cols].bitcast(FP8X4),
-                            rhs_scale=wo_scales[:, g, cols],
-                            start=(g == 0),
-                            stop=(g == E // K_PASS - 1),
-                        )
-                    nc.vector.tensor_tensor(out=result[:, cols], in0=acc[:], in1=bias_rows[:, cols], op=ALU.add)
-                nc.sync.dma_start(out=out[b, q * P : (q + 1) * P, :], in_=result[:])
+        table_probe = keep.tile([P, 1], F32)
+        nc.vector.memset(table_probe[:], 0.0)
+        nc.scalar.activation(out=table_probe[:], in_=table_probe[:], func=ACT.Exp)
 
-        load_pair(0)
+        load_unit(0)
+        rel_values = keep.tile([P, D], BF16)
+        nc.vector.memset(rel_values[:], 0.0)
+        nc.sync.dma_start(out=rel_values[0:NREL, :], in_=emb_rel_v[0])
         load_v(0)
-        load_pair(1)
+        load_unit(1)
 
         ident = keep.tile([P, P], F32)
         make_identity(nc, ident[:])
+        ident_bf16 = keep.tile([P, P], BF16)
+        make_identity(nc, ident_bf16[:])
 
-        edge_mask = keep.tile([P, QT, 2, NREL], F32)
+        edge_mask = keep.tile([P, QT, NREL], F32)
         nc.gpsimd.memset(edge_mask[:], 0.0)
         nc.gpsimd.affine_select(
-            out=edge_mask[:], in_=edge_mask[:], pattern=[[P, QT], [0, 2], [1, NREL]],
+            out=edge_mask[:], in_=edge_mask[:], pattern=[[P, QT], [1, NREL]],
             compare_op=ALU.is_ge, fill=MASKED, base=-WINDOW, channel_multiplier=1,
         )
         nc.gpsimd.affine_select(
-            out=edge_mask[:], in_=edge_mask[:], pattern=[[-P, QT], [0, 2], [-1, NREL]],
+            out=edge_mask[:], in_=edge_mask[:], pattern=[[-P, QT], [-1, NREL]],
             compare_op=ALU.is_ge, fill=MASKED, base=L - 1 + WINDOW, channel_multiplier=-1,
         )
 
-        band_padded_0 = keep.tile([P, P], F32)
-        band_padded_1 = keep.tile([P, P], F32)
+        band_padded_0 = keep.tile([P, 2, P], BF16)
+        band_padded_1 = keep.tile([P, 2, P], BF16)
         band_padded = (band_padded_0, band_padded_1)
         nc.gpsimd.memset(band_padded_0[:], 0.0)
         nc.gpsimd.memset(band_padded_1[:], 0.0)
 
-        rel_rows_bf16 = keep.tile([P, N_TILE], BF16)
-        nc.vector.memset(rel_rows_bf16[:], 0.0)
-        for tile_of_pair in range(2 * QT):
-            nc.scalar.dma_start(
-                out=rel_rows_bf16[
-                    tile_of_pair * NREL : (tile_of_pair + 1) * NREL, tile_of_pair * D : (tile_of_pair + 1) * D
-                ],
-                in_=emb_rel_v[0],
+        rel_spread = keep.tile([P, P], BF16)
+        nc.gpsimd.memset(rel_spread[:], 0.0)
+        nc.gpsimd.affine_select(
+            out=rel_spread[:, 0:BAND_ROWS], in_=rel_spread[:, 0:BAND_ROWS],
+            pattern=[[0, HALF * BAND_TERMS], [-1, NREL]],
+            compare_op=ALU.not_equal, fill=1.0, base=0, channel_multiplier=1,
+        )
+        rel_rows = keep.tile([P, HALF, D], BF16)
+
+        def build_rel_rows():
+            rel_bank = psum_acc.tile([P, D], F32, name="rel_bank", tag="acc")
+            nc.tensor.matmul(out=rel_bank[:], lhsT=rel_spread[:], rhs=rel_values[:], start=True, stop=True)
+            nc.vector.tensor_copy(out=rel_rows[:], in_=rel_bank[:].unsqueeze(1).to_broadcast([P, HALF, D]))
+            rows_of_slot = BAND_TERMS * NREL
+            nc.gpsimd.affine_select(
+                out=rel_rows[:], in_=rel_rows[:], pattern=[[-rows_of_slot, HALF], [0, D]],
+                compare_op=ALU.is_ge, fill=0.0, base=0, channel_multiplier=1,
             )
-        rel_rows = keep.tile([P, N_TILE], F32)
-        nc.vector.tensor_copy(out=rel_rows[:], in_=rel_rows_bf16[:])
+            nc.gpsimd.affine_select(
+                out=rel_rows[:], in_=rel_rows[:], pattern=[[rows_of_slot, HALF], [0, D]],
+                compare_op=ALU.is_ge, fill=0.0, base=rows_of_slot - 1, channel_multiplier=-1,
+            )
 
-        row_max(0, (0,))
-        row_max(0, (1,))
+        weight_pieces = (
+            (regroup_v, quantise_v, 0),
+            (regroup_wo, quantise_wo, 0),
+            (regroup_v, quantise_v, 1),
+            (regroup_wo, quantise_wo, 1),
+            (regroup_wo, quantise_wo, 2),
+            (regroup_v, quantise_v, 2),
+            (regroup_wo, quantise_wo, 3),
+            (regroup_v, quantise_v, 3),
+        )
+        regroup_step = [-1] + [3 * x // 2 for x in range(1, len(weight_pieces))]
 
-        for s in range(PAIRS + 2):
-            if s + 2 < PAIRS:
-                load_pair(s + 2)
-            if s % 4 == 0 and s // 4 + 1 < NH // V_CHUNK:
-                load_v(s // 4 + 1)
-            if s < E // K_PASS:
-                load_wo(s)
-            if s == E // K_PASS:
-                nc.sync.dma_start(out=bias_rows[:], in_=bo.partition_broadcast(P))
+        def weight_work(s):
+            for x, (regroup, quantise, piece) in enumerate(weight_pieces):
+                if s == regroup_step[x] + 1:
+                    quantise(piece)
+            for x, (regroup, quantise, piece) in enumerate(weight_pieces):
+                if s == regroup_step[x]:
+                    regroup(piece)
 
-            if 0 <= s - 1 < PAIRS:
-                normalise_band(s - 1)
-                transpose_words(("e", 2 * s - 2), e_tiles[2 * s - 2][:].bitcast(F32), 0)
-                transpose_words(("e", 2 * s - 1), e_tiles[2 * s - 1][:].bitcast(F32), 0)
-                transpose_band(s - 1)
-            if s < PAIRS:
-                shift_band(s)
-            if 0 <= s - 2 < PAIRS:
-                quantise_rows(("e", 2 * s - 4))
-                quantise_rows(("e", 2 * s - 3))
-                relative(s - 2)
-                context(s - 2)
-            for hh in range(2):
-                if s < PAIRS:
-                    exponentials(2 * s + hh)
-                if 0 <= s - 1 < PAIRS:
-                    to_vector = hh == 1 or s % 2 == 0
-                    second_copy = nc.vector.tensor_copy if to_vector else nc.scalar.copy
-                    regroup_words(("e", 2 * s - 2 + hh), (nc.scalar.copy, second_copy))
-            if s < PAIRS:
-                band_exponentials(s)
-            if s + 1 < PAIRS:
-                row_max(s + 1, (0, 1))
-            if s % 4 == 0 and s // 4 < NH // V_CHUNK:
-                regroup_v(s // 4)
-            if s % 4 == 1 and s // 4 < NH // V_CHUNK:
-                quantise_v(s // 4)
-            if s % 2 == 0 and 0 <= s // 2 - 1 < 2 * E // N_TILE:
-                regroup_wo(s // 2 - 1)
-            if s % 2 == 1 and 0 <= s // 2 - 1 < 2 * E // N_TILE:
-                quantise_wo(s // 2 - 1)
-            if 0 <= s - 1 < PAIRS:
-                keep_band(s - 1)
-            if 0 <= s - 2 < PAIRS:
-                attention(s - 2)
-                if (s - 2) % PAIRS_PER_BATCH == PAIRS_PER_BATCH - 1:
-                    project((s - 2) // PAIRS_PER_BATCH)
+        def first_rows_ready(b, q):
+            if b == 0:
+                return PAIRS_PER_BATCH + 2 + q
+            return PAIR_UNITS + 2 + q
+
+        with tc.manual_schedule(
+            engines={mybir.EngineType.PE, mybir.EngineType.Activation, mybir.EngineType.DVE}
+        ):
+            for half in range(2):
+                for level in range(len(FOLD_WIDTHS)):
+                    fold(0, level, half * HALF, (half + 1) * HALF)
+                finish_max(0, half * HALF, (half + 1) * HALF)
+            shift_band(0)
+            weight_work(-1)
+
+            for s in range(UNITS + 2):
+                now, last, older = s, s - 1, s - 2
+                has_next, has_now, has_last, has_older = (
+                    s + 1 < UNITS, s < UNITS, 0 <= s - 1 < UNITS, 0 <= s - 2 < UNITS
+                )
+                if s + 2 < UNITS:
+                    load_unit(s + 2)
+                if s == 0:
+                    load_wo(0)
+                if s == 2:
+                    load_wo(1)
+                if s in (1, 5, 8):
+                    load_v((1, 5, 8).index(s) + 1)
+                if s == 4:
+                    nc.sync.dma_start(out=bias_rows[:], in_=bo.partition_broadcast(P))
+                to_project = [(b, q) for b in range(B) for q in range(QT) if first_rows_ready(b, q) == s - 1]
+                to_transpose = [(b, q) for b in range(B) for q in range(QT) if first_rows_ready(b, q) == s]
+
+                if has_last:
+                    invert_sums(last)
+                    split_band(last)
+                if has_older:
+                    relative(older)
+                if has_last:
+                    transpose_e(last, 1)
+                for b, q in to_project:
+                    quantise_merged(b, q)
+                if has_next:
+                    fold(s + 1, 0)
+                if has_now:
+                    exponentials(now, 0)
+                if has_last:
+                    quantise_e(last, 0)
+                    context(last, 0)
+                if has_next:
+                    fold(s + 1, 1)
+                if has_older:
+                    scale_context(older)
+                if has_next:
+                    fold(s + 1, 2)
+                if has_older:
+                    merge(older)
+                if has_next:
+                    fold(s + 1, 3)
+                if has_last:
+                    regroup_e(last, 1, 0, nc.scalar.copy)
+                    regroup_e(last, 1, 1, nc.vector.tensor_copy)
+                if has_now:
+                    transpose_e(now, 0)
+                for b, q in to_project:
+                    project(b, q, 0)
+                    project(b, q, 1)
+                if has_now:
+                    exponentials(now, 1)
+                if has_next:
+                    finish_max(s + 1)
+                    shift_band(s + 1)
+                for b, q in to_project:
+                    finish_output(b, q, 0)
+                    finish_output(b, q, 1)
+                weight_work(s)
+                if has_last:
+                    quantise_e(last, 1)
+                    transpose_band(last)
+                    context(last, 1)
+                    keep_band(last)
+                if s == 0:
+                    build_rel_rows()
+                for b, q in to_transpose:
+                    transpose_merged(b, q)
+                    regroup_merged(b, q, nc.scalar.copy)
+                if has_now:
+                    regroup_e(now, 0, 0, nc.scalar.copy)
+                    regroup_e(now, 0, 1, nc.scalar.copy if s in regroup_step else nc.vector.tensor_copy)
+                    band_exponentials(now)
+
+            b, q = B - 1, QT - 1
+            quantise_merged(b, q)
+            for part in range(2):
+                project(b, q, part)
+                finish_output(b, q, part)

@@ -32,8 +32,7 @@ BAND_PITCH = 16
 FOLD_WIDTHS = (L // 2, L // 4, L // 8, L // 16)
 V_CHUNK = 8
 RUN = 4
-BAND_TERMS = 3
-BAND_ROWS = HALF * BAND_TERMS * NREL
+BAND_ROWS = SLOTS * NREL
 MASKED = -1.0e30
 
 FLOPS = 2 * NH * L * L * D + 2 * NH * L * NREL * D + 2 * B * L * E * E
@@ -55,8 +54,8 @@ def tile_vitsattention_pa_kernel(tc, logits, v, emb_rel_v, Wo, bo, out):
 
     with ExitStack() as stack:
         keep = stack.enter_context(tc.tile_pool(name="keep", bufs=1))
-        logit_pool = stack.enter_context(tc.tile_pool(name="logit_pool", bufs=4))
-        band_pool = stack.enter_context(tc.tile_pool(name="band_pool", bufs=4))
+        logit_pool = stack.enter_context(tc.tile_pool(name="logit_pool", bufs=5))
+        band_pool = stack.enter_context(tc.tile_pool(name="band_pool", bufs=5))
         fold_pool = stack.enter_context(tc.tile_pool(name="fold_pool", bufs=2))
         e_pool = stack.enter_context(tc.tile_pool(name="e_pool", bufs=3))
         grouped_pool = stack.enter_context(tc.tile_pool(name="grouped_pool", bufs=4))
@@ -64,9 +63,8 @@ def tile_vitsattention_pa_kernel(tc, logits, v, emb_rel_v, Wo, bo, out):
         weight_pool = stack.enter_context(tc.tile_pool(name="weight_pool", bufs=2))
         attn_pool = stack.enter_context(tc.tile_pool(name="attn_pool", bufs=3))
         out_pool = stack.enter_context(tc.tile_pool(name="out_pool", bufs=3))
-        psum_words = stack.enter_context(tc.psum_pool(name="psum_words", bufs=4))
-        psum_band = stack.enter_context(tc.psum_pool(name="psum_band", bufs=1))
-        psum_acc = stack.enter_context(tc.psum_pool(name="psum_acc", bufs=3))
+        psum_words = stack.enter_context(tc.psum_pool(name="psum_words", bufs=3))
+        psum_acc = stack.enter_context(tc.psum_pool(name="psum_acc", bufs=5))
 
         neg_max = keep.tile([P, UNITS, SLOTS], F32)
         row_sum = keep.tile([P, UNITS, SLOTS], F32)
@@ -136,25 +134,30 @@ def tile_vitsattention_pa_kernel(tc, logits, v, emb_rel_v, Wo, bo, out):
                     in_=flat_logits[NH * L * L - (WINDOW + 1) : NH * L * L].unsqueeze(0),
                 )
 
-        def load_unit(u):
+        def load_logits(u):
             a = logit_pool.tile([P, SLOTS, L], BF16, name="a")
-            band_logits = band_pool.tile([P, SLOTS, BAND_PITCH], BF16, name="band_logits")
-            if u == 0 or u == UNITS - 1:
-                nc.gpsimd.memset(band_logits[:], 0.0)
             if is_pair(u):
                 for hh in range(2):
-                    k0 = hh * QT
                     nc.sync.dma_start(
-                        out=a[:, k0 : k0 + QT, :], in_=logits[2 * u + hh].rearrange("(q p) k -> p q k", p=P)
+                        out=a[:, hh * QT : (hh + 1) * QT, :],
+                        in_=logits[2 * u + hh].rearrange("(q p) k -> p q k", p=P),
                     )
-                    load_band_pair(band_logits, 2 * u + hh, k0)
             else:
                 q = u - PAIR_UNITS
                 nc.sync.dma_start(
                     out=a[:], in_=logits[LAST_HEADS:NH, q * P : (q + 1) * P, :].rearrange("n p k -> p n k")
                 )
-                load_band_tile(band_logits, q)
             logit_tiles[u] = a
+
+        def load_band(u):
+            band_logits = band_pool.tile([P, SLOTS, BAND_PITCH], BF16, name="band_logits")
+            if u == 0 or u == UNITS - 1:
+                nc.gpsimd.memset(band_logits[:], 0.0)
+            if is_pair(u):
+                for hh in range(2):
+                    load_band_pair(band_logits, 2 * u + hh, hh * QT)
+            else:
+                load_band_tile(band_logits, u - PAIR_UNITS)
             band_logit_tiles[u] = band_logits
 
         def load_v(c):
@@ -231,11 +234,11 @@ def tile_vitsattention_pa_kernel(tc, logits, v, emb_rel_v, Wo, bo, out):
                 negate=True,
             )
 
-        def exponentials(u, half):
-            if half == 0:
+        def exponentials(u, slots):
+            if u not in e_tiles:
                 e = e_pool.tile([P, SLOTS, L], BF16, name="e")
                 e_tiles[u] = e
-            for k in range(half * HALF, (half + 1) * HALF):
+            for k in slots:
                 nc.scalar.activation(
                     out=e_tiles[u][:, k, :],
                     in_=logit_tiles[u][:, k, :],
@@ -318,42 +321,33 @@ def tile_vitsattention_pa_kernel(tc, logits, v, emb_rel_v, Wo, bo, out):
         def invert_sums(u):
             nc.vector.reciprocal(out=inv_sum[:, u], in_=row_sum[:, u])
 
-        def split_band(u):
-            spread_inv = (
-                inv_sum[:, u].rearrange("p (g k) -> p g k", k=HALF).unsqueeze(3).to_broadcast([P, 2, HALF, NREL])
+        def weigh_band(u):
+            nc.gpsimd.tensor_tensor(
+                out=band_padded[u % 2][:, 0:BAND_ROWS].rearrange("p (k j) -> p k j", j=NREL),
+                in0=band_e_tiles[u][:],
+                in1=inv_sum[:, u].unsqueeze(2).to_broadcast([P, SLOTS, NREL]),
+                op=ALU.mult,
             )
-            columns = band_padded[u % 2][:, :, 0:BAND_ROWS].rearrange("p g (k t j) -> p g k t j", k=HALF, t=BAND_TERMS)
-            high, middle, low = (columns[:, :, :, term, :] for term in range(BAND_TERMS))
-            weight = band_pool.tile([P, 2, HALF, NREL], F32, name="weight")
-            rest = band_pool.tile([P, 2, HALF, NREL], F32, name="rest")
-            band_e = band_e_tiles[u][:].rearrange("p (g k) j -> p g k j", k=HALF)
-            nc.gpsimd.tensor_tensor(out=weight[:], in0=band_e, in1=spread_inv, op=ALU.mult)
-            nc.gpsimd.tensor_tensor(out=high, in0=band_e, in1=spread_inv, op=ALU.mult)
-            nc.gpsimd.tensor_tensor(out=rest[:], in0=weight[:], in1=high, op=ALU.subtract)
-            nc.gpsimd.tensor_tensor(out=middle, in0=weight[:], in1=high, op=ALU.subtract)
-            nc.gpsimd.tensor_tensor(out=low, in0=rest[:], in1=middle, op=ALU.subtract)
 
         def transpose_band(u):
-            band_bank = psum_band.tile([P, 2, P], BF16, name="band_bank")
-            for half in range(2):
-                nc.tensor.transpose(band_bank[:, half, :], band_padded[u % 2][:, half, :], ident_bf16[:])
+            band_bank = psum_acc.tile([P, P], F32, name="band_bank", tag="acc")
+            nc.tensor.transpose(band_bank[:], band_padded[u % 2][:], ident[:])
             band_bank_tiles[u] = band_bank
 
         def keep_band(u):
-            band_t = attn_pool.tile([P, 2, P], BF16, name="band_t")
+            band_t = attn_pool.tile([P, P], F32, name="band_t")
             nc.scalar.copy(out=band_t[:], in_=band_bank_tiles[u][:])
             band_t_tiles[u] = band_t
 
         def relative(u):
             rel = psum_acc.tile([P, SLOTS, D], F32, name="rel", tag="acc")
-            for half in range(2):
-                nc.tensor.matmul(
-                    out=rel[:, half * HALF : (half + 1) * HALF, :].rearrange("p k d -> p (k d)"),
-                    lhsT=band_t_tiles[u][:, half, :],
-                    rhs=rel_rows[:].rearrange("p k d -> p (k d)"),
-                    start=True,
-                    stop=True,
-                )
+            nc.tensor.matmul(
+                out=rel[:].rearrange("p k d -> p (k d)"),
+                lhsT=band_t_tiles[u][:],
+                rhs=rel_rows[:].rearrange("p k d -> p (k d)"),
+                start=True,
+                stop=True,
+            )
             acc_tiles[("rel", u)] = rel
 
         def scale_context(u):
@@ -428,21 +422,24 @@ def tile_vitsattention_pa_kernel(tc, logits, v, emb_rel_v, Wo, bo, out):
             )
             nc.sync.dma_start(out=out[b, q * P : (q + 1) * P, cols], in_=result[:])
 
+
         table_probe = keep.tile([P, 1], F32)
         nc.vector.memset(table_probe[:], 0.0)
         nc.scalar.activation(out=table_probe[:], in_=table_probe[:], func=ACT.Exp)
 
-        load_unit(0)
+        load_logits(0)
+        load_logits(1)
+        load_band(0)
         rel_values = keep.tile([P, D], BF16)
         nc.vector.memset(rel_values[:], 0.0)
         nc.sync.dma_start(out=rel_values[0:NREL, :], in_=emb_rel_v[0])
         load_v(0)
-        load_unit(1)
+        load_logits(2)
+        load_band(1)
+        load_band(2)
 
         ident = keep.tile([P, P], F32)
         make_identity(nc, ident[:])
-        ident_bf16 = keep.tile([P, P], BF16)
-        make_identity(nc, ident_bf16[:])
 
         edge_mask = keep.tile([P, QT, NREL], F32)
         nc.gpsimd.memset(edge_mask[:], 0.0)
@@ -455,8 +452,8 @@ def tile_vitsattention_pa_kernel(tc, logits, v, emb_rel_v, Wo, bo, out):
             compare_op=ALU.is_ge, fill=MASKED, base=L - 1 + WINDOW, channel_multiplier=-1,
         )
 
-        band_padded_0 = keep.tile([P, 2, P], BF16)
-        band_padded_1 = keep.tile([P, 2, P], BF16)
+        band_padded_0 = keep.tile([P, P], F32)
+        band_padded_1 = keep.tile([P, P], F32)
         band_padded = (band_padded_0, band_padded_1)
         nc.gpsimd.memset(band_padded_0[:], 0.0)
         nc.gpsimd.memset(band_padded_1[:], 0.0)
@@ -465,23 +462,22 @@ def tile_vitsattention_pa_kernel(tc, logits, v, emb_rel_v, Wo, bo, out):
         nc.gpsimd.memset(rel_spread[:], 0.0)
         nc.gpsimd.affine_select(
             out=rel_spread[:, 0:BAND_ROWS], in_=rel_spread[:, 0:BAND_ROWS],
-            pattern=[[0, HALF * BAND_TERMS], [-1, NREL]],
+            pattern=[[0, SLOTS], [-1, NREL]],
             compare_op=ALU.not_equal, fill=1.0, base=0, channel_multiplier=1,
         )
-        rel_rows = keep.tile([P, HALF, D], BF16)
+        rel_rows = keep.tile([P, SLOTS, D], F32)
 
         def build_rel_rows():
             rel_bank = psum_acc.tile([P, D], F32, name="rel_bank", tag="acc")
             nc.tensor.matmul(out=rel_bank[:], lhsT=rel_spread[:], rhs=rel_values[:], start=True, stop=True)
-            nc.vector.tensor_copy(out=rel_rows[:], in_=rel_bank[:].unsqueeze(1).to_broadcast([P, HALF, D]))
-            rows_of_slot = BAND_TERMS * NREL
+            nc.vector.tensor_copy(out=rel_rows[:], in_=rel_bank[:].unsqueeze(1).to_broadcast([P, SLOTS, D]))
             nc.gpsimd.affine_select(
-                out=rel_rows[:], in_=rel_rows[:], pattern=[[-rows_of_slot, HALF], [0, D]],
+                out=rel_rows[:], in_=rel_rows[:], pattern=[[-NREL, SLOTS], [0, D]],
                 compare_op=ALU.is_ge, fill=0.0, base=0, channel_multiplier=1,
             )
             nc.gpsimd.affine_select(
-                out=rel_rows[:], in_=rel_rows[:], pattern=[[rows_of_slot, HALF], [0, D]],
-                compare_op=ALU.is_ge, fill=0.0, base=rows_of_slot - 1, channel_multiplier=-1,
+                out=rel_rows[:], in_=rel_rows[:], pattern=[[NREL, SLOTS], [0, D]],
+                compare_op=ALU.is_ge, fill=0.0, base=NREL - 1, channel_multiplier=-1,
             )
 
         weight_pieces = (
@@ -494,20 +490,15 @@ def tile_vitsattention_pa_kernel(tc, logits, v, emb_rel_v, Wo, bo, out):
             (regroup_wo, quantise_wo, 3),
             (regroup_v, quantise_v, 3),
         )
-        regroup_step = [-1] + [3 * x // 2 for x in range(1, len(weight_pieces))]
+        weight_at = {1 + 3 * x: piece for x, piece in enumerate(weight_pieces)}
+        last_half_step = 2 * UNITS + 11
 
-        def weight_work(s):
-            for x, (regroup, quantise, piece) in enumerate(weight_pieces):
-                if s == regroup_step[x] + 1:
-                    quantise(piece)
-            for x, (regroup, quantise, piece) in enumerate(weight_pieces):
-                if s == regroup_step[x]:
-                    regroup(piece)
-
-        def first_rows_ready(b, q):
-            if b == 0:
-                return PAIRS_PER_BATCH + 2 + q
-            return PAIR_UNITS + 2 + q
+        def rows_at(h):
+            for b, first in ((0, 2 * PAIRS_PER_BATCH + 6), (1, 2 * PAIR_UNITS + 8)):
+                q, odd = divmod(h - first, 2)
+                if odd == 0 and 0 <= q < QT:
+                    return b, q
+            return None
 
         with tc.manual_schedule(
             engines={mybir.EngineType.PE, mybir.EngineType.Activation, mybir.EngineType.DVE}
@@ -517,86 +508,95 @@ def tile_vitsattention_pa_kernel(tc, logits, v, emb_rel_v, Wo, bo, out):
                     fold(0, level, half * HALF, (half + 1) * HALF)
                 finish_max(0, half * HALF, (half + 1) * HALF)
             shift_band(0)
-            weight_work(-1)
+            fold(1, 0)
+            fold(1, 1)
 
-            for s in range(UNITS + 2):
-                now, last, older = s, s - 1, s - 2
-                has_next, has_now, has_last, has_older = (
-                    s + 1 < UNITS, s < UNITS, 0 <= s - 1 < UNITS, 0 <= s - 2 < UNITS
-                )
-                if s + 2 < UNITS:
-                    load_unit(s + 2)
-                if s == 0:
-                    load_wo(0)
-                if s == 2:
-                    load_wo(1)
-                if s in (1, 5, 8):
-                    load_v((1, 5, 8).index(s) + 1)
-                if s == 4:
+            for h in range(last_half_step + 1):
+                s, half = divmod(h, 2)
+                even = half == 0
+                if even and s + 3 < UNITS:
+                    load_logits(s + 3)
+                    load_band(s + 3)
+                if h in (0, 4):
+                    load_wo(h // 4)
+                if h in (2, 10, 16):
+                    load_v((2, 10, 16).index(h) + 1)
+                if h == 8:
                     nc.sync.dma_start(out=bias_rows[:], in_=bo.partition_broadcast(P))
-                to_project = [(b, q) for b in range(B) for q in range(QT) if first_rows_ready(b, q) == s - 1]
-                to_transpose = [(b, q) for b in range(B) for q in range(QT) if first_rows_ready(b, q) == s]
 
-                if has_last:
-                    invert_sums(last)
-                    split_band(last)
-                if has_older:
-                    relative(older)
-                if has_last:
-                    transpose_e(last, 1)
-                for b, q in to_project:
-                    quantise_merged(b, q)
-                if has_next:
-                    fold(s + 1, 0)
-                if has_now:
-                    exponentials(now, 0)
-                if has_last:
-                    quantise_e(last, 0)
-                    context(last, 0)
-                if has_next:
-                    fold(s + 1, 1)
-                if has_older:
-                    scale_context(older)
-                if has_next:
-                    fold(s + 1, 2)
-                if has_older:
-                    merge(older)
-                if has_next:
-                    fold(s + 1, 3)
-                if has_last:
-                    regroup_e(last, 1, 0, nc.scalar.copy)
-                    regroup_e(last, 1, 1, nc.vector.tensor_copy)
-                if has_now:
-                    transpose_e(now, 0)
-                for b, q in to_project:
-                    project(b, q, 0)
-                    project(b, q, 1)
-                if has_now:
-                    exponentials(now, 1)
-                if has_next:
+                to_exp = s if s < UNITS else None
+                to_transpose = h - 1 if 0 <= h - 1 < 2 * UNITS else None
+                to_regroup = h - 2 if 0 <= h - 2 < 2 * UNITS else None
+                to_quantise = h - 3 if 0 <= h - 3 < 2 * UNITS else None
+                to_multiply = h - 4 if 0 <= h - 4 < 2 * UNITS else None
+
+                if to_regroup is not None and h not in weight_at:
+                    regroup_e(to_regroup // 2, to_regroup % 2, 0, nc.vector.tensor_copy)
+                if even and 0 <= s - 3 < UNITS:
+                    relative(s - 3)
+                if to_exp is not None:
+                    exponentials(s, range(half * HALF, half * HALF + 2))
+                if to_regroup is not None and h in weight_at:
+                    regroup_e(to_regroup // 2, to_regroup % 2, 0, nc.scalar.copy)
+                if to_exp is not None:
+                    exponentials(s, range(half * HALF + 2, half * HALF + 4))
+                if to_regroup is not None:
+                    regroup_e(to_regroup // 2, to_regroup % 2, 1, nc.scalar.copy)
+
+                if not even and 0 <= s - 1 < UNITS:
+                    transpose_band(s - 1)
+                if to_transpose is not None:
+                    transpose_e(to_transpose // 2, to_transpose % 2)
+
+                if even:
+                    if s + 1 < UNITS:
+                        fold(s + 1, 2)
+                elif s + 2 < UNITS:
+                    fold(s + 2, 0)
+                if to_quantise is not None:
+                    quantise_e(to_quantise // 2, to_quantise % 2)
+                if to_multiply is not None:
+                    context(to_multiply // 2, to_multiply % 2)
+                if even:
+                    if s + 1 < UNITS:
+                        fold(s + 1, 3)
+                elif s + 2 < UNITS:
+                    fold(s + 2, 1)
+                if even and 0 <= s - 1 < UNITS:
+                    invert_sums(s - 1)
+                    weigh_band(s - 1)
+                if even and 0 <= s - 3 < UNITS:
+                    scale_context(s - 3)
+                if not even and 0 <= s - 3 < UNITS:
+                    merge(s - 3)
+                if even and s + 1 < UNITS:
                     finish_max(s + 1)
                     shift_band(s + 1)
-                for b, q in to_project:
-                    finish_output(b, q, 0)
-                    finish_output(b, q, 1)
-                weight_work(s)
-                if has_last:
-                    quantise_e(last, 1)
-                    transpose_band(last)
-                    context(last, 1)
-                    keep_band(last)
-                if s == 0:
-                    build_rel_rows()
-                for b, q in to_transpose:
-                    transpose_merged(b, q)
-                    regroup_merged(b, q, nc.scalar.copy)
-                if has_now:
-                    regroup_e(now, 0, 0, nc.scalar.copy)
-                    regroup_e(now, 0, 1, nc.scalar.copy if s in regroup_step else nc.vector.tensor_copy)
-                    band_exponentials(now)
+                if h in weight_at:
+                    regroup, quantise, piece = weight_at[h]
+                    regroup(piece)
+                if h - 1 in weight_at:
+                    regroup, quantise, piece = weight_at[h - 1]
+                    quantise(piece)
 
-            b, q = B - 1, QT - 1
-            quantise_merged(b, q)
-            for part in range(2):
-                project(b, q, part)
-                finish_output(b, q, part)
+                if rows_at(h - 4) is not None:
+                    finish_output(*rows_at(h - 4), 0)
+                if rows_at(h - 5) is not None:
+                    finish_output(*rows_at(h - 5), 1)
+                if rows_at(h - 3) is not None:
+                    project(*rows_at(h - 3), 0)
+                if rows_at(h - 4) is not None:
+                    project(*rows_at(h - 4), 1)
+                if rows_at(h - 2) is not None:
+                    quantise_merged(*rows_at(h - 2))
+                if rows_at(h - 1) is not None:
+                    regroup_merged(*rows_at(h - 1), nc.scalar.copy)
+                if rows_at(h) is not None:
+                    transpose_merged(*rows_at(h))
+
+                if not even and s < UNITS:
+                    band_exponentials(s)
+                if not even and 0 <= s - 1 < UNITS:
+                    keep_band(s - 1)
+                if h == 2:
+                    build_rel_rows()

@@ -25,12 +25,10 @@ N_TILE = 512
 SLOTS = 8
 HALF = SLOTS // 2
 UNITS = NH * QT // SLOTS
-PAIR_UNITS = UNITS - QT
-PAIRS_PER_BATCH = H // 2
-LAST_HEADS = NH - SLOTS
+PAIR_UNITS = H // 2
 BAND_PITCH = 16
 FOLD_WIDTHS = (L // 2, L // 4, L // 8, L // 16)
-V_CHUNK = 8
+V_CHUNK = 4
 RUN = 4
 BAND_ROWS = SLOTS * NREL
 MASKED = -1.0e30
@@ -45,7 +43,8 @@ def is_pair(u):
 def slots_of(u):
     if is_pair(u):
         return [(2 * u + k // QT, k % QT) for k in range(SLOTS)]
-    return [(LAST_HEADS + k, u - PAIR_UNITS) for k in range(SLOTS)]
+    q, group = divmod(u - PAIR_UNITS, GROUPS)
+    return [(H + group * SLOTS + k, q) for k in range(SLOTS)]
 
 
 def tile_vitsattention_pa_kernel(tc, logits, v, emb_rel_v, Wo, bo, out):
@@ -62,7 +61,7 @@ def tile_vitsattention_pa_kernel(tc, logits, v, emb_rel_v, Wo, bo, out):
         code_pool = stack.enter_context(tc.tile_pool(name="code_pool", bufs=4))
         weight_pool = stack.enter_context(tc.tile_pool(name="weight_pool", bufs=2))
         attn_pool = stack.enter_context(tc.tile_pool(name="attn_pool", bufs=3))
-        out_pool = stack.enter_context(tc.tile_pool(name="out_pool", bufs=3))
+        out_pool = stack.enter_context(tc.tile_pool(name="out_pool", bufs=8))
         psum_words = stack.enter_context(tc.psum_pool(name="psum_words", bufs=3))
         psum_acc = stack.enter_context(tc.psum_pool(name="psum_acc", bufs=5))
 
@@ -115,19 +114,20 @@ def tile_vitsattention_pa_kernel(tc, logits, v, emb_rel_v, Wo, bo, out):
                     in_=band_windows(n, 0, L).rearrange("(q p) j -> p q j", p=P),
                 )
 
-        def load_band_tile(band_logits, q):
-            start = LAST_HEADS * L * L + q * P * (L + 1) - WINDOW
+        def load_band_tile(band_logits, n0, q):
+            start = n0 * L * L + q * P * (L + 1) - WINDOW
             whole = SLOTS - 1
             heads = flat_logits[start : start + whole * L * L].rearrange("(n x) -> n x", x=L * L)
             nc.sync.dma_start(
                 out=band_logits[:, 0:whole, 0:NREL],
                 in_=heads[:, 0 : P * (L + 1)].rearrange("n (t s) -> t n s", s=L + 1)[:, :, 0:NREL],
             )
-            if q < QT - 1:
-                nc.sync.dma_start(out=band_logits[:, whole, 0:NREL], in_=band_windows(NH - 1, q * P, P))
+            n = n0 + whole
+            if n < NH - 1 or q < QT - 1:
+                nc.sync.dma_start(out=band_logits[:, whole, 0:NREL], in_=band_windows(n, q * P, P))
             else:
                 nc.sync.dma_start(
-                    out=band_logits[0 : P - 1, whole, 0:NREL], in_=band_windows(NH - 1, q * P, P - 1)
+                    out=band_logits[0 : P - 1, whole, 0:NREL], in_=band_windows(n, q * P, P - 1)
                 )
                 nc.sync.dma_start(
                     out=band_logits[P - 1 : P, whole, 0 : WINDOW + 1],
@@ -136,16 +136,21 @@ def tile_vitsattention_pa_kernel(tc, logits, v, emb_rel_v, Wo, bo, out):
 
         def load_logits(u):
             a = logit_pool.tile([P, SLOTS, L], BF16, name="a")
-            if is_pair(u):
+            if u == 0:
+                for k in range(0, SLOTS, 2):
+                    n, q = slots_of(u)[k]
+                    rows = logits[n, q * P : (q + 2) * P, :]
+                    nc.sync.dma_start(out=a[:, k : k + 2, :], in_=rows.rearrange("(q p) k -> p q k", p=P))
+            elif is_pair(u):
                 for hh in range(2):
                     nc.sync.dma_start(
                         out=a[:, hh * QT : (hh + 1) * QT, :],
                         in_=logits[2 * u + hh].rearrange("(q p) k -> p q k", p=P),
                     )
             else:
-                q = u - PAIR_UNITS
+                n, q = slots_of(u)[0]
                 nc.sync.dma_start(
-                    out=a[:], in_=logits[LAST_HEADS:NH, q * P : (q + 1) * P, :].rearrange("n p k -> p n k")
+                    out=a[:], in_=logits[n : n + SLOTS, q * P : (q + 1) * P, :].rearrange("n p k -> p n k")
                 )
             logit_tiles[u] = a
 
@@ -157,7 +162,7 @@ def tile_vitsattention_pa_kernel(tc, logits, v, emb_rel_v, Wo, bo, out):
                 for hh in range(2):
                     load_band_pair(band_logits, 2 * u + hh, hh * QT)
             else:
-                load_band_tile(band_logits, u - PAIR_UNITS)
+                load_band_tile(band_logits, *slots_of(u)[0])
             band_logit_tiles[u] = band_logits
 
         def load_v(c):
@@ -268,15 +273,17 @@ def tile_vitsattention_pa_kernel(tc, logits, v, emb_rel_v, Wo, bo, out):
             rows = grouped_tiles[(u, half)][:].bitcast(F32)[:, part * 2 * P : (part + 1) * 2 * P, :]
             copy(out=rows, in_=word_banks[(u, half, part)][:].rearrange("p w r -> p r w"))
 
-        def quantise_e(u, half):
-            codes = code_pool.tile([P, L], U32, name="codes", align_bytes=64)
-            scales = code_pool.tile([P, L], U8, name="scales", align_bytes=64)
+        def quantise_e(u, half, rows=slice(0, L)):
+            if (u, half) not in code_tiles:
+                codes = code_pool.tile([P, L], U32, name="codes", align_bytes=64)
+                scales = code_pool.tile([P, L], U8, name="scales", align_bytes=64)
+                code_tiles[(u, half)] = (codes, scales)
+            codes, scales = code_tiles[(u, half)]
             nc.vector.quantize_mx(
-                out=codes[:].bitcast(FP8X4),
-                scales=scales[:],
-                in_=grouped_tiles[(u, half)][:].rearrange("p r t -> p (r t)"),
+                out=codes[:, rows].bitcast(FP8X4),
+                scales=scales[:, rows],
+                in_=grouped_tiles[(u, half)][:, rows, :].rearrange("p r t -> p (r t)"),
             )
-            code_tiles[(u, half)] = (codes, scales)
 
         def context(u, half):
             if half == 0:
@@ -360,51 +367,73 @@ def tile_vitsattention_pa_kernel(tc, logits, v, emb_rel_v, Wo, bo, out):
             )
             scaled_tiles[u] = scaled
 
+        def scale_context_scalar(u):
+            scaled = attn_pool.tile([P, SLOTS, D], F32, name="scaled")
+            for k in range(SLOTS):
+                nc.scalar.activation(
+                    out=scaled[:, k, :],
+                    in_=acc_tiles[("ctx", u)][:, k, :],
+                    func=ACT.Copy,
+                    scale=inv_sum[:, u, k : k + 1],
+                )
+            scaled_tiles[u] = scaled
+
         def merge(u):
             scaled = scaled_tiles[u][:]
             rel = acc_tiles[("rel", u)][:]
             if is_pair(u):
-                b, pair_in_batch = divmod(u, PAIRS_PER_BATCH)
-                cols = slice(pair_in_batch * 2 * D, (pair_in_batch + 1) * 2 * D)
-                target = merged[:, b, :, cols].rearrange("p q (h d) -> p h q d", h=2)
+                target = merged[:, 0, :, u * 2 * D : (u + 1) * 2 * D].rearrange("p q (h d) -> p h q d", h=2)
                 scaled = scaled.rearrange("p (h q) d -> p h q d", q=QT)
                 rel = rel.rearrange("p (h q) d -> p h q d", q=QT)
             else:
-                cols = slice(E - SLOTS * D, E)
-                target = merged[:, B - 1, u - PAIR_UNITS, cols].rearrange("p (k d) -> p k d", d=D)
+                q, group = divmod(u - PAIR_UNITS, GROUPS)
+                cols = slice(group * SLOTS * D, (group + 1) * SLOTS * D)
+                target = merged[:, 1, q, cols].rearrange("p (k d) -> p k d", d=D)
             nc.vector.tensor_tensor(out=target, in0=scaled, in1=rel, op=ALU.add)
 
-        def transpose_merged(b, q):
+        def transpose_merged(b, q, g0=0, g1=GROUPS):
             words = merged[:, b, q, :].bitcast(F32)
-            bank = psum_words.tile([P, GROUPS, 2, P], F32, name="bank")
-            for g in range(GROUPS):
+            if ("m", b, q) not in word_banks:
+                bank = psum_words.tile([P, GROUPS, 2, P], F32, name="bank")
+                word_banks[("m", b, q)] = bank
+            for g in range(g0, g1):
                 for w in range(2):
                     first_word = g * K_PASS // 2 + w * P
-                    nc.tensor.transpose(bank[:, g, w, :], words[:, first_word : first_word + P], ident[:])
-            word_banks[("m", b, q)] = bank
+                    nc.tensor.transpose(
+                        word_banks[("m", b, q)][:, g, w, :], words[:, first_word : first_word + P], ident[:]
+                    )
 
-        def regroup_merged(b, q, copy):
-            grouped = grouped_pool.tile([P, GROUPS, P, PACK], BF16, name="grouped_m", align_bytes=64)
-            copy(out=grouped[:].bitcast(F32), in_=word_banks[("m", b, q)][:].rearrange("p g w r -> p g r w"))
-            grouped_tiles[("m", b, q)] = grouped
-
-        def quantise_merged(b, q):
-            codes = code_pool.tile([P, GROUPS * P], U32, name="codes_m", align_bytes=64)
-            scales = code_pool.tile([P, GROUPS * P], U8, name="scales_m", align_bytes=64)
-            nc.vector.quantize_mx(
-                out=codes[:].bitcast(FP8X4),
-                scales=scales[:],
-                in_=grouped_tiles[("m", b, q)][:].rearrange("p g r t -> p (g r t)"),
+        def regroup_merged(b, q, copy, g0=0, g1=GROUPS):
+            if ("m", b, q) not in grouped_tiles:
+                grouped = grouped_pool.tile([P, GROUPS, P, PACK], BF16, name="grouped_m", align_bytes=64)
+                grouped_tiles[("m", b, q)] = grouped
+            copy(
+                out=grouped_tiles[("m", b, q)][:].bitcast(F32)[:, g0:g1],
+                in_=word_banks[("m", b, q)][:, g0:g1].rearrange("p g w r -> p g r w"),
             )
-            code_tiles[("m", b, q)] = (codes, scales)
 
-        def project(b, q, part):
+        def quantise_merged(b, q, g0=0, g1=GROUPS):
+            if ("m", b, q) not in code_tiles:
+                codes = code_pool.tile([P, GROUPS * P], U32, name="codes_m", align_bytes=64)
+                scales = code_pool.tile([P, GROUPS * P], U8, name="scales_m", align_bytes=64)
+                code_tiles[("m", b, q)] = (codes, scales)
+            codes, scales = code_tiles[("m", b, q)]
+            cols = slice(g0 * P, g1 * P)
+            nc.vector.quantize_mx(
+                out=codes[:, cols].bitcast(FP8X4),
+                scales=scales[:, cols],
+                in_=grouped_tiles[("m", b, q)][:, g0:g1].rearrange("p g r t -> p (g r t)"),
+            )
+
+        def project(b, q, part, g0=0, g1=GROUPS):
             cols = slice(part * N_TILE, (part + 1) * N_TILE)
             codes, scales = code_tiles[("m", b, q)]
-            acc = psum_acc.tile([P, N_TILE], F32, name="acc", tag="acc")
-            for g in range(GROUPS):
+            if ("out", b, q, part) not in acc_tiles:
+                acc = psum_acc.tile([P, N_TILE], F32, name="acc", tag="acc")
+                acc_tiles[("out", b, q, part)] = acc
+            for g in range(g0, g1):
                 nc.tensor.matmul_mx(
-                    out=acc[:],
+                    out=acc_tiles[("out", b, q, part)][:],
                     lhsT=codes[:, g * P : (g + 1) * P].bitcast(FP8X4),
                     lhsT_scale=scales[:, g * P : (g + 1) * P],
                     rhs=wo_codes[:, g, cols].bitcast(FP8X4),
@@ -412,7 +441,6 @@ def tile_vitsattention_pa_kernel(tc, logits, v, emb_rel_v, Wo, bo, out):
                     start=(g == 0),
                     stop=(g == GROUPS - 1),
                 )
-            acc_tiles[("out", b, q, part)] = acc
 
         def finish_output(b, q, part):
             cols = slice(part * N_TILE, (part + 1) * N_TILE)
@@ -430,11 +458,11 @@ def tile_vitsattention_pa_kernel(tc, logits, v, emb_rel_v, Wo, bo, out):
         load_logits(0)
         load_logits(1)
         load_band(0)
+        load_logits(2)
         rel_values = keep.tile([P, D], BF16)
         nc.vector.memset(rel_values[:], 0.0)
         nc.sync.dma_start(out=rel_values[0:NREL, :], in_=emb_rel_v[0])
         load_v(0)
-        load_logits(2)
         load_band(1)
         load_band(2)
 
@@ -480,48 +508,52 @@ def tile_vitsattention_pa_kernel(tc, logits, v, emb_rel_v, Wo, bo, out):
                 compare_op=ALU.is_ge, fill=0.0, base=NREL - 1, channel_multiplier=-1,
             )
 
-        weight_pieces = (
-            (regroup_v, quantise_v, 0),
-            (regroup_wo, quantise_wo, 0),
-            (regroup_v, quantise_v, 1),
-            (regroup_wo, quantise_wo, 1),
-            (regroup_wo, quantise_wo, 2),
-            (regroup_v, quantise_v, 2),
-            (regroup_wo, quantise_wo, 3),
-            (regroup_v, quantise_v, 3),
-        )
-        weight_at = {1 + 3 * x: piece for x, piece in enumerate(weight_pieces)}
-        last_half_step = 2 * UNITS + 11
+        def finish_output_shared(b, q, part):
+            cols = slice(part * N_TILE, (part + 1) * N_TILE)
+            product = attn_pool.tile([P, N_TILE], F32, name="product")
+            result = out_pool.tile([P, N_TILE], F32, name="result")
+            nc.scalar.copy(out=product[:], in_=acc_tiles[("out", b, q, part)][:])
+            nc.gpsimd.tensor_tensor(out=result[:], in0=product[:], in1=bias_rows[:, cols], op=ALU.add)
+            nc.sync.dma_start(out=out[b, q * P : (q + 1) * P, cols], in_=result[:])
+
+        pieces = ("v", "v", "wo", "v", "wo", "v", "wo", "v", "v", "wo", "v", "v")
+        weight_at = {}
+        for x, kind in enumerate(pieces):
+            number = pieces[:x].count(kind)
+            work = (regroup_v, quantise_v, number) if kind == "v" else (regroup_wo, quantise_wo, number)
+            weight_at[5 + 3 * (x - 1) // 2 if x else 2] = work
 
         def rows_at(h):
-            for b, first in ((0, 2 * PAIRS_PER_BATCH + 6), (1, 2 * PAIR_UNITS + 8)):
-                q, odd = divmod(h - first, 2)
-                if odd == 0 and 0 <= q < QT:
+            for b, first, pitch in ((0, 2 * PAIR_UNITS + 6, 2), (1, 2 * PAIR_UNITS + 9, 4)):
+                q, between = divmod(h - first, pitch)
+                if between == 0 and 0 <= q < QT:
                     return b, q
             return None
 
         with tc.manual_schedule(
             engines={mybir.EngineType.PE, mybir.EngineType.Activation, mybir.EngineType.DVE}
         ):
-            for half in range(2):
+            for k0, k1 in ((0, 2), (2, HALF), (HALF, SLOTS)):
                 for level in range(len(FOLD_WIDTHS)):
-                    fold(0, level, half * HALF, (half + 1) * HALF)
-                finish_max(0, half * HALF, (half + 1) * HALF)
+                    fold(0, level, k0, k1)
+                finish_max(0, k0, k1)
             shift_band(0)
             fold(1, 0)
             fold(1, 1)
 
-            for h in range(last_half_step + 1):
+            for h in range(2 * UNITS):
                 s, half = divmod(h, 2)
                 even = half == 0
                 if even and s + 3 < UNITS:
                     load_logits(s + 3)
                     load_band(s + 3)
-                if h in (0, 4):
-                    load_wo(h // 4)
-                if h in (2, 10, 16):
-                    load_v((2, 10, 16).index(h) + 1)
-                if h == 8:
+                if h + 3 in weight_at:
+                    regroup, quantise, piece = weight_at[h + 3]
+                    if regroup == regroup_v:
+                        load_v(piece)
+                    elif piece % 2 == 0:
+                        load_wo(piece // 2)
+                if h == 16:
                     nc.sync.dma_start(out=bias_rows[:], in_=bo.partition_broadcast(P))
 
                 to_exp = s if s < UNITS else None
@@ -530,13 +562,14 @@ def tile_vitsattention_pa_kernel(tc, logits, v, emb_rel_v, Wo, bo, out):
                 to_quantise = h - 3 if 0 <= h - 3 < 2 * UNITS else None
                 to_multiply = h - 4 if 0 <= h - 4 < 2 * UNITS else None
 
-                if to_regroup is not None and h not in weight_at:
+                vector_copies = to_exp is not None and not (h in weight_at and h > 8)
+                if to_regroup is not None and vector_copies:
                     regroup_e(to_regroup // 2, to_regroup % 2, 0, nc.vector.tensor_copy)
                 if even and 0 <= s - 3 < UNITS:
                     relative(s - 3)
                 if to_exp is not None:
                     exponentials(s, range(half * HALF, half * HALF + 2))
-                if to_regroup is not None and h in weight_at:
+                if to_regroup is not None and not vector_copies:
                     regroup_e(to_regroup // 2, to_regroup % 2, 0, nc.scalar.copy)
                 if to_exp is not None:
                     exponentials(s, range(half * HALF + 2, half * HALF + 4))
@@ -600,3 +633,56 @@ def tile_vitsattention_pa_kernel(tc, logits, v, emb_rel_v, Wo, bo, out):
                     keep_band(s - 1)
                 if h == 2:
                     build_rel_rows()
+
+            last, before = UNITS - 1, UNITS - 2
+            b = B - 1
+            regroup_e(last, 0, 0, nc.vector.tensor_copy)
+            regroup_e(last, 0, 1, nc.scalar.copy)
+            finish_output_shared(0, QT - 1, 0)
+            transpose_e(last, 1)
+            project(0, QT - 1, 1)
+            quantise_e(before, 1)
+            context(before, 0)
+            relative(before - 1)
+            scale_context_scalar(before - 1)
+            invert_sums(last)
+            weigh_band(last)
+            quantise_e(last, 0)
+            regroup_e(last, 1, 0, nc.scalar.copy)
+            regroup_e(last, 1, 1, nc.vector.tensor_copy)
+            context(before, 1)
+            merge(before - 1)
+            finish_output(0, QT - 1, 1)
+            relative(before)
+            transpose_band(last)
+            keep_band(last)
+            context(last, 0)
+            for part in range(2):
+                quantise_e(last, 1, slice(part * L // 2, (part + 1) * L // 2))
+            scale_context_scalar(before)
+            project(b, 1, 0)
+            transpose_merged(b, 2)
+            merge(before)
+            context(last, 1)
+            relative(last)
+            regroup_merged(b, 2, nc.scalar.copy)
+            finish_output_shared(b, 1, 0)
+            scale_context(last)
+            transpose_merged(b, 3, 0, 1)
+            merge(last)
+            quantise_merged(b, 2)
+            regroup_merged(b, 3, nc.scalar.copy, 0, 1)
+            transpose_merged(b, 3, 1, 2)
+            project(b, 1, 1)
+            quantise_merged(b, 3, 0, 1)
+            regroup_merged(b, 3, nc.scalar.copy, 1, 2)
+            project(b, 2, 0)
+            project(b, 2, 1)
+            finish_output(b, 1, 1)
+            quantise_merged(b, 3, 1, 2)
+            finish_output_shared(b, 2, 0)
+            project(b, 3, 0)
+            project(b, 3, 1)
+            finish_output(b, 2, 1)
+            finish_output(b, 3, 0)
+            finish_output(b, 3, 1)

@@ -96,21 +96,22 @@ def tile_vitsattention_pa_kernel(tc, logits, v, emb_rel_v, Wo, bo, out):
         def band_windows(n, t0, rows):
             start = n * L * L + t0 * (L + 1) - WINDOW
             run = flat_logits[start : start + rows * (L + 1)]
-            return run.rearrange("(t s) -> t s", s=L + 1)[:, 0:NREL]
+            return run.rearrange("(t s) -> t s", s=L + 1)[:, 0:BAND_PITCH]
 
         def load_band_pair(band_logits, n, k0):
             if n == 0:
                 nc.sync.dma_start(
-                    out=band_logits[:, 1:QT, 0:NREL],
+                    out=band_logits[:, 1:QT, :],
                     in_=band_windows(n, P, L - P).rearrange("(q p) j -> p q j", p=P),
                 )
-                nc.sync.dma_start(out=band_logits[1:P, 0, 0:NREL], in_=band_windows(n, 1, P - 1))
+                nc.sync.dma_start(out=band_logits[1:P, 0, :], in_=band_windows(n, 1, P - 1))
                 nc.sync.dma_start(
-                    out=band_logits[0:1, 0, WINDOW:NREL], in_=flat_logits[0 : WINDOW + 1].unsqueeze(0)
+                    out=band_logits[0:1, 0, WINDOW:BAND_PITCH],
+                    in_=flat_logits[0 : BAND_PITCH - WINDOW].unsqueeze(0),
                 )
             else:
                 nc.sync.dma_start(
-                    out=band_logits[:, k0 : k0 + QT, 0:NREL],
+                    out=band_logits[:, k0 : k0 + QT, :],
                     in_=band_windows(n, 0, L).rearrange("(q p) j -> p q j", p=P),
                 )
 
@@ -119,15 +120,15 @@ def tile_vitsattention_pa_kernel(tc, logits, v, emb_rel_v, Wo, bo, out):
             whole = SLOTS - 1
             heads = flat_logits[start : start + whole * L * L].rearrange("(n x) -> n x", x=L * L)
             nc.sync.dma_start(
-                out=band_logits[:, 0:whole, 0:NREL],
-                in_=heads[:, 0 : P * (L + 1)].rearrange("n (t s) -> t n s", s=L + 1)[:, :, 0:NREL],
+                out=band_logits[:, 0:whole, :],
+                in_=heads[:, 0 : P * (L + 1)].rearrange("n (t s) -> t n s", s=L + 1)[:, :, 0:BAND_PITCH],
             )
             n = n0 + whole
             if n < NH - 1 or q < QT - 1:
-                nc.sync.dma_start(out=band_logits[:, whole, 0:NREL], in_=band_windows(n, q * P, P))
+                nc.sync.dma_start(out=band_logits[:, whole, :], in_=band_windows(n, q * P, P))
             else:
                 nc.sync.dma_start(
-                    out=band_logits[0 : P - 1, whole, 0:NREL], in_=band_windows(n, q * P, P - 1)
+                    out=band_logits[0 : P - 1, whole, :], in_=band_windows(n, q * P, P - 1)
                 )
                 nc.sync.dma_start(
                     out=band_logits[P - 1 : P, whole, 0 : WINDOW + 1],

@@ -28,6 +28,7 @@ UNITS = NH * QT // SLOTS
 PAIR_UNITS = H // 2
 BAND_PITCH = 16
 FOLD_WIDTHS = (L // 2, L // 4, L // 8, L // 16)
+FIRST_PIECES = ((0, 1, 0), (1, 2, 0), (2, HALF, 1), (HALF, SLOTS, len(FOLD_WIDTHS)))
 V_CHUNK = 4
 RUN = 4
 BAND_ROWS = SLOTS * NREL
@@ -138,10 +139,10 @@ def tile_vitsattention_pa_kernel(tc, logits, v, emb_rel_v, Wo, bo, out):
         def load_logits(u):
             a = logit_pool.tile([P, SLOTS, L], BF16, name="a")
             if u == 0:
-                for k in range(0, SLOTS, 2):
-                    n, q = slots_of(u)[k]
-                    rows = logits[n, q * P : (q + 2) * P, :]
-                    nc.sync.dma_start(out=a[:, k : k + 2, :], in_=rows.rearrange("(q p) k -> p q k", p=P))
+                for k0, k1, levels in FIRST_PIECES:
+                    n, q = slots_of(u)[k0]
+                    rows = logits[n, q * P : (q + k1 - k0) * P, :]
+                    nc.sync.dma_start(out=a[:, k0:k1, :], in_=rows.rearrange("(q p) k -> p q k", p=P))
             elif is_pair(u):
                 for hh in range(2):
                     nc.sync.dma_start(
@@ -231,10 +232,11 @@ def tile_vitsattention_pa_kernel(tc, logits, v, emb_rel_v, Wo, bo, out):
                 op=ALU.max,
             )
 
-        def finish_max(u, k0=0, k1=SLOTS):
+        def finish_max(u, k0=0, k1=SLOTS, levels=len(FOLD_WIDTHS)):
+            rest = folded_tiles[(u, levels - 1)] if levels else logit_tiles[u]
             nc.vector.tensor_reduce(
                 out=neg_max[:, u, k0:k1],
-                in_=folded_tiles[(u, len(FOLD_WIDTHS) - 1)][:, k0:k1, :],
+                in_=rest[:, k0:k1, :],
                 axis=AXIS.X,
                 op=ALU.max,
                 negate=True,
@@ -534,10 +536,10 @@ def tile_vitsattention_pa_kernel(tc, logits, v, emb_rel_v, Wo, bo, out):
         with tc.manual_schedule(
             engines={mybir.EngineType.PE, mybir.EngineType.Activation, mybir.EngineType.DVE}
         ):
-            for k0, k1 in ((0, 2), (2, HALF), (HALF, SLOTS)):
-                for level in range(len(FOLD_WIDTHS)):
+            for k0, k1, levels in FIRST_PIECES:
+                for level in range(levels):
                     fold(0, level, k0, k1)
-                finish_max(0, k0, k1)
+                finish_max(0, k0, k1, levels)
             shift_band(0)
             fold(1, 0)
             fold(1, 1)

@@ -26,6 +26,7 @@ SLOTS = 8
 HALF = SLOTS // 2
 UNITS = NH * QT // SLOTS
 PAIR_UNITS = H // 2
+ROW_STEPS = ((QT, 1), (1, P))
 BAND_PITCH = 16
 FOLD_WIDTHS = (L // 2, L // 4, L // 8, L // 16)
 FIRST_PIECES = ((0, 1, 0), (1, 2, 0), (2, HALF, 1), (HALF, SLOTS, len(FOLD_WIDTHS)))
@@ -101,11 +102,16 @@ def tile_vitsattention_pa_kernel(tc, logits, v, emb_rel_v, Wo, bo, out):
 
         def load_band_pair(band_logits, n, k0):
             if n == 0:
-                nc.sync.dma_start(
-                    out=band_logits[:, 1:QT, :],
-                    in_=band_windows(n, P, L - P).rearrange("(q p) j -> p q j", p=P),
-                )
-                nc.sync.dma_start(out=band_logits[1:P, 0, :], in_=band_windows(n, 1, P - 1))
+                pitch = QT * (L + 1)
+                rest = flat_logits[L + 1 - WINDOW : L + 1 - WINDOW + P * pitch].rearrange("(p s) -> p s", s=pitch)
+                windows = rest[:, 0 : (QT - 1) * (L + 1)].rearrange("p (q s) -> p q s", s=L + 1)
+                nc.sync.dma_start(out=band_logits[:, 1:QT, :], in_=windows[:, :, 0:BAND_PITCH])
+                for p0, count in ((64, 64), (32, 32), (1, 31)):
+                    first = flat_logits[p0 * pitch - WINDOW : (p0 + count) * pitch - WINDOW]
+                    nc.sync.dma_start(
+                        out=band_logits[p0 : p0 + count, 0, :],
+                        in_=first.rearrange("(p s) -> p s", s=pitch)[:, 0:BAND_PITCH],
+                    )
                 nc.sync.dma_start(
                     out=band_logits[0:1, 0, WINDOW:BAND_PITCH],
                     in_=flat_logits[0 : BAND_PITCH - WINDOW].unsqueeze(0),
@@ -113,7 +119,7 @@ def tile_vitsattention_pa_kernel(tc, logits, v, emb_rel_v, Wo, bo, out):
             else:
                 nc.sync.dma_start(
                     out=band_logits[:, k0 : k0 + QT, :],
-                    in_=band_windows(n, 0, L).rearrange("(q p) j -> p q j", p=P),
+                    in_=band_windows(n, 0, L).rearrange("(p q) j -> p q j", q=QT),
                 )
 
         def load_band_tile(band_logits, n0, q):
@@ -128,9 +134,10 @@ def tile_vitsattention_pa_kernel(tc, logits, v, emb_rel_v, Wo, bo, out):
             if n < NH - 1 or q < QT - 1:
                 nc.sync.dma_start(out=band_logits[:, whole, :], in_=band_windows(n, q * P, P))
             else:
-                nc.sync.dma_start(
-                    out=band_logits[0 : P - 1, whole, :], in_=band_windows(n, q * P, P - 1)
-                )
+                for p0, count in ((0, 64), (64, 32), (96, 31)):
+                    nc.sync.dma_start(
+                        out=band_logits[p0 : p0 + count, whole, :], in_=band_windows(n, q * P + p0, count)
+                    )
                 nc.sync.dma_start(
                     out=band_logits[P - 1 : P, whole, 0 : WINDOW + 1],
                     in_=flat_logits[NH * L * L - (WINDOW + 1) : NH * L * L].unsqueeze(0),
@@ -141,13 +148,13 @@ def tile_vitsattention_pa_kernel(tc, logits, v, emb_rel_v, Wo, bo, out):
             if u == 0:
                 for k0, k1, levels in FIRST_PIECES:
                     n, q = slots_of(u)[k0]
-                    rows = logits[n, q * P : (q + k1 - k0) * P, :]
-                    nc.sync.dma_start(out=a[:, k0:k1, :], in_=rows.rearrange("(q p) k -> p q k", p=P))
+                    rows = logits[n].rearrange("(p q) k -> p q k", q=QT)
+                    nc.sync.dma_start(out=a[:, k0:k1, :], in_=rows[:, q : q + k1 - k0, :])
             elif is_pair(u):
                 for hh in range(2):
                     nc.sync.dma_start(
                         out=a[:, hh * QT : (hh + 1) * QT, :],
-                        in_=logits[2 * u + hh].rearrange("(q p) k -> p q k", p=P),
+                        in_=logits[2 * u + hh].rearrange("(p q) k -> p q k", q=QT),
                     )
             else:
                 n, q = slots_of(u)[0]
@@ -316,10 +323,10 @@ def tile_vitsattention_pa_kernel(tc, logits, v, emb_rel_v, Wo, bo, out):
             )
             if is_pair(u):
                 by_tile = shifted[:].rearrange("p (h q) j -> p h q j", q=QT)
-                mask = edge_mask[:].unsqueeze(1).to_broadcast([P, 2, QT, NREL])
+                mask = edge_mask_0[:].unsqueeze(1).to_broadcast([P, 2, QT, NREL])
                 nc.gpsimd.tensor_tensor(out=by_tile, in0=by_tile, in1=mask, op=ALU.add)
             elif slots_of(u)[0][1] in (0, QT - 1):
-                mask = edge_mask[:, slots_of(u)[0][1]].unsqueeze(1).to_broadcast([P, SLOTS, NREL])
+                mask = edge_mask_1[:, slots_of(u)[0][1]].unsqueeze(1).to_broadcast([P, SLOTS, NREL])
                 nc.gpsimd.tensor_tensor(out=shifted[:], in0=shifted[:], in1=mask, op=ALU.add)
             shifted_tiles[u] = shifted
 
@@ -445,13 +452,18 @@ def tile_vitsattention_pa_kernel(tc, logits, v, emb_rel_v, Wo, bo, out):
                     stop=(g == GROUPS - 1),
                 )
 
+        def rows_of_output(b, q, cols):
+            if b == 0:
+                return out[b].rearrange("(p q) o -> p q o", q=QT)[:, q, cols]
+            return out[b, q * P : (q + 1) * P, cols]
+
         def finish_output(b, q, part):
             cols = slice(part * N_TILE, (part + 1) * N_TILE)
             result = out_pool.tile([P, N_TILE], F32, name="result")
             nc.vector.tensor_tensor(
                 out=result[:], in0=acc_tiles[("out", b, q, part)][:], in1=bias_rows[:, cols], op=ALU.add
             )
-            nc.sync.dma_start(out=out[b, q * P : (q + 1) * P, cols], in_=result[:])
+            nc.sync.dma_start(out=rows_of_output(b, q, cols), in_=result[:])
 
 
         table_probe = keep.tile([P, 1], F32)
@@ -467,21 +479,25 @@ def tile_vitsattention_pa_kernel(tc, logits, v, emb_rel_v, Wo, bo, out):
         nc.sync.dma_start(out=rel_values[0:NREL, :], in_=emb_rel_v[0])
         load_v(0)
         load_band(1)
+        load_logits(3)
         load_band(2)
 
         ident = keep.tile([P, P], F32)
         make_identity(nc, ident[:])
 
-        edge_mask = keep.tile([P, QT, NREL], F32)
-        nc.gpsimd.memset(edge_mask[:], 0.0)
-        nc.gpsimd.affine_select(
-            out=edge_mask[:], in_=edge_mask[:], pattern=[[P, QT], [1, NREL]],
-            compare_op=ALU.is_ge, fill=MASKED, base=-WINDOW, channel_multiplier=1,
-        )
-        nc.gpsimd.affine_select(
-            out=edge_mask[:], in_=edge_mask[:], pattern=[[-P, QT], [-1, NREL]],
-            compare_op=ALU.is_ge, fill=MASKED, base=L - 1 + WINDOW, channel_multiplier=-1,
-        )
+        edge_mask_0 = keep.tile([P, QT, NREL], F32)
+        edge_mask_1 = keep.tile([P, QT, NREL], F32)
+        edge_masks = (edge_mask_0, edge_mask_1)
+        for mask, (row_step, tile_step) in zip(edge_masks, ROW_STEPS):
+            nc.gpsimd.memset(mask[:], 0.0)
+            nc.gpsimd.affine_select(
+                out=mask[:], in_=mask[:], pattern=[[tile_step, QT], [1, NREL]],
+                compare_op=ALU.is_ge, fill=MASKED, base=-WINDOW, channel_multiplier=row_step,
+            )
+            nc.gpsimd.affine_select(
+                out=mask[:], in_=mask[:], pattern=[[-tile_step, QT], [-1, NREL]],
+                compare_op=ALU.is_ge, fill=MASKED, base=L - 1 + WINDOW, channel_multiplier=-row_step,
+            )
 
         band_padded_0 = keep.tile([P, P], F32)
         band_padded_1 = keep.tile([P, P], F32)
@@ -517,7 +533,7 @@ def tile_vitsattention_pa_kernel(tc, logits, v, emb_rel_v, Wo, bo, out):
             result = out_pool.tile([P, N_TILE], F32, name="result")
             nc.scalar.copy(out=product[:], in_=acc_tiles[("out", b, q, part)][:])
             nc.gpsimd.tensor_tensor(out=result[:], in0=product[:], in1=bias_rows[:, cols], op=ALU.add)
-            nc.sync.dma_start(out=out[b, q * P : (q + 1) * P, cols], in_=result[:])
+            nc.sync.dma_start(out=rows_of_output(b, q, cols), in_=result[:])
 
         pieces = ("v", "v", "wo", "v", "wo", "v", "wo", "v", "v", "wo", "v", "v")
         weight_at = {}
@@ -547,8 +563,9 @@ def tile_vitsattention_pa_kernel(tc, logits, v, emb_rel_v, Wo, bo, out):
             for h in range(2 * UNITS):
                 s, half = divmod(h, 2)
                 even = half == 0
+                if even and s + 4 < UNITS:
+                    load_logits(s + 4)
                 if even and s + 3 < UNITS:
-                    load_logits(s + 3)
                     load_band(s + 3)
                 if h + 3 in weight_at:
                     regroup, quantise, piece = weight_at[h + 3]

from contextlib import ExitStack

import concourse.mybir as mybir
from concourse.masks import make_identity

F32 = mybir.dt.float32
BF16 = mybir.dt.bfloat16
U32 = mybir.dt.uint32
U8 = mybir.dt.uint8
FP8X4 = mybir.dt.float8_e4m3fn_x4
ALU = mybir.AluOpType
ACT = mybir.ActivationFunctionType
AXIS = mybir.AxisListType

P = 128
B, H, L, D, WINDOW = 2, 16, 512, 64, 4
E = H * D
NH = B * H
NREL = 2 * WINDOW + 1
QT = L // P
PACK = 4
K_PASS = P * PACK
GROUPS = E // K_PASS
N_TILE = 512
SLOTS = 8
HALF = SLOTS // 2
UNITS = NH * QT // SLOTS
PAIR_UNITS = H // 2
ROW_STEPS = ((QT, 1), (1, P))
BAND_PITCH = 16
FOLD_WIDTHS = (L // 2, L // 4, L // 8, L // 16)
FIRST_PIECES = ((0, 1, 0), (1, 2, 0), (2, HALF, 1), (HALF, SLOTS, len(FOLD_WIDTHS)))
V_CHUNK = 4
RUN = 4
BAND_ROWS = SLOTS * NREL
MASKED = -1.0e30

FLOPS = 2 * NH * L * L * D + 2 * NH * L * NREL * D + 2 * B * L * E * E


def is_pair(u):
    return u < PAIR_UNITS


def slots_of(u):
    if is_pair(u):
        return [(2 * u + k // QT, k % QT) for k in range(SLOTS)]
    q, group = divmod(u - PAIR_UNITS, GROUPS)
    return [(H + group * SLOTS + k, q) for k in range(SLOTS)]


def tile_vitsattention_pa_kernel(tc, logits, v, emb_rel_v, Wo, bo, out):
    nc = tc.nc
    flat_logits = logits.rearrange("n t k -> (n t k)")

    with ExitStack() as stack:
        keep = stack.enter_context(tc.tile_pool(name="keep", bufs=1))
        logit_pool = stack.enter_context(tc.tile_pool(name="logit_pool", bufs=5))
        band_pool = stack.enter_context(tc.tile_pool(name="band_pool", bufs=5))
        fold_pool = stack.enter_context(tc.tile_pool(name="fold_pool", bufs=2))
        e_pool = stack.enter_context(tc.tile_pool(name="e_pool", bufs=3))
        grouped_pool = stack.enter_context(tc.tile_pool(name="grouped_pool", bufs=4))
        code_pool = stack.enter_context(tc.tile_pool(name="code_pool", bufs=4))
        weight_pool = stack.enter_context(tc.tile_pool(name="weight_pool", bufs=2))
        attn_pool = stack.enter_context(tc.tile_pool(name="attn_pool", bufs=3))
        out_pool = stack.enter_context(tc.tile_pool(name="out_pool", bufs=8))
        psum_words = stack.enter_context(tc.psum_pool(name="psum_words", bufs=3))
        psum_acc = stack.enter_context(tc.psum_pool(name="psum_acc", bufs=5))

        neg_max = keep.tile([P, UNITS, SLOTS], F32)
        row_sum = keep.tile([P, UNITS, SLOTS], F32)
        inv_sum = keep.tile([P, UNITS, SLOTS], F32)
        merged = keep.tile([P, B, QT, E], BF16)
        v_codes = keep.tile([P, NH * D], U32, align_bytes=64)
        v_scales = keep.tile([P, NH * D], U8, align_bytes=64)
        wo_raw = keep.tile([P, GROUPS, PACK, E], BF16)
        wo_codes = keep.tile([P, GROUPS, E], U32, align_bytes=64)
        wo_scales = keep.tile([P, GROUPS, E], U8, align_bytes=64)
        bias_rows = keep.tile([P, E], BF16)

        logit_tiles = {}
        band_logit_tiles = {}
        shifted_tiles = {}
        band_e_tiles = {}
        band_t_tiles = {}
        band_bank_tiles = {}
        folded_tiles = {}
        e_tiles = {}
        word_banks = {}
        grouped_tiles = {}
        code_tiles = {}
        v_raw_tiles = {}
        v_grouped_tiles = {}
        wo_grouped_tiles = {}
        acc_tiles = {}
        scaled_tiles = {}

        def band_windows(n, t0, rows):
            start = n * L * L + t0 * (L + 1) - WINDOW
            run = flat_logits[start : start + rows * (L + 1)]
            return run.rearrange("(t s) -> t s", s=L + 1)[:, 0:BAND_PITCH]

        def load_band_pair(band_logits, n, k0):
            if n == 0:
                pitch = QT * (L + 1)
                rest = flat_logits[L + 1 - WINDOW : L + 1 - WINDOW + P * pitch].rearrange("(p s) -> p s", s=pitch)
                windows = rest[:, 0 : (QT - 1) * (L + 1)].rearrange("p (q s) -> p q s", s=L + 1)
                nc.sync.dma_start(out=band_logits[:, 1:QT, :], in_=windows[:, :, 0:BAND_PITCH])
                for p0, count in ((64, 64), (32, 32), (1, 31)):
                    first = flat_logits[p0 * pitch - WINDOW : (p0 + count) * pitch - WINDOW]
                    nc.sync.dma_start(
                        out=band_logits[p0 : p0 + count, 0, :],
                        in_=first.rearrange("(p s) -> p s", s=pitch)[:, 0:BAND_PITCH],
                    )
                nc.sync.dma_start(
                    out=band_logits[0:1, 0, WINDOW:BAND_PITCH],
                    in_=flat_logits[0 : BAND_PITCH - WINDOW].unsqueeze(0),
                )
            else:
                nc.sync.dma_start(
                    out=band_logits[:, k0 : k0 + QT, :],
                    in_=band_windows(n, 0, L).rearrange("(p q) j -> p q j", q=QT),
                )

        def load_band_tile(band_logits, n0, q):
            start = n0 * L * L + q * P * (L + 1) - WINDOW
            whole = SLOTS - 1
            heads = flat_logits[start : start + whole * L * L].rearrange("(n x) -> n x", x=L * L)
            nc.sync.dma_start(
                out=band_logits[:, 0:whole, :],
                in_=heads[:, 0 : P * (L + 1)].rearrange("n (t s) -> t n s", s=L + 1)[:, :, 0:BAND_PITCH],
            )
            n = n0 + whole
            if n < NH - 1 or q < QT - 1:
                nc.sync.dma_start(out=band_logits[:, whole, :], in_=band_windows(n, q * P, P))
            else:
                for p0, count in ((0, 64), (64, 32), (96, 31)):
                    nc.sync.dma_start(
                        out=band_logits[p0 : p0 + count, whole, :], in_=band_windows(n, q * P + p0, count)
                    )
                nc.sync.dma_start(
                    out=band_logits[P - 1 : P, whole, 0 : WINDOW + 1],
                    in_=flat_logits[NH * L * L - (WINDOW + 1) : NH * L * L].unsqueeze(0),
                )

        def load_logits(u):
            a = logit_pool.tile([P, SLOTS, L], BF16, name="a")
            if u == 0:
                for k0, k1, levels in FIRST_PIECES:
                    n, q = slots_of(u)[k0]
                    rows = logits[n].rearrange("(p q) k -> p q k", q=QT)
                    nc.sync.dma_start(out=a[:, k0:k1, :], in_=rows[:, q : q + k1 - k0, :])
            elif is_pair(u):
                for hh in range(2):
                    nc.sync.dma_start(
                        out=a[:, hh * QT : (hh + 1) * QT, :],
                        in_=logits[2 * u + hh].rearrange("(p q) k -> p q k", q=QT),
                    )
            else:
                n, q = slots_of(u)[0]
                nc.sync.dma_start(
                    out=a[:], in_=logits[n : n + SLOTS, q * P : (q + 1) * P, :].rearrange("n p k -> p n k")
                )
            logit_tiles[u] = a

        def load_band(u):
            band_logits = band_pool.tile([P, SLOTS, BAND_PITCH], BF16, name="band_logits")
            if u == 0 or u == UNITS - 1:
                nc.gpsimd.memset(band_logits[:], 0.0)
            if is_pair(u):
                for hh in range(2):
                    load_band_pair(band_logits, 2 * u + hh, hh * QT)
            else:
                load_band_tile(band_logits, *slots_of(u)[0])
            band_logit_tiles[u] = band_logits

        def load_v(c):
            v_raw = weight_pool.tile([P, V_CHUNK, PACK, D], BF16, name="v_raw")
            nc.sync.dma_start(
                out=v_raw[:].rearrange("p n (u c) d -> p n u (c d)", u=2),
                in_=v[c * V_CHUNK : (c + 1) * V_CHUNK].rearrange("n (u p c) d -> p n u (c d)", u=2, p=P, c=2),
            )
            v_raw_tiles[c] = v_raw

        def load_wo(g):
            nc.sync.dma_start(
                out=wo_raw[:, g].rearrange("p (u c) o -> p u (c o)", u=2),
                in_=Wo[g * K_PASS : (g + 1) * K_PASS, :].rearrange("(u p c) o -> p u (c o)", u=2, p=P, c=2),
            )

        def regroup_v(c):
            v_grouped = weight_pool.tile([P, V_CHUNK, D, PACK], BF16, name="v_grouped", align_bytes=64)
            nc.vector.tensor_copy(
                out=v_grouped[:].rearrange("p n (c i) t -> p n c t i", i=RUN),
                in_=v_raw_tiles[c][:].rearrange("p n t (c i) -> p n c t i", i=RUN),
            )
            v_grouped_tiles[c] = v_grouped

        def quantise_v(c):
            cols = slice(c * V_CHUNK * D, (c + 1) * V_CHUNK * D)
            nc.vector.quantize_mx(
                out=v_codes[:, cols].bitcast(FP8X4),
                scales=v_scales[:, cols],
                in_=v_grouped_tiles[c][:].rearrange("p n d t -> p (n d t)"),
            )

        def regroup_wo(w):
            g, half = divmod(w, E // N_TILE)
            cols = slice(half * N_TILE, (half + 1) * N_TILE)
            wo_grouped = weight_pool.tile([P, N_TILE, PACK], BF16, name="wo_grouped", align_bytes=64)
            nc.vector.tensor_copy(
                out=wo_grouped[:].rearrange("p (c i) t -> p c t i", i=RUN),
                in_=wo_raw[:, g, :, cols].rearrange("p t (c i) -> p c t i", i=RUN),
            )
            wo_grouped_tiles[w] = wo_grouped

        def quantise_wo(w):
            g, half = divmod(w, E // N_TILE)
            cols = slice(half * N_TILE, (half + 1) * N_TILE)
            nc.vector.quantize_mx(
                out=wo_codes[:, g, cols].bitcast(FP8X4),
                scales=wo_scales[:, g, cols],
                in_=wo_grouped_tiles[w][:].rearrange("p o t -> p (o t)"),
            )

        def fold(u, level, k0=0, k1=SLOTS):
            width = FOLD_WIDTHS[level]
            if level == 0:
                wide = logit_tiles[u][:, k0:k1, :]
            else:
                wide = folded_tiles[(u, level - 1)][:, k0:k1, :]
            if (u, level) not in folded_tiles:
                folded = fold_pool.tile([P, SLOTS, width], BF16, name="folded", tag="folded_%d" % width)
                folded_tiles[(u, level)] = folded
            nc.vector.tensor_tensor(
                out=folded_tiles[(u, level)][:, k0:k1, :],
                in0=wide[:, :, 0:width],
                in1=wide[:, :, width : 2 * width],
                op=ALU.max,
            )

        def finish_max(u, k0=0, k1=SLOTS, levels=len(FOLD_WIDTHS)):
            rest = folded_tiles[(u, levels - 1)] if levels else logit_tiles[u]
            nc.vector.tensor_reduce(
                out=neg_max[:, u, k0:k1],
                in_=rest[:, k0:k1, :],
                axis=AXIS.X,
                op=ALU.max,
                negate=True,
            )

        def exponentials(u, slots):
            if u not in e_tiles:
                e = e_pool.tile([P, SLOTS, L], BF16, name="e")
                e_tiles[u] = e
            for k in slots:
                nc.scalar.activation(
                    out=e_tiles[u][:, k, :],
                    in_=logit_tiles[u][:, k, :],
                    func=ACT.Exp,
                    bias=neg_max[:, u, k : k + 1],
                    scale=1.0,
                    accum_out=row_sum[:, u, k : k + 1],
                )

        def transpose_e(u, half):
            words = e_tiles[u][:].bitcast(F32)
            for part in range(2):
                bank = psum_words.tile([P, 2, 2 * P], F32, name="bank")
                for w in range(2):
                    for r in range(2):
                        nc.tensor.transpose(
                            bank[:, w, r * P : (r + 1) * P],
                            words[:, half * HALF + 2 * part + r, w * P : (w + 1) * P],
                            ident[:],
                        )
                word_banks[(u, half, part)] = bank

        def regroup_e(u, half, part, copy):
            if (u, half) not in grouped_tiles:
                grouped = grouped_pool.tile([P, L, PACK], BF16, name="grouped", align_bytes=64)
                grouped_tiles[(u, half)] = grouped
            rows = grouped_tiles[(u, half)][:].bitcast(F32)[:, part * 2 * P : (part + 1) * 2 * P, :]
            copy(out=rows, in_=word_banks[(u, half, part)][:].rearrange("p w r -> p r w"))

        def quantise_e(u, half, rows=slice(0, L)):
            if (u, half) not in code_tiles:
                codes = code_pool.tile([P, L], U32, name="codes", align_bytes=64)
                scales = code_pool.tile([P, L], U8, name="scales", align_bytes=64)
                code_tiles[(u, half)] = (codes, scales)
            codes, scales = code_tiles[(u, half)]
            nc.vector.quantize_mx(
                out=codes[:, rows].bitcast(FP8X4),
                scales=scales[:, rows],
                in_=grouped_tiles[(u, half)][:, rows, :].rearrange("p r t -> p (r t)"),
            )

        def context(u, half):
            if half == 0:
                ctx = psum_acc.tile([P, SLOTS, D], F32, name="ctx", tag="acc")
                acc_tiles[("ctx", u)] = ctx
            codes, scales = code_tiles[(u, half)]
            for j in range(HALF):
                k = half * HALF + j
                n = slots_of(u)[k][0]
                nc.tensor.matmul_mx(
                    out=acc_tiles[("ctx", u)][:, k, :],
                    lhsT=codes[:, j * P : (j + 1) * P].bitcast(FP8X4),
                    lhsT_scale=scales[:, j * P : (j + 1) * P],
                    rhs=v_codes[:, n * D : (n + 1) * D].bitcast(FP8X4),
                    rhs_scale=v_scales[:, n * D : (n + 1) * D],
                    start=True,
                    stop=True,
                )

        def shift_band(u):
            shifted = band_pool.tile([P, SLOTS, NREL], F32, name="shifted")
            nc.gpsimd.tensor_tensor(
                out=shifted[:],
                in0=band_logit_tiles[u][:, :, 0:NREL],
                in1=neg_max[:, u].unsqueeze(2).to_broadcast([P, SLOTS, NREL]),
                op=ALU.add,
            )
            if is_pair(u):
                by_tile = shifted[:].rearrange("p (h q) j -> p h q j", q=QT)
                mask = edge_mask_0[:].unsqueeze(1).to_broadcast([P, 2, QT, NREL])
                nc.gpsimd.tensor_tensor(out=by_tile, in0=by_tile, in1=mask, op=ALU.add)
            elif slots_of(u)[0][1] in (0, QT - 1):
                mask = edge_mask_1[:, slots_of(u)[0][1]].unsqueeze(1).to_broadcast([P, SLOTS, NREL])
                nc.gpsimd.tensor_tensor(out=shifted[:], in0=shifted[:], in1=mask, op=ALU.add)
            shifted_tiles[u] = shifted

        def band_exponentials(u):
            band_e = band_pool.tile([P, SLOTS, NREL], F32, name="band_e")
            nc.scalar.activation(out=band_e[:], in_=shifted_tiles[u][:], func=ACT.Exp)
            band_e_tiles[u] = band_e

        def invert_sums(u):
            nc.vector.reciprocal(out=inv_sum[:, u], in_=row_sum[:, u])

        def weigh_band(u):
            nc.gpsimd.tensor_tensor(
                out=band_padded[u % 2][:, 0:BAND_ROWS].rearrange("p (k j) -> p k j", j=NREL),
                in0=band_e_tiles[u][:],
                in1=inv_sum[:, u].unsqueeze(2).to_broadcast([P, SLOTS, NREL]),
                op=ALU.mult,
            )

        def transpose_band(u):
            band_bank = psum_acc.tile([P, P], F32, name="band_bank", tag="acc")
            nc.tensor.transpose(band_bank[:], band_padded[u % 2][:], ident[:])
            band_bank_tiles[u] = band_bank

        def keep_band(u):
            band_t = attn_pool.tile([P, P], F32, name="band_t")
            nc.scalar.copy(out=band_t[:], in_=band_bank_tiles[u][:])
            band_t_tiles[u] = band_t

        def relative(u):
            rel = psum_acc.tile([P, SLOTS, D], F32, name="rel", tag="acc")
            nc.tensor.matmul(
                out=rel[:].rearrange("p k d -> p (k d)"),
                lhsT=band_t_tiles[u][:],
                rhs=rel_rows[:].rearrange("p k d -> p (k d)"),
                start=True,
                stop=True,
            )
            acc_tiles[("rel", u)] = rel

        def scale_context(u):
            scaled = attn_pool.tile([P, SLOTS, D], F32, name="scaled")
            nc.vector.tensor_tensor(
                out=scaled[:],
                in0=acc_tiles[("ctx", u)][:],
                in1=inv_sum[:, u].unsqueeze(2).to_broadcast([P, SLOTS, D]),
                op=ALU.mult,
            )
            scaled_tiles[u] = scaled

        def scale_context_scalar(u):
            scaled = attn_pool.tile([P, SLOTS, D], F32, name="scaled")
            for k in range(SLOTS):
                nc.scalar.activation(
                    out=scaled[:, k, :],
                    in_=acc_tiles[("ctx", u)][:, k, :],
                    func=ACT.Copy,
                    scale=inv_sum[:, u, k : k + 1],
                )
            scaled_tiles[u] = scaled

        def merge(u):
            scaled = scaled_tiles[u][:]
            rel = acc_tiles[("rel", u)][:]
            if is_pair(u):
                target = merged[:, 0, :, u * 2 * D : (u + 1) * 2 * D].rearrange("p q (h d) -> p h q d", h=2)
                scaled = scaled.rearrange("p (h q) d -> p h q d", q=QT)
                rel = rel.rearrange("p (h q) d -> p h q d", q=QT)
            else:
                q, group = divmod(u - PAIR_UNITS, GROUPS)
                cols = slice(group * SLOTS * D, (group + 1) * SLOTS * D)
                target = merged[:, 1, q, cols].rearrange("p (k d) -> p k d", d=D)
            nc.vector.tensor_tensor(out=target, in0=scaled, in1=rel, op=ALU.add)

        def transpose_merged(b, q, g0=0, g1=GROUPS):
            words = merged[:, b, q, :].bitcast(F32)
            if ("m", b, q) not in word_banks:
                bank = psum_words.tile([P, GROUPS, 2, P], F32, name="bank")
                word_banks[("m", b, q)] = bank
            for g in range(g0, g1):
                for w in range(2):
                    first_word = g * K_PASS // 2 + w * P
                    nc.tensor.transpose(
                        word_banks[("m", b, q)][:, g, w, :], words[:, first_word : first_word + P], ident[:]
                    )

        def regroup_merged(b, q, copy, g0=0, g1=GROUPS):
            if ("m", b, q) not in grouped_tiles:
                grouped = grouped_pool.tile([P, GROUPS, P, PACK], BF16, name="grouped_m", align_bytes=64)
                grouped_tiles[("m", b, q)] = grouped
            copy(
                out=grouped_tiles[("m", b, q)][:].bitcast(F32)[:, g0:g1],
                in_=word_banks[("m", b, q)][:, g0:g1].rearrange("p g w r -> p g r w"),
            )

        def quantise_merged(b, q, g0=0, g1=GROUPS):
            if ("m", b, q) not in code_tiles:
                codes = code_pool.tile([P, GROUPS * P], U32, name="codes_m", align_bytes=64)
                scales = code_pool.tile([P, GROUPS * P], U8, name="scales_m", align_bytes=64)
                code_tiles[("m", b, q)] = (codes, scales)
            codes, scales = code_tiles[("m", b, q)]
            cols = slice(g0 * P, g1 * P)
            nc.vector.quantize_mx(
                out=codes[:, cols].bitcast(FP8X4),
                scales=scales[:, cols],
                in_=grouped_tiles[("m", b, q)][:, g0:g1].rearrange("p g r t -> p (g r t)"),
            )

        def project(b, q, part, g0=0, g1=GROUPS):
            cols = slice(part * N_TILE, (part + 1) * N_TILE)
            codes, scales = code_tiles[("m", b, q)]
            if ("out", b, q, part) not in acc_tiles:
                acc = psum_acc.tile([P, N_TILE], F32, name="acc", tag="acc")
                acc_tiles[("out", b, q, part)] = acc
            for g in range(g0, g1):
                nc.tensor.matmul_mx(
                    out=acc_tiles[("out", b, q, part)][:],
                    lhsT=codes[:, g * P : (g + 1) * P].bitcast(FP8X4),
                    lhsT_scale=scales[:, g * P : (g + 1) * P],
                    rhs=wo_codes[:, g, cols].bitcast(FP8X4),
                    rhs_scale=wo_scales[:, g, cols],
                    start=(g == 0),
                    stop=(g == GROUPS - 1),
                )

        def rows_of_output(b, q, cols):
            if b == 0:
                return out[b].rearrange("(p q) o -> p q o", q=QT)[:, q, cols]
            return out[b, q * P : (q + 1) * P, cols]

        def finish_output(b, q, part):
            cols = slice(part * N_TILE, (part + 1) * N_TILE)
            result = out_pool.tile([P, N_TILE], F32, name="result")
            nc.vector.tensor_tensor(
                out=result[:], in0=acc_tiles[("out", b, q, part)][:], in1=bias_rows[:, cols], op=ALU.add
            )
            nc.sync.dma_start(out=rows_of_output(b, q, cols), in_=result[:])


        table_probe = keep.tile([P, 1], F32)
        nc.vector.memset(table_probe[:], 0.0)
        nc.scalar.activation(out=table_probe[:], in_=table_probe[:], func=ACT.Exp)

        load_logits(0)
        load_logits(1)
        load_band(0)
        load_logits(2)
        rel_values = keep.tile([P, D], BF16)
        nc.vector.memset(rel_values[:], 0.0)
        nc.sync.dma_start(out=rel_values[0:NREL, :], in_=emb_rel_v[0])
        load_v(0)
        load_band(1)
        load_logits(3)
        load_band(2)

        ident = keep.tile([P, P], F32)
        make_identity(nc, ident[:])

        edge_mask_0 = keep.tile([P, QT, NREL], F32)
        edge_mask_1 = keep.tile([P, QT, NREL], F32)
        edge_masks = (edge_mask_0, edge_mask_1)
        for mask, (row_step, tile_step) in zip(edge_masks, ROW_STEPS):
            nc.gpsimd.memset(mask[:], 0.0)
            nc.gpsimd.affine_select(
                out=mask[:], in_=mask[:], pattern=[[tile_step, QT], [1, NREL]],
                compare_op=ALU.is_ge, fill=MASKED, base=-WINDOW, channel_multiplier=row_step,
            )
            nc.gpsimd.affine_select(
                out=mask[:], in_=mask[:], pattern=[[-tile_step, QT], [-1, NREL]],
                compare_op=ALU.is_ge, fill=MASKED, base=L - 1 + WINDOW, channel_multiplier=-row_step,
            )

        band_padded_0 = keep.tile([P, P], F32)
        band_padded_1 = keep.tile([P, P], F32)
        band_padded = (band_padded_0, band_padded_1)
        nc.gpsimd.memset(band_padded_0[:], 0.0)
        nc.gpsimd.memset(band_padded_1[:], 0.0)

        rel_spread = keep.tile([P, P], BF16)
        nc.gpsimd.memset(rel_spread[:], 0.0)
        nc.gpsimd.affine_select(
            out=rel_spread[:, 0:BAND_ROWS], in_=rel_spread[:, 0:BAND_ROWS],
            pattern=[[0, SLOTS], [-1, NREL]],
            compare_op=ALU.not_equal, fill=1.0, base=0, channel_multiplier=1,
        )
        rel_rows = keep.tile([P, SLOTS, D], F32)

        def build_rel_rows():
            rel_bank = psum_acc.tile([P, D], F32, name="rel_bank", tag="acc")
            nc.tensor.matmul(out=rel_bank[:], lhsT=rel_spread[:], rhs=rel_values[:], start=True, stop=True)
            nc.vector.tensor_copy(out=rel_rows[:], in_=rel_bank[:].unsqueeze(1).to_broadcast([P, SLOTS, D]))
            nc.gpsimd.affine_select(
                out=rel_rows[:], in_=rel_rows[:], pattern=[[-NREL, SLOTS], [0, D]],
                compare_op=ALU.is_ge, fill=0.0, base=0, channel_multiplier=1,
            )
            nc.gpsimd.affine_select(
                out=rel_rows[:], in_=rel_rows[:], pattern=[[NREL, SLOTS], [0, D]],
                compare_op=ALU.is_ge, fill=0.0, base=NREL - 1, channel_multiplier=-1,
            )

        def finish_output_shared(b, q, part):
            cols = slice(part * N_TILE, (part + 1) * N_TILE)
            product = attn_pool.tile([P, N_TILE], F32, name="product")
            result = out_pool.tile([P, N_TILE], F32, name="result")
            nc.scalar.copy(out=product[:], in_=acc_tiles[("out", b, q, part)][:])
            nc.gpsimd.tensor_tensor(out=result[:], in0=product[:], in1=bias_rows[:, cols], op=ALU.add)
            nc.sync.dma_start(out=rows_of_output(b, q, cols), in_=result[:])

        pieces = ("v", "v", "wo", "v", "wo", "v", "wo", "v", "v", "wo", "v", "v")
        weight_at = {}
        for x, kind in enumerate(pieces):
            number = pieces[:x].count(kind)
            work = (regroup_v, quantise_v, number) if kind == "v" else (regroup_wo, quantise_wo, number)
            weight_at[5 + 3 * (x - 1) // 2 if x else 2] = work

        def rows_at(h):
            for b, first, pitch in ((0, 2 * PAIR_UNITS + 6, 2), (1, 2 * PAIR_UNITS + 9, 4)):
                q, between = divmod(h - first, pitch)
                if between == 0 and 0 <= q < QT:
                    return b, q
            return None

        with tc.manual_schedule(
            engines={mybir.EngineType.PE, mybir.EngineType.Activation, mybir.EngineType.DVE}
        ):
            for k0, k1, levels in FIRST_PIECES:
                for level in range(levels):
                    fold(0, level, k0, k1)
                finish_max(0, k0, k1, levels)
            shift_band(0)
            fold(1, 0)
            fold(1, 1)

            for h in range(2 * UNITS):
                s, half = divmod(h, 2)
                even = half == 0
                if even and s + 4 < UNITS:
                    load_logits(s + 4)
                if even and s + 3 < UNITS:
                    load_band(s + 3)
                if h + 3 in weight_at:
                    regroup, quantise, piece = weight_at[h + 3]
                    if regroup == regroup_v:
                        load_v(piece)
                    elif piece % 2 == 0:
                        load_wo(piece // 2)
                if h == 16:
                    nc.sync.dma_start(out=bias_rows[:], in_=bo.partition_broadcast(P))

                to_exp = s if s < UNITS else None
                to_transpose = h - 1 if 0 <= h - 1 < 2 * UNITS else None
                to_regroup = h - 2 if 0 <= h - 2 < 2 * UNITS else None
                to_quantise = h - 3 if 0 <= h - 3 < 2 * UNITS else None
                to_multiply = h - 4 if 0 <= h - 4 < 2 * UNITS else None

                vector_copies = to_exp is not None and not (h in weight_at and h > 8)
                if to_regroup is not None and vector_copies:
                    regroup_e(to_regroup // 2, to_regroup % 2, 0, nc.vector.tensor_copy)
                if even and 0 <= s - 3 < UNITS:
                    relative(s - 3)
                if to_exp is not None:
                    exponentials(s, range(half * HALF, half * HALF + 2))
                if to_regroup is not None and not vector_copies:
                    regroup_e(to_regroup // 2, to_regroup % 2, 0, nc.scalar.copy)
                if to_exp is not None:
                    exponentials(s, range(half * HALF + 2, half * HALF + 4))
                if to_regroup is not None:
                    regroup_e(to_regroup // 2, to_regroup % 2, 1, nc.scalar.copy)

                if not even and 0 <= s - 1 < UNITS:
                    transpose_band(s - 1)
                if to_transpose is not None:
                    transpose_e(to_transpose // 2, to_transpose % 2)

                if even:
                    if s + 1 < UNITS:
                        fold(s + 1, 2)
                elif s + 2 < UNITS:
                    fold(s + 2, 0)
                if to_quantise is not None:
                    quantise_e(to_quantise // 2, to_quantise % 2)
                if to_multiply is not None:
                    context(to_multiply // 2, to_multiply % 2)
                if even:
                    if s + 1 < UNITS:
                        fold(s + 1, 3)
                elif s + 2 < UNITS:
                    fold(s + 2, 1)
                if even and 0 <= s - 1 < UNITS:
                    invert_sums(s - 1)
                    weigh_band(s - 1)
                if even and 0 <= s - 3 < UNITS:
                    scale_context(s - 3)
                if not even and 0 <= s - 3 < UNITS:
                    merge(s - 3)
                if even and s + 1 < UNITS:
                    finish_max(s + 1)
                    shift_band(s + 1)
                if h in weight_at:
                    regroup, quantise, piece = weight_at[h]
                    regroup(piece)
                if h - 1 in weight_at:
                    regroup, quantise, piece = weight_at[h - 1]
                    quantise(piece)

                if rows_at(h - 4) is not None:
                    finish_output(*rows_at(h - 4), 0)
                if rows_at(h - 5) is not None:
                    finish_output(*rows_at(h - 5), 1)
                if rows_at(h - 3) is not None:
                    project(*rows_at(h - 3), 0)
                if rows_at(h - 4) is not None:
                    project(*rows_at(h - 4), 1)
                if rows_at(h - 2) is not None:
                    quantise_merged(*rows_at(h - 2))
                if rows_at(h - 1) is not None:
                    regroup_merged(*rows_at(h - 1), nc.scalar.copy)
                if rows_at(h) is not None:
                    transpose_merged(*rows_at(h))

                if not even and s < UNITS:
                    band_exponentials(s)
                if not even and 0 <= s - 1 < UNITS:
                    keep_band(s - 1)
                if h == 2:
                    build_rel_rows()

            last, before = UNITS - 1, UNITS - 2
            b = B - 1
            regroup_e(last, 0, 0, nc.vector.tensor_copy)
            regroup_e(last, 0, 1, nc.scalar.copy)
            finish_output_shared(0, QT - 1, 0)
            transpose_e(last, 1)
            project(0, QT - 1, 1)
            quantise_e(before, 1)
            context(before, 0)
            relative(before - 1)
            scale_context_scalar(before - 1)
            invert_sums(last)
            weigh_band(last)
            quantise_e(last, 0)
            regroup_e(last, 1, 0, nc.scalar.copy)
            regroup_e(last, 1, 1, nc.vector.tensor_copy)
            context(before, 1)
            merge(before - 1)
            finish_output(0, QT - 1, 1)
            relative(before)
            transpose_band(last)
            keep_band(last)
            context(last, 0)
            for part in range(2):
                quantise_e(last, 1, slice(part * L // 2, (part + 1) * L // 2))
            scale_context_scalar(before)
            project(b, 1, 0)
            transpose_merged(b, 2)
            merge(before)
            context(last, 1)
            relative(last)
            regroup_merged(b, 2, nc.scalar.copy)
            finish_output_shared(b, 1, 0)
            scale_context(last)
            transpose_merged(b, 3, 0, 1)
            merge(last)
            quantise_merged(b, 2)
            regroup_merged(b, 3, nc.scalar.copy, 0, 1)
            transpose_merged(b, 3, 1, 2)
            project(b, 1, 1)
            quantise_merged(b, 3, 0, 1)
            regroup_merged(b, 3, nc.scalar.copy, 1, 2)
            project(b, 2, 0)
            project(b, 2, 1)
            finish_output(b, 1, 1)
            quantise_merged(b, 3, 1, 2)
            finish_output_shared(b, 2, 0)
            project(b, 3, 0)
            project(b, 3, 1)
            finish_output(b, 2, 1)
            finish_output(b, 3, 0)
            finish_output(b, 3, 1)
